import numpy as np
import ml_dtypes


def mxq(x, axis, fmt="e4m3"):
    dtype, down = {"e4m3": (ml_dtypes.float8_e4m3fn, 7), "e5m2": (ml_dtypes.float8_e5m2, 14)}[fmt]
    v = np.moveaxis(np.asarray(x, np.float32).astype(ml_dtypes.bfloat16).astype(np.float64), axis, -1)
    blocks = v.reshape(v.shape[:-1] + (-1, 32))
    amax = np.abs(blocks).max(-1, keepdims=True)
    byte = np.maximum(np.where(amax > 0, np.frexp(amax)[1] - 1 + 127, 0) - down, 1)
    scale = np.exp2(byte - 127.0)
    codes = (blocks / scale).astype(np.float32).astype(dtype).astype(np.float64)
    return np.moveaxis((codes * scale).reshape(v.shape), -1, axis)


WIDE = False


def mx_kscale(k):
    if not WIDE:
        return np.ones(k)
    levels = np.array([10, -10, 5, -5, 0])
    a = np.random.permutation(np.resize(levels, k // 512 * 4)).reshape(k // 512, 4)
    idx = np.arange(k)
    return np.exp2(a[idx // 512, idx % 128 // 32])


BF16 = ml_dtypes.bfloat16


def bf(x):
    return np.asarray(x, np.float32).astype(BF16)


def f64(x):
    return np.asarray(x).astype(np.float64)


E2M1 = np.array([0.0, 0.5, 1.0, 1.5, 2.0, 3.0, 4.0, 6.0, -0.0, -0.5, -1.0, -1.5, -2.0, -3.0, -4.0, -6.0])


def pack_weight(w, fmt):
    k, n = w.shape
    w = f64(bf(w)).reshape(k // 32, 32, n)
    amax = np.abs(w).max(1)
    if fmt == "e4m3":
        byte = np.frexp(amax)[1] - 1 + 127 - 7
    else:
        mant, ex = np.frexp(amax / 6.0)
        byte = np.where(mant > 0.5, ex, ex - 1) + 127
    byte = np.clip(np.where(amax > 0, byte, 1), 1, 254)
    scaled = (w * np.exp2(127.0 - byte)[:, None, :]).reshape(k, n).astype(np.float32)
    by_word = np.ascontiguousarray(scaled.reshape(k // 512, 128, 4, n).transpose(0, 1, 3, 2))
    if fmt == "e4m3":
        words = by_word.astype(ml_dtypes.float8_e4m3fn).view(np.uint8)
    else:
        c = by_word.astype(ml_dtypes.float4_e2m1fn).view(np.uint8) & 0xF
        words = c[..., 0::2] | (c[..., 1::2] << 4)
    return np.ascontiguousarray(words), np.ascontiguousarray(byte.astype(np.uint8).reshape(k // 512, 16, n))


def unpack_weight(words, scales, fmt):
    g, p, n, _ = words.shape
    if fmt == "e4m3":
        vals = np.ascontiguousarray(words).view(ml_dtypes.float8_e4m3fn).astype(np.float64)
    else:
        nib = np.empty((g, p, n, 4), np.uint8)
        nib[..., 0::2] = words & 0xF
        nib[..., 1::2] = words >> 4
        vals = E2M1[nib]
    vals = vals * np.repeat(np.exp2(scales.astype(np.float64) - 127.0), 8, axis=1)[..., None]
    return vals.transpose(0, 1, 3, 2).reshape(g * 512, n)


B, T, C = 4, 256, 1024
EPS = 1e-8
FMT = "e4m3"


def sigmoid(z):
    return 1.0 / (1.0 + np.exp(-z))


def setup_inputs():
    s = mx_kscale(C)
    t = mx_kscale(C)
    g = 1.0 / np.sqrt(C)
    x = bf(np.random.standard_normal((B, T, C)) * s)
    a0 = bf(np.random.standard_normal((B, C)) * t)
    b0 = bf(0.5 + np.random.uniform(size=(B, C)))
    x_prev0 = bf(np.random.standard_normal((B, C)) * s)
    w = bf((0.5 + 2.0 * np.random.uniform(size=C)) / T)
    u = bf(np.random.standard_normal(C) * 0.5)
    mu_r = bf(np.random.uniform(size=C))
    mu_k = bf(np.random.uniform(size=C))
    mu_v = bf(np.random.uniform(size=C))
    W_r_words, W_r_scales = pack_weight(np.ascontiguousarray((np.random.standard_normal((C, C)) * g / s[None, :]).T), FMT)
    W_k_words, W_k_scales = pack_weight(np.ascontiguousarray((np.random.standard_normal((C, C)) * g / s[None, :]).T), FMT)
    W_v_words, W_v_scales = pack_weight(np.ascontiguousarray((np.random.standard_normal((C, C)) * g / s[None, :] * t[:, None]).T), FMT)
    W_out_words, W_out_scales = pack_weight(np.ascontiguousarray((np.random.standard_normal((C, C)) * 2.0 * g / t[None, :]).T), FMT)
    return {
        "x": x,
        "a0": a0,
        "b0": b0,
        "x_prev0": x_prev0,
        "w": w,
        "u": u,
        "mu_r": mu_r,
        "mu_k": mu_k,
        "mu_v": mu_v,
        "W_r_words": W_r_words,
        "W_r_scales": W_r_scales,
        "W_k_words": W_k_words,
        "W_k_scales": W_k_scales,
        "W_v_words": W_v_words,
        "W_v_scales": W_v_scales,
        "W_out_words": W_out_words,
        "W_out_scales": W_out_scales,
    }


def reference(x, a0, b0, x_prev0, w, u, mu_r, mu_k, mu_v, W_r_words, W_r_scales, W_k_words, W_k_scales, W_v_words, W_v_scales, W_out_words, W_out_scales):
    x, a0, b0, x_prev0 = f64(x), f64(a0), f64(b0), f64(x_prev0)
    w, u = f64(w), f64(u)
    mu_r, mu_k, mu_v = f64(mu_r), f64(mu_k), f64(mu_v)
    x_shift = np.concatenate([x_prev0[:, None, :], x[:, :-1, :]], axis=1)
    xr = mu_r * x + (1.0 - mu_r) * x_shift
    xk = mu_k * x + (1.0 - mu_k) * x_shift
    xv = mu_v * x + (1.0 - mu_v) * x_shift
    r = sigmoid(mxq(xr, 2, "e4m3") @ unpack_weight(W_r_words, W_r_scales, FMT))
    k = mxq(xk, 2, "e4m3") @ unpack_weight(W_k_words, W_k_scales, FMT)
    v = mxq(xv, 2, "e4m3") @ unpack_weight(W_v_words, W_v_scales, FMT)
    ek = np.exp(u + k)
    steps = np.arange(1, T + 1).astype(np.float64)
    decay_pow = np.exp(-w[None, :] * steps[:, None])
    a_t = a0[:, None, :] * decay_pow[None]
    b_t = b0[:, None, :] * decay_pow[None]
    wkv = (a_t + ek * v) / (b_t + ek + EPS)
    h = r * wkv
    return mxq(h, 2, "e4m3") @ unpack_weight(W_out_words, W_out_scales, FMT)

@@ -1,0 +1,360 @@
+from contextlib import ExitStack
+
+import concourse.mybir as mybir
+from concourse.masks import make_identity
+
+F32 = mybir.dt.float32
+BF16 = mybir.dt.bfloat16
+I32 = mybir.dt.int32
+U32 = mybir.dt.uint32
+U8 = mybir.dt.uint8
+FP8X4 = mybir.dt.float8_e4m3fn_x4
+ALU = mybir.AluOpType
+ACT = mybir.ActivationFunctionType
+
+P = 128
+B, T, C = 4, 256, 1024
+EPS = 1e-8
+PACK = 4
+GROUPS = C // (P * PACK)
+PLANES = GROUPS * PACK
+CH_TILES = C // P
+HALVES = 2
+HALF = B * T // HALVES
+SEQ_HALF = B // HALVES
+TOK_TILES = HALF // P
+LEAD = 16
+PITCH = LEAD + T
+
+ROW_W, ROW_U, ROW_A0, ROW_B0, ROW_XPREV, ROW_MU, ROWS = 0, 1, 2, 6, 10, 14, 17
+MIX_R, MIX_K, MIX_V, W_OUT = 0, 1, 2, 3
+
+FLOPS = 4 * 2 * B * T * C * C
+
+
+def tile_rwkv_timemix_pa_kernel(
+    tc, x, a0, b0, x_prev0, w, u, mu_r, mu_k, mu_v,
+    W_r_words, W_r_scales, W_k_words, W_k_scales, W_v_words, W_v_scales,
+    W_out_words, W_out_scales, out,
+):
+    nc = tc.nc
+    x_rows = x.flatten_outer_dims()
+    out_rows = out.flatten_outer_dims()
+    weight_words = (W_r_words, W_k_words, W_v_words, W_out_words)
+    weight_scales = (W_r_scales, W_k_scales, W_v_scales, W_out_scales)
+
+    with ExitStack() as ctx:
+        keep = ctx.enter_context(tc.tile_pool(name="keep", bufs=1))
+        rows = ctx.enter_context(tc.tile_pool(name="rows", bufs=HALVES))
+        psum = ctx.enter_context(tc.psum_pool(name="psum", bufs=2))
+        ctx.enter_context(tc.manual_schedule())
+
+        small = keep.tile([P, C], BF16, name="small")
+        nc.vector.memset(small[:].bitcast(I32), 0)
+        nc.scalar.dma_start(out=small[ROW_W : ROW_W + 1, :], in_=w.unsqueeze(0))
+        nc.scalar.dma_start(out=small[ROW_U : ROW_U + 1, :], in_=u.unsqueeze(0))
+        nc.scalar.dma_start(out=small[ROW_A0 : ROW_A0 + B, :], in_=a0)
+        nc.scalar.dma_start(out=small[ROW_B0 : ROW_B0 + B, :], in_=b0)
+        nc.scalar.dma_start(out=small[ROW_XPREV : ROW_XPREV + B, :], in_=x_prev0)
+        for m, mu in enumerate((mu_r, mu_k, mu_v)):
+            nc.scalar.dma_start(out=small[ROW_MU + m : ROW_MU + m + 1, :], in_=mu.unsqueeze(0))
+
+        x_half = []
+        for hf in range(HALVES):
+            xh = rows.tile([P, TOK_TILES, C], BF16, name="x_half%d" % hf, tag="rows")
+            nc.sync.dma_start(
+                out=xh[:],
+                in_=x_rows[hf * HALF : (hf + 1) * HALF, :].rearrange("(q p) c -> p q c", p=P),
+            )
+            x_half.append(xh)
+
+        w_scale = keep.tile([P, 4, GROUPS, C], U8, name="w_scale", align_bytes=64)
+        nc.vector.memset(w_scale[:].rearrange("p a g n -> p (a g n)").bitcast(I32), 0)
+        for wi in (MIX_K, MIX_V, MIX_R, W_OUT):
+            by_row = weight_scales[wi].rearrange("g (q r) n -> r q g n", r=4)
+            for r in range(4):
+                nc.sync.dma_start(
+                    out=w_scale[r:P:32, wi, :, :].bitcast(I32), in_=by_row[r].bitcast(I32)
+                )
+        w_code = []
+        for wi in range(4):
+            w_code.append(keep.tile([P, GROUPS, C], U32, name="w_code%d" % wi, align_bytes=64))
+        for wi in (MIX_K, MIX_V, MIX_R, W_OUT):
+            for g in range(GROUPS):
+                nc.sync.dma_start(
+                    out=w_code[wi][:, g, :].bitcast(I32),
+                    in_=weight_words[wi][g].rearrange("p n t -> p (n t)").bitcast(I32),
+                )
+
+        ident_bf = keep.tile([P, P], BF16, name="ident_bf")
+        make_identity(nc, ident_bf[:])
+        ident_f32 = keep.tile([P, P], F32, name="ident_f32")
+        make_identity(nc, ident_f32[:])
+        steps_int = keep.tile([P, T], I32, name="steps_int")
+        nc.gpsimd.iota(steps_int[:], pattern=[[1, T]], base=1, channel_multiplier=0)
+        steps = keep.tile([P, T], F32, name="steps")
+        nc.vector.tensor_copy(out=steps[:], in_=steps_int[:])
+        eps_col = keep.tile([P, 1], F32, name="eps_col")
+        nc.vector.memset(eps_col[:], EPS)
+
+        by_tile_ps = psum.tile([P, CH_TILES, P], BF16, name="by_tile_ps", tag="k")
+        for j in range(CH_TILES):
+            nc.tensor.transpose(by_tile_ps[:, j, :], small[:, j * P : (j + 1) * P], ident_bf[:])
+        by_tile = keep.tile([P, CH_TILES, ROWS], F32, name="by_tile")
+        nc.vector.tensor_copy(out=by_tile[:], in_=by_tile_ps[:, :, 0:ROWS])
+
+        by_plane_ps = psum.tile([P, PLANES, P], BF16, name="by_plane_ps", tag="v")
+        for pl in range(PLANES):
+            g, t = divmod(pl, PACK)
+            nc.tensor.transpose(
+                by_plane_ps[:, pl, :], small[:, g * 512 + t : (g + 1) * 512 : PACK], ident_bf[:]
+            )
+        mu_plane = keep.tile([P, PLANES, 3], F32, name="mu_plane")
+        nc.vector.tensor_copy(out=mu_plane[:], in_=by_plane_ps[:, :, ROW_MU : ROW_MU + 3])
+
+        a0_t = by_tile[:, :, ROW_A0 : ROW_A0 + B]
+        b0_t = by_tile[:, :, ROW_B0 : ROW_B0 + B]
+        neg_w = keep.tile([P, CH_TILES, 1], F32, name="neg_w")
+        nc.vector.tensor_scalar_mul(out=neg_w[:], in0=by_tile[:, :, ROW_W : ROW_W + 1], scalar1=-1.0)
+        neg_u = keep.tile([P, CH_TILES, 1], F32, name="neg_u")
+        nc.vector.tensor_scalar_mul(out=neg_u[:], in0=by_tile[:, :, ROW_U : ROW_U + 1], scalar1=-1.0)
+        inv_b0 = keep.tile([P, CH_TILES, B], F32, name="inv_b0")
+        nc.vector.reciprocal(out=inv_b0[:], in_=b0_t)
+        neg_ratio = keep.tile([P, CH_TILES, B], F32, name="neg_ratio")
+        nc.vector.scalar_tensor_tensor(
+            out=neg_ratio[:], in0=a0_t, scalar=-1.0, in1=inv_b0[:], op0=ALU.mult, op1=ALU.mult
+        )
+
+        decay = keep.tile([P, CH_TILES, T], F32, name="decay")
+        for j in range(CH_TILES):
+            nc.scalar.activation(out=decay[:, j, :], in_=steps[:], func=ACT.Exp, scale=neg_w[:, j, :])
+        ln_b0_eps = keep.tile([P, CH_TILES, B], F32, name="ln_b0_eps")
+        nc.scalar.activation(out=ln_b0_eps[:], in_=b0_t, func=ACT.Ln, scale=1.0 / EPS)
+        ln_bt = keep.tile([P, CH_TILES, B, T], F32, name="ln_bt")
+
+        def log_of_bt(j):
+            for b in range(B):
+                nc.scalar.activation(
+                    out=ln_bt[:, j, b, :], in_=decay[:, j, :], func=ACT.Ln,
+                    scale=by_tile[:, j, ROW_B0 + b : ROW_B0 + b + 1], bias=eps_col[:],
+                )
+
+        def mx_product(acc, lhs_code, lhs_scale, lhs_cols, rhs_code, rhs_scale, rhs_cols):
+            for g in range(GROUPS):
+                nc.tensor.matmul_mx(
+                    out=acc,
+                    lhsT=lhs_code[:, g, lhs_cols].bitcast(FP8X4),
+                    lhsT_scale=lhs_scale[:, g, lhs_cols],
+                    rhs=rhs_code[:, g, rhs_cols].bitcast(FP8X4),
+                    rhs_scale=rhs_scale[:, g, rhs_cols],
+                    start=(g == 0),
+                    stop=(g == GROUPS - 1),
+                )
+
+        x_code, x_scale = [], []
+        for m in range(3):
+            x_code.append(keep.tile([P, GROUPS, B * T], U32, name="x_code%d" % m, align_bytes=64))
+            x_scale.append(keep.tile([P, GROUPS, B * T], U8, name="x_scale%d" % m, align_bytes=64))
+
+        gate = []
+        for hf in range(HALVES):
+            gate.append(keep.tile([P, TOK_TILES, C], F32, name="gate%d" % hf))
+
+        def gate_piece(hf, piece):
+            q, nh = divmod(piece, C // 512)
+            first = hf * HALF + q * P
+            n_cols = slice(nh * 512, (nh + 1) * 512)
+            r_ps = psum.tile([P, 512], F32, name="r_ps", tag="misc")
+            mx_product(
+                r_ps[:], x_code[MIX_R], x_scale[MIX_R], slice(first, first + P),
+                w_code[MIX_R], w_scale[:, MIX_R], n_cols,
+            )
+            nc.scalar.activation(out=gate[hf][:, q, n_cols], in_=r_ps[:], func=ACT.Sigmoid)
+
+        with tc.tile_pool(name="mix", bufs=2) as mix:
+            x_planes = mix.tile([P, PLANES, B, PITCH], BF16, name="x_planes", bufs=1)
+            nc.vector.tensor_copy(
+                out=x_planes[:, :, :, LEAD - 1 : LEAD],
+                in_=by_plane_ps[:, :, ROW_XPREV : ROW_XPREV + B].unsqueeze(3),
+            )
+
+            def transpose_x(hf, pair):
+                xt_ps = psum.tile([P, 2, HALF], BF16, name="xt_ps", tag="misc")
+                for k in range(2):
+                    g, t = divmod(2 * pair + k, PACK)
+                    for q in range(TOK_TILES):
+                        nc.tensor.transpose(
+                            xt_ps[:, k, q * P : (q + 1) * P],
+                            x_half[hf][:, q, g * 512 + t : (g + 1) * 512 : PACK],
+                            ident_bf[:],
+                        )
+                nc.scalar.copy(
+                    out=x_planes[:, 2 * pair : 2 * pair + 2, hf * SEQ_HALF : (hf + 1) * SEQ_HALF, LEAD:PITCH],
+                    in_=xt_ps[:].rearrange("p k (s t) -> p k s t", s=SEQ_HALF),
+                )
+
+            def quantise_x(grouped, m, g, hf):
+                cols = slice(hf * HALF, (hf + 1) * HALF)
+                nc.vector.quantize_mx(
+                    out=x_code[m][:, g, cols].bitcast(FP8X4),
+                    scales=x_scale[m][:, g, cols],
+                    in_=grouped[:].rearrange("p n t -> p (n t)"),
+                )
+
+            for pair in range(PLANES // 2):
+                transpose_x(0, pair)
+
+            waiting = None
+            for hf in range(HALVES):
+                seqs = slice(hf * SEQ_HALF, (hf + 1) * SEQ_HALF)
+                for g in range(GROUPS):
+                    planes = slice(g * PACK, (g + 1) * PACK)
+                    diff = mix.tile([P, PACK, SEQ_HALF, T], F32, name="diff", bufs=1)
+                    nc.vector.tensor_tensor(
+                        out=diff[:], in0=x_planes[:, planes, seqs, LEAD:PITCH],
+                        in1=x_planes[:, planes, seqs, LEAD - 1 : PITCH - 1], op=ALU.subtract,
+                    )
+                    for m in (MIX_R, MIX_K, MIX_V):
+                        mixed = mix.tile([P, PACK, HALF], BF16, name="mixed%d" % m)
+                        for t in range(PACK):
+                            nc.vector.scalar_tensor_tensor(
+                                out=mixed[:, t, :].rearrange("p (s t) -> p s t", s=SEQ_HALF),
+                                in0=diff[:, t, :, :], scalar=mu_plane[:, g * PACK + t, m : m + 1],
+                                in1=x_planes[:, g * PACK + t, seqs, LEAD - 1 : PITCH - 1],
+                                op0=ALU.mult, op1=ALU.add,
+                            )
+                        grouped = mix.tile([P, HALF, PACK], BF16, name="grouped", bufs=3, align_bytes=64)
+                        by_token = mixed[:].rearrange("p t n -> p n t")
+                        if m == MIX_V:
+                            nc.vector.tensor_copy(out=grouped[:], in_=by_token)
+                        else:
+                            nc.scalar.copy(out=grouped[:], in_=by_token)
+                        if waiting is not None:
+                            quantise_x(*waiting)
+                        waiting = (grouped, m, g, hf)
+                    step = hf * GROUPS + g
+                    if hf + 1 < HALVES:
+                        transpose_x(hf + 1, 2 * g)
+                        transpose_x(hf + 1, 2 * g + 1)
+                    for j in range(3 * step, min(3 * step + 3, CH_TILES)):
+                        log_of_bt(j)
+            quantise_x(*waiting)
+            for piece in range(2 * TOK_TILES):
+                gate_piece(0, piece)
+
+        with tc.tile_pool(name="epi", bufs=2, reuse_waits="tile") as epi:
+            h_half = []
+            for hf in range(HALVES):
+                h_half.append(rows.tile([P, TOK_TILES, C], BF16, name="h_half%d" % hf, tag="rows"))
+
+            units = [(hf, j) for hf in range(HALVES) for j in range(CH_TILES)]
+            tiles = {}
+
+            def start_unit(n):
+                hf, j = units[n]
+                ch = slice(j * P, (j + 1) * P)
+                tokens = slice(hf * HALF, (hf + 1) * HALF)
+                k_ps = psum.tile([P, HALF], F32, name="k_ps", tag="k")
+                mx_product(k_ps[:], w_code[MIX_K], w_scale[:, MIX_K], ch, x_code[MIX_K], x_scale[MIX_K], tokens)
+                v_ps = psum.tile([P, HALF], F32, name="v_ps", tag="v")
+                mx_product(v_ps[:], w_code[MIX_V], w_scale[:, MIX_V], ch, x_code[MIX_V], x_scale[MIX_V], tokens)
+                rho = epi.tile([P, SEQ_HALF, T], F32, name="rho")
+                for s in range(SEQ_HALF):
+                    b = hf * SEQ_HALF + s
+                    nc.scalar.activation(
+                        out=rho[:, s, :], in_=steps[:], func=ACT.Sigmoid,
+                        scale=neg_w[:, j, :], bias=ln_b0_eps[:, j, b : b + 1],
+                    )
+                tiles[n] = (k_ps, v_ps, rho)
+
+            def weigh_unit(n):
+                hf, j = units[n]
+                k_ps, v_ps, rho = tiles[n]
+                sb = epi.tile([P, HALF], F32, name="sb")
+                nc.vector.tensor_tensor(
+                    out=sb[:], in0=k_ps[:], op=ALU.subtract,
+                    in1=ln_bt[:, j, hf * SEQ_HALF : (hf + 1) * SEQ_HALF, :].rearrange("p s t -> p (s t)"),
+                )
+                nc.scalar.activation(out=sb[:], in_=sb[:], func=ACT.Sigmoid, scale=-1.0, bias=neg_u[:, j, :])
+                wkv = epi.tile([P, HALF], F32, name="wkv")
+                for s in range(SEQ_HALF):
+                    b = hf * SEQ_HALF + s
+                    nc.vector.scalar_tensor_tensor(
+                        out=wkv[:, s * T : (s + 1) * T], in0=rho[:, s, :],
+                        scalar=neg_ratio[:, j, b : b + 1], in1=v_ps[:, s * T : (s + 1) * T],
+                        op0=ALU.mult, op1=ALU.add,
+                    )
+                tiles[n] = (v_ps, sb, wkv)
+
+            def blend_unit(n):
+                v_ps, sb, wkv = tiles[n]
+                nc.vector.tensor_tensor(out=wkv[:], in0=wkv[:], in1=sb[:], op=ALU.mult)
+                nc.vector.tensor_tensor(out=wkv[:], in0=v_ps[:], in1=wkv[:], op=ALU.subtract)
+                wkv_ps = psum.tile([P, TOK_TILES, P], F32, name="wkv_ps", tag="wkv")
+                for q in range(TOK_TILES):
+                    nc.tensor.transpose(wkv_ps[:, q, :], wkv[:, q * P : (q + 1) * P], ident_f32[:])
+                tiles[n] = wkv_ps
+
+            def gate_unit(n):
+                hf, j = units[n]
+                ch = slice(j * P, (j + 1) * P)
+                nc.vector.tensor_tensor(
+                    out=h_half[hf][:, :, ch], in0=tiles[n][:], in1=gate[hf][:, :, ch], op=ALU.mult
+                )
+
+            def copy_out(on_vector, dst, src):
+                if on_vector:
+                    nc.vector.tensor_copy(out=dst, in_=src)
+                else:
+                    nc.scalar.copy(out=dst, in_=src)
+
+            def regroup_h(hf, q, on_vector):
+                h_ps = psum.tile([P, PLANES, P], BF16, name="h_ps", tag="misc")
+                for pl in range(PLANES):
+                    g, t = divmod(pl, PACK)
+                    nc.tensor.transpose(
+                        h_ps[:, pl, :], h_half[hf][:, q, g * 512 + t : (g + 1) * 512 : PACK], ident_bf[:]
+                    )
+                h_grouped = epi.tile([P, GROUPS, P, PACK], BF16, name="h_grouped", align_bytes=64)
+                copy_out(on_vector, h_grouped[:], h_ps[:].rearrange("p (g t) n -> p g n t", g=GROUPS))
+                tiles[(hf, q)] = h_grouped
+
+            def project(hf, q, on_vector):
+                h_code = epi.tile([P, GROUPS, P], U32, name="h_code", align_bytes=64)
+                h_scale = epi.tile([P, GROUPS, P], U8, name="h_scale", align_bytes=64)
+                nc.vector.quantize_mx(
+                    out=h_code[:].rearrange("p g n -> p (g n)").bitcast(FP8X4),
+                    scales=h_scale[:].rearrange("p g n -> p (g n)"),
+                    in_=tiles[(hf, q)][:].rearrange("p g n t -> p (g n t)"),
+                )
+                result = epi.tile([P, C], F32, name="result")
+                for nh in range(C // 512):
+                    n_cols = slice(nh * 512, (nh + 1) * 512)
+                    out_ps = psum.tile([P, 512], F32, name="out_ps", tag="misc")
+                    mx_product(out_ps[:], h_code, h_scale, slice(0, P), w_code[W_OUT], w_scale[:, W_OUT], n_cols)
+                    copy_out(on_vector, result[:, n_cols], out_ps[:])
+                first = hf * HALF + q * P
+                nc.sync.dma_start(out=out_rows[first : first + P, :], in_=result[:])
+
+            start_unit(0)
+            for n in range(len(units)):
+                hf, j = units[n]
+                weigh_unit(n)
+                if n + 1 < len(units):
+                    start_unit(n + 1)
+                if n >= 1:
+                    gate_unit(n - 1)
+                if hf + 1 < HALVES:
+                    gate_piece(hf + 1, j)
+                if hf >= 1 and j % 2 == 0:
+                    regroup_h(hf - 1, j // 2, False)
+                if hf >= 1 and j % 2 == 1:
+                    project(hf - 1, j // 2, False)
+                blend_unit(n)
+            gate_unit(len(units) - 1)
+            last = HALVES - 1
+            regroup_h(last, 0, False)
+            for q in range(TOK_TILES):
+                if q + 1 < TOK_TILES:
+                    regroup_h(last, q + 1, (q + 1) % 2 == 1)
+                project(last, q, q % 2 == 1)

@@ -26,7 +26,10 @@ TOK_TILES = HALF // P
 LEAD = 16
 PITCH = LEAD + T
 
-ROW_W, ROW_U, ROW_A0, ROW_B0, ROW_XPREV, ROW_MU, ROWS = 0, 1, 2, 6, 10, 14, 17
+ROW_XPREV, ROW_MU = 0, 4
+ROW_W, ROW_B0 = 0, 1
+ROW_U, ROW_A0 = 0, 1
+ROWS = 1 + B
 MIX_R, MIX_K, MIX_V, W_OUT = 0, 1, 2, 3
 
 FLOPS = 4 * 2 * B * T * C * C
@@ -46,31 +49,44 @@ def tile_rwkv_timemix_pa_kernel(
     with ExitStack() as ctx:
         keep = ctx.enter_context(tc.tile_pool(name="keep", bufs=1))
         rows = ctx.enter_context(tc.tile_pool(name="rows", bufs=HALVES))
-        psum = ctx.enter_context(tc.psum_pool(name="psum", bufs=2))
         ctx.enter_context(tc.manual_schedule())
 
-        small = keep.tile([P, C], BF16, name="small")
-        nc.vector.memset(small[:].bitcast(I32), 0)
-        nc.scalar.dma_start(out=small[ROW_W : ROW_W + 1, :], in_=w.unsqueeze(0))
-        nc.scalar.dma_start(out=small[ROW_U : ROW_U + 1, :], in_=u.unsqueeze(0))
-        nc.scalar.dma_start(out=small[ROW_A0 : ROW_A0 + B, :], in_=a0)
-        nc.scalar.dma_start(out=small[ROW_B0 : ROW_B0 + B, :], in_=b0)
-        nc.scalar.dma_start(out=small[ROW_XPREV : ROW_XPREV + B, :], in_=x_prev0)
-        for m, mu in enumerate((mu_r, mu_k, mu_v)):
-            nc.scalar.dma_start(out=small[ROW_MU + m : ROW_MU + m + 1, :], in_=mu.unsqueeze(0))
-
+        small_mix = keep.tile([P, C], BF16, name="small_mix")
+        nc.vector.memset(small_mix[:].bitcast(I32), 0)
+        small_decay = keep.tile([P, C], BF16, name="small_decay")
+        nc.vector.memset(small_decay[:].bitcast(I32), 0)
+        small_state = keep.tile([P, C], BF16, name="small_state")
+        nc.vector.memset(small_state[:].bitcast(I32), 0)
         x_half = []
         for hf in range(HALVES):
-            xh = rows.tile([P, TOK_TILES, C], BF16, name="x_half%d" % hf, tag="rows")
+            x_half.append(rows.tile([P, TOK_TILES, C], BF16, name="x_half%d" % hf, tag="rows"))
+
+        def load_x(hf):
             nc.sync.dma_start(
-                out=xh[:],
+                out=x_half[hf][:],
                 in_=x_rows[hf * HALF : (hf + 1) * HALF, :].rearrange("(q p) c -> p q c", p=P),
             )
-            x_half.append(xh)
+
+        load_x(0)
+        nc.scalar.dma_start(out=small_mix[ROW_XPREV : ROW_XPREV + B, :], in_=x_prev0)
+        for m, mu in enumerate((mu_r, mu_k, mu_v)):
+            nc.scalar.dma_start(out=small_mix[ROW_MU + m : ROW_MU + m + 1, :], in_=mu.unsqueeze(0))
+        nc.scalar.dma_start(out=small_decay[ROW_W : ROW_W + 1, :], in_=w.unsqueeze(0))
+        nc.scalar.dma_start(out=small_decay[ROW_B0 : ROW_B0 + B, :], in_=b0)
+        nc.scalar.dma_start(out=small_state[ROW_U : ROW_U + 1, :], in_=u.unsqueeze(0))
+        nc.scalar.dma_start(out=small_state[ROW_A0 : ROW_A0 + B, :], in_=a0)
+        load_x(1)
+
+        ident_bf = keep.tile([P, P], BF16, name="ident_bf")
+        make_identity(nc, ident_bf[:])
+        steps_int = keep.tile([P, T], I32, name="steps_int")
+        nc.gpsimd.iota(steps_int[:], pattern=[[1, T]], base=1, channel_multiplier=0)
+        ident_f32 = keep.tile([P, P], F32, name="ident_f32")
+        make_identity(nc, ident_f32[:])
 
         w_scale = keep.tile([P, 4, GROUPS, C], U8, name="w_scale", align_bytes=64)
         nc.vector.memset(w_scale[:].rearrange("p a g n -> p (a g n)").bitcast(I32), 0)
-        for wi in (MIX_K, MIX_V, MIX_R, W_OUT):
+        for wi in (MIX_R, MIX_K, MIX_V, W_OUT):
             by_row = weight_scales[wi].rearrange("g (q r) n -> r q g n", r=4)
             for r in range(4):
                 nc.sync.dma_start(
@@ -79,119 +95,98 @@ def tile_rwkv_timemix_pa_kernel(
         w_code = []
         for wi in range(4):
             w_code.append(keep.tile([P, GROUPS, C], U32, name="w_code%d" % wi, align_bytes=64))
-        for wi in (MIX_K, MIX_V, MIX_R, W_OUT):
+        for wi in (MIX_R, MIX_K, MIX_V, W_OUT):
             for g in range(GROUPS):
                 nc.sync.dma_start(
                     out=w_code[wi][:, g, :].bitcast(I32),
                     in_=weight_words[wi][g].rearrange("p n t -> p (n t)").bitcast(I32),
                 )
 
-        ident_bf = keep.tile([P, P], BF16, name="ident_bf")
-        make_identity(nc, ident_bf[:])
-        ident_f32 = keep.tile([P, P], F32, name="ident_f32")
-        make_identity(nc, ident_f32[:])
-        steps_int = keep.tile([P, T], I32, name="steps_int")
-        nc.gpsimd.iota(steps_int[:], pattern=[[1, T]], base=1, channel_multiplier=0)
+        minus_before = keep.tile([P, 2, T], BF16, name="minus_before")
+        nc.vector.memset(minus_before[:].rearrange("p a n -> p (a n)").bitcast(I32), 0)
+        minus_prev0 = keep.tile([P, B, T], BF16, name="minus_prev0")
+        nc.vector.memset(minus_prev0[:].rearrange("p a n -> p (a n)").bitcast(I32), 0)
+        for a in range(2):
+            own = minus_before[:, a, a * P : (a + 1) * P]
+            nc.vector.tensor_copy(out=own, in_=ident_bf[:])
+            width = min(P, T - a * P - 1)
+            nxt = minus_before[:, a, a * P + 1 : a * P + 1 + width]
+            nc.vector.tensor_tensor(out=nxt, in0=nxt, in1=ident_bf[:, 0:width], op=ALU.subtract)
+        for b in range(B):
+            nc.vector.tensor_scalar_mul(
+                out=minus_prev0[:, b, 0:1], in0=ident_bf[:, ROW_XPREV + b : ROW_XPREV + b + 1], scalar1=-1.0
+            )
         steps = keep.tile([P, T], F32, name="steps")
         nc.vector.tensor_copy(out=steps[:], in_=steps_int[:])
         eps_col = keep.tile([P, 1], F32, name="eps_col")
         nc.vector.memset(eps_col[:], EPS)
 
-        by_tile_ps = psum.tile([P, CH_TILES, P], BF16, name="by_tile_ps", tag="k")
-        for j in range(CH_TILES):
-            nc.tensor.transpose(by_tile_ps[:, j, :], small[:, j * P : (j + 1) * P], ident_bf[:])
-        by_tile = keep.tile([P, CH_TILES, ROWS], F32, name="by_tile")
-        nc.vector.tensor_copy(out=by_tile[:], in_=by_tile_ps[:, :, 0:ROWS])
-
-        by_plane_ps = psum.tile([P, PLANES, P], BF16, name="by_plane_ps", tag="v")
-        for pl in range(PLANES):
-            g, t = divmod(pl, PACK)
-            nc.tensor.transpose(
-                by_plane_ps[:, pl, :], small[:, g * 512 + t : (g + 1) * 512 : PACK], ident_bf[:]
-            )
-        mu_plane = keep.tile([P, PLANES, 3], F32, name="mu_plane")
-        nc.vector.tensor_copy(out=mu_plane[:], in_=by_plane_ps[:, :, ROW_MU : ROW_MU + 3])
-
-        a0_t = by_tile[:, :, ROW_A0 : ROW_A0 + B]
-        b0_t = by_tile[:, :, ROW_B0 : ROW_B0 + B]
-        neg_w = keep.tile([P, CH_TILES, 1], F32, name="neg_w")
-        nc.vector.tensor_scalar_mul(out=neg_w[:], in0=by_tile[:, :, ROW_W : ROW_W + 1], scalar1=-1.0)
-        neg_u = keep.tile([P, CH_TILES, 1], F32, name="neg_u")
-        nc.vector.tensor_scalar_mul(out=neg_u[:], in0=by_tile[:, :, ROW_U : ROW_U + 1], scalar1=-1.0)
-        inv_b0 = keep.tile([P, CH_TILES, B], F32, name="inv_b0")
-        nc.vector.reciprocal(out=inv_b0[:], in_=b0_t)
-        neg_ratio = keep.tile([P, CH_TILES, B], F32, name="neg_ratio")
-        nc.vector.scalar_tensor_tensor(
-            out=neg_ratio[:], in0=a0_t, scalar=-1.0, in1=inv_b0[:], op0=ALU.mult, op1=ALU.mult
-        )
-
-        decay = keep.tile([P, CH_TILES, T], F32, name="decay")
-        for j in range(CH_TILES):
-            nc.scalar.activation(out=decay[:, j, :], in_=steps[:], func=ACT.Exp, scale=neg_w[:, j, :])
-        ln_b0_eps = keep.tile([P, CH_TILES, B], F32, name="ln_b0_eps")
-        nc.scalar.activation(out=ln_b0_eps[:], in_=b0_t, func=ACT.Ln, scale=1.0 / EPS)
-        ln_bt = keep.tile([P, CH_TILES, B, T], F32, name="ln_bt")
-
-        def log_of_bt(j):
-            for b in range(B):
-                nc.scalar.activation(
-                    out=ln_bt[:, j, b, :], in_=decay[:, j, :], func=ACT.Ln,
-                    scale=by_tile[:, j, ROW_B0 + b : ROW_B0 + b + 1], bias=eps_col[:],
-                )
-
-        def mx_product(acc, lhs_code, lhs_scale, lhs_cols, rhs_code, rhs_scale, rhs_cols):
-            for g in range(GROUPS):
-                nc.tensor.matmul_mx(
-                    out=acc,
-                    lhsT=lhs_code[:, g, lhs_cols].bitcast(FP8X4),
-                    lhsT_scale=lhs_scale[:, g, lhs_cols],
-                    rhs=rhs_code[:, g, rhs_cols].bitcast(FP8X4),
-                    rhs_scale=rhs_scale[:, g, rhs_cols],
-                    start=(g == 0),
-                    stop=(g == GROUPS - 1),
-                )
-
         x_code, x_scale = [], []
         for m in range(3):
             x_code.append(keep.tile([P, GROUPS, B * T], U32, name="x_code%d" % m, align_bytes=64))
             x_scale.append(keep.tile([P, GROUPS, B * T], U8, name="x_scale%d" % m, align_bytes=64))
-
+        by_decay = keep.tile([P, CH_TILES, ROWS], F32, name="by_decay")
+        by_state = keep.tile([P, CH_TILES, ROWS], F32, name="by_state")
+        mu_plane = keep.tile([P, PLANES, 3], F32, name="mu_plane")
+        neg_w = keep.tile([P, CH_TILES, 1], F32, name="neg_w")
+        neg_u = keep.tile([P, CH_TILES, 1], F32, name="neg_u")
+        inv_b0 = keep.tile([P, CH_TILES, B], F32, name="inv_b0")
+        neg_ratio = keep.tile([P, CH_TILES, B], F32, name="neg_ratio")
+        decay = keep.tile([P, CH_TILES, T], F32, name="decay")
+        ln_b0_eps = keep.tile([P, CH_TILES, B], F32, name="ln_b0_eps")
+        ln_bt = keep.tile([P, CH_TILES, B, T], F32, name="ln_bt")
         gate = []
         for hf in range(HALVES):
             gate.append(keep.tile([P, TOK_TILES, C], F32, name="gate%d" % hf))
 
-        def gate_piece(hf, piece):
-            q, nh = divmod(piece, C // 512)
-            first = hf * HALF + q * P
-            n_cols = slice(nh * 512, (nh + 1) * 512)
-            r_ps = psum.tile([P, 512], F32, name="r_ps", tag="misc")
-            mx_product(
-                r_ps[:], x_code[MIX_R], x_scale[MIX_R], slice(first, first + P),
-                w_code[MIX_R], w_scale[:, MIX_R], n_cols,
-            )
-            nc.scalar.activation(out=gate[hf][:, q, n_cols], in_=r_ps[:], func=ACT.Sigmoid)
-
-        with tc.tile_pool(name="mix", bufs=2) as mix:
+        with tc.psum_pool(name="psum_mix", bufs=2) as psum_mix, tc.tile_pool(name="mix", bufs=2) as mix:
+            by_plane_ps = psum_mix.tile([P, PLANES, P], BF16, name="by_plane_ps", tag="xt")
+            for pl in range(PLANES):
+                g, t = divmod(pl, PACK)
+                nc.tensor.transpose(
+                    by_plane_ps[:, pl, :], small_mix[:, g * 512 + t : (g + 1) * 512 : PACK], ident_bf[:]
+                )
+            nc.vector.tensor_copy(out=mu_plane[:], in_=by_plane_ps[:, :, ROW_MU : ROW_MU + 3])
             x_planes = mix.tile([P, PLANES, B, PITCH], BF16, name="x_planes", bufs=1)
             nc.vector.tensor_copy(
                 out=x_planes[:, :, :, LEAD - 1 : LEAD],
                 in_=by_plane_ps[:, :, ROW_XPREV : ROW_XPREV + B].unsqueeze(3),
             )
 
-            def transpose_x(hf, pair):
-                xt_ps = psum.tile([P, 2, HALF], BF16, name="xt_ps", tag="misc")
-                for k in range(2):
-                    g, t = divmod(2 * pair + k, PACK)
-                    for q in range(TOK_TILES):
-                        nc.tensor.transpose(
-                            xt_ps[:, k, q * P : (q + 1) * P],
-                            x_half[hf][:, q, g * 512 + t : (g + 1) * 512 : PACK],
-                            ident_bf[:],
-                        )
-                nc.scalar.copy(
-                    out=x_planes[:, 2 * pair : 2 * pair + 2, hf * SEQ_HALF : (hf + 1) * SEQ_HALF, LEAD:PITCH],
-                    in_=xt_ps[:].rearrange("p k (s t) -> p k s t", s=SEQ_HALF),
-                )
+            def prepare(hf, g):
+                banks = []
+                for pair in range(PACK // 2):
+                    first_plane = g * PACK + 2 * pair
+                    xt_ps = psum_mix.tile([P, 2, HALF], BF16, name="xt_ps", tag="xt")
+                    for k in range(2):
+                        chans = slice(g * 512 + 2 * pair + k, (g + 1) * 512, PACK)
+                        for q in range(TOK_TILES):
+                            nc.tensor.transpose(
+                                xt_ps[:, k, q * P : (q + 1) * P], x_half[hf][:, q, chans], ident_bf[:]
+                            )
+                    nc.scalar.copy(
+                        out=x_planes[:, first_plane : first_plane + 2, hf * SEQ_HALF : (hf + 1) * SEQ_HALF, LEAD:PITCH],
+                        in_=xt_ps[:].rearrange("p k (s t) -> p k s t", s=SEQ_HALF),
+                    )
+                    for k in range(2):
+                        chans = slice(g * 512 + 2 * pair + k, (g + 1) * 512, PACK)
+                        diff_ps = psum_mix.tile([P, SEQ_HALF, T], F32, name="diff_ps", tag="diff", bufs=6)
+                        for s in range(SEQ_HALF):
+                            acc = diff_ps[:, s, :]
+                            nc.tensor.matmul(
+                                acc, lhsT=x_half[hf][:, 2 * s, chans], rhs=minus_before[:, 0, :],
+                                start=True, stop=False,
+                            )
+                            nc.tensor.matmul(
+                                acc, lhsT=x_half[hf][:, 2 * s + 1, chans], rhs=minus_before[:, 1, :],
+                                start=False, stop=False,
+                            )
+                            nc.tensor.matmul(
+                                acc, lhsT=small_mix[:, chans], rhs=minus_prev0[:, hf * SEQ_HALF + s, :],
+                                start=False, stop=True,
+                            )
+                        banks.append(diff_ps)
+                return banks
 
             def quantise_x(grouped, m, g, hf):
                 cols = slice(hf * HALF, (hf + 1) * HALF)
@@ -201,48 +196,91 @@ def tile_rwkv_timemix_pa_kernel(
                     in_=grouped[:].rearrange("p n t -> p (n t)"),
                 )
 
-            for pair in range(PLANES // 2):
-                transpose_x(0, pair)
+            def log_of_bt(j):
+                for b in range(B):
+                    nc.scalar.activation(
+                        out=ln_bt[:, j, b, :], in_=decay[:, j, :], func=ACT.Ln,
+                        scale=by_decay[:, j, ROW_B0 + b : ROW_B0 + b + 1], bias=eps_col[:],
+                    )
+
+            def by_channel_tile(dst, small):
+                small_ps = psum_mix.tile([P, CH_TILES, P], BF16, name="small_ps", tag="xt")
+                for j in range(CH_TILES):
+                    nc.tensor.transpose(small_ps[:, j, :], small[:, j * P : (j + 1) * P], ident_bf[:])
+                nc.vector.tensor_copy(out=dst[:], in_=small_ps[:, :, 0:ROWS])
+
+            by_channel_tile(by_decay, small_decay)
+            nc.vector.tensor_scalar_mul(out=neg_w[:], in0=by_decay[:, :, ROW_W : ROW_W + 1], scalar1=-1.0)
+            for j in range(CH_TILES):
+                nc.scalar.activation(out=decay[:, j, :], in_=steps[:], func=ACT.Exp, scale=neg_w[:, j, :])
+            nc.scalar.activation(
+                out=ln_b0_eps[:], in_=by_decay[:, :, ROW_B0 : ROW_B0 + B], func=ACT.Ln, scale=1.0 / EPS
+            )
+
+            steps_of_mix = [(hf, g) for hf in range(HALVES) for g in range(GROUPS)]
+            diff_banks = prepare(*steps_of_mix[0])
 
             waiting = None
-            for hf in range(HALVES):
+            for step, (hf, g) in enumerate(steps_of_mix):
                 seqs = slice(hf * SEQ_HALF, (hf + 1) * SEQ_HALF)
-                for g in range(GROUPS):
-                    planes = slice(g * PACK, (g + 1) * PACK)
-                    diff = mix.tile([P, PACK, SEQ_HALF, T], F32, name="diff", bufs=1)
-                    nc.vector.tensor_tensor(
-                        out=diff[:], in0=x_planes[:, planes, seqs, LEAD:PITCH],
-                        in1=x_planes[:, planes, seqs, LEAD - 1 : PITCH - 1], op=ALU.subtract,
-                    )
-                    for m in (MIX_R, MIX_K, MIX_V):
-                        mixed = mix.tile([P, PACK, HALF], BF16, name="mixed%d" % m)
-                        for t in range(PACK):
-                            nc.vector.scalar_tensor_tensor(
-                                out=mixed[:, t, :].rearrange("p (s t) -> p s t", s=SEQ_HALF),
-                                in0=diff[:, t, :, :], scalar=mu_plane[:, g * PACK + t, m : m + 1],
-                                in1=x_planes[:, g * PACK + t, seqs, LEAD - 1 : PITCH - 1],
-                                op0=ALU.mult, op1=ALU.add,
-                            )
-                        grouped = mix.tile([P, HALF, PACK], BF16, name="grouped", bufs=3, align_bytes=64)
-                        by_token = mixed[:].rearrange("p t n -> p n t")
-                        if m == MIX_V:
-                            nc.vector.tensor_copy(out=grouped[:], in_=by_token)
-                        else:
-                            nc.scalar.copy(out=grouped[:], in_=by_token)
-                        if waiting is not None:
-                            quantise_x(*waiting)
-                        waiting = (grouped, m, g, hf)
-                    step = hf * GROUPS + g
-                    if hf + 1 < HALVES:
-                        transpose_x(hf + 1, 2 * g)
-                        transpose_x(hf + 1, 2 * g + 1)
-                    for j in range(3 * step, min(3 * step + 3, CH_TILES)):
-                        log_of_bt(j)
+                for m in (MIX_R, MIX_K, MIX_V):
+                    mixed = mix.tile([P, PACK, HALF], BF16, name="mixed%d" % m)
+                    for t in range(PACK):
+                        nc.vector.scalar_tensor_tensor(
+                            out=mixed[:, t, :].rearrange("p (s t) -> p s t", s=SEQ_HALF),
+                            in0=diff_banks[t][:], scalar=mu_plane[:, g * PACK + t, m : m + 1],
+                            in1=x_planes[:, g * PACK + t, seqs, LEAD - 1 : PITCH - 1],
+                            op0=ALU.mult, op1=ALU.add,
+                        )
+                    grouped = mix.tile([P, HALF, PACK], BF16, name="grouped", bufs=3, align_bytes=64)
+                    dst = grouped[:].rearrange("p (c i) t -> p c t i", i=4)
+                    src = mixed[:].rearrange("p t (c i) -> p c t i", i=4)
+                    if m == MIX_V:
+                        nc.vector.tensor_copy(out=dst, in_=src)
+                    else:
+                        nc.scalar.copy(out=dst, in_=src)
+                    if waiting is not None:
+                        quantise_x(*waiting)
+                    waiting = (grouped, m, g, hf)
+                if step + 1 < len(steps_of_mix):
+                    diff_banks = prepare(*steps_of_mix[step + 1])
+                for j in range(3 * step, min(3 * step + 3, CH_TILES)):
+                    log_of_bt(j)
             quantise_x(*waiting)
-            for piece in range(2 * TOK_TILES):
-                gate_piece(0, piece)
 
-        with tc.tile_pool(name="epi", bufs=2, reuse_waits="tile") as epi:
+            by_channel_tile(by_state, small_state)
+            nc.vector.tensor_scalar_mul(out=neg_u[:], in0=by_state[:, :, ROW_U : ROW_U + 1], scalar1=-1.0)
+            nc.vector.reciprocal(out=inv_b0[:], in_=by_decay[:, :, ROW_B0 : ROW_B0 + B])
+            nc.vector.scalar_tensor_tensor(
+                out=neg_ratio[:], in0=by_state[:, :, ROW_A0 : ROW_A0 + B], scalar=-1.0, in1=inv_b0[:],
+                op0=ALU.mult, op1=ALU.mult,
+            )
+
+        with tc.psum_pool(name="psum", bufs=2, reuse_waits="tile") as psum, tc.tile_pool(name="epi", bufs=2, reuse_waits="tile") as epi:
+
+            def mx_product(acc, lhs_code, lhs_scale, lhs_cols, rhs_code, rhs_scale, rhs_cols):
+                for g in range(GROUPS):
+                    nc.tensor.matmul_mx(
+                        out=acc,
+                        lhsT=lhs_code[:, g, lhs_cols].bitcast(FP8X4),
+                        lhsT_scale=lhs_scale[:, g, lhs_cols],
+                        rhs=rhs_code[:, g, rhs_cols].bitcast(FP8X4),
+                        rhs_scale=rhs_scale[:, g, rhs_cols],
+                        start=(g == 0),
+                        stop=(g == GROUPS - 1),
+                    )
+
+            def gate_piece(hf, piece):
+                q, nh = divmod(piece, C // 512)
+                first = hf * HALF + q * P
+                n_cols = slice(nh * 512, (nh + 1) * 512)
+                r_ps = psum.tile([P, 512], F32, name="r_ps", tag="misc")
+                mx_product(
+                    r_ps[:], x_code[MIX_R], x_scale[MIX_R], slice(first, first + P),
+                    w_code[MIX_R], w_scale[:, MIX_R], n_cols,
+                )
+                nc.scalar.activation(out=gate[hf][:, q, n_cols], in_=r_ps[:], func=ACT.Sigmoid)
+
             h_half = []
             for hf in range(HALVES):
                 h_half.append(rows.tile([P, TOK_TILES, C], BF16, name="h_half%d" % hf, tag="rows"))
@@ -254,9 +292,9 @@ def tile_rwkv_timemix_pa_kernel(
                 hf, j = units[n]
                 ch = slice(j * P, (j + 1) * P)
                 tokens = slice(hf * HALF, (hf + 1) * HALF)
-                k_ps = psum.tile([P, HALF], F32, name="k_ps", tag="k")
+                k_ps = psum.tile([P, HALF], F32, name="k_ps", tag="k", bufs=1)
                 mx_product(k_ps[:], w_code[MIX_K], w_scale[:, MIX_K], ch, x_code[MIX_K], x_scale[MIX_K], tokens)
-                v_ps = psum.tile([P, HALF], F32, name="v_ps", tag="v")
+                v_ps = psum.tile([P, HALF], F32, name="v_ps", tag="v", bufs=3)
                 mx_product(v_ps[:], w_code[MIX_V], w_scale[:, MIX_V], ch, x_code[MIX_V], x_scale[MIX_V], tokens)
                 rho = epi.tile([P, SEQ_HALF, T], F32, name="rho")
                 for s in range(SEQ_HALF):
@@ -276,7 +314,7 @@ def tile_rwkv_timemix_pa_kernel(
                     in1=ln_bt[:, j, hf * SEQ_HALF : (hf + 1) * SEQ_HALF, :].rearrange("p s t -> p (s t)"),
                 )
                 nc.scalar.activation(out=sb[:], in_=sb[:], func=ACT.Sigmoid, scale=-1.0, bias=neg_u[:, j, :])
-                wkv = epi.tile([P, HALF], F32, name="wkv")
+                wkv = epi.tile([P, HALF], F32, name="wkv", bufs=3)
                 for s in range(SEQ_HALF):
                     b = hf * SEQ_HALF + s
                     nc.vector.scalar_tensor_tensor(
@@ -288,7 +326,7 @@ def tile_rwkv_timemix_pa_kernel(
 
             def blend_unit(n):
                 v_ps, sb, wkv = tiles[n]
-                nc.vector.tensor_tensor(out=wkv[:], in0=wkv[:], in1=sb[:], op=ALU.mult)
+                nc.gpsimd.tensor_tensor(out=wkv[:], in0=wkv[:], in1=sb[:], op=ALU.mult)
                 nc.vector.tensor_tensor(out=wkv[:], in0=v_ps[:], in1=wkv[:], op=ALU.subtract)
                 wkv_ps = psum.tile([P, TOK_TILES, P], F32, name="wkv_ps", tag="wkv")
                 for q in range(TOK_TILES):
@@ -336,22 +374,26 @@ def tile_rwkv_timemix_pa_kernel(
                 first = hf * HALF + q * P
                 nc.sync.dma_start(out=out_rows[first : first + P, :], in_=result[:])
 
+            for piece in range(2 * TOK_TILES):
+                gate_piece(0, piece)
             start_unit(0)
-            for n in range(len(units)):
-                hf, j = units[n]
-                weigh_unit(n)
+            for n in range(len(units) + 2):
+                if n < len(units):
+                    weigh_unit(n)
                 if n + 1 < len(units):
                     start_unit(n + 1)
-                if n >= 1:
-                    gate_unit(n - 1)
-                if hf + 1 < HALVES:
-                    gate_piece(hf + 1, j)
-                if hf >= 1 and j % 2 == 0:
-                    regroup_h(hf - 1, j // 2, False)
-                if hf >= 1 and j % 2 == 1:
-                    project(hf - 1, j // 2, False)
-                blend_unit(n)
-            gate_unit(len(units) - 1)
+                if 1 <= n <= len(units):
+                    blend_unit(n - 1)
+                if n >= 2:
+                    gate_unit(n - 2)
+                if n >= 2:
+                    hf, j = units[n - 2]
+                    if hf + 1 < HALVES:
+                        gate_piece(hf + 1, j)
+                    if hf >= 1 and j % 2 == 0:
+                        regroup_h(hf - 1, j // 2, False)
+                    if hf >= 1 and j % 2 == 1:
+                        project(hf - 1, j // 2, False)
             last = HALVES - 1
             regroup_h(last, 0, False)
             for q in range(TOK_TILES):

@@ -153,8 +153,7 @@ def tile_rwkv_timemix_pa_kernel(
                 in_=by_plane_ps[:, :, ROW_XPREV : ROW_XPREV + B].unsqueeze(3),
             )
 
-            def prepare(hf, g):
-                banks = []
+            def prepare_planes(hf, g):
                 for pair in range(PACK // 2):
                     first_plane = g * PACK + 2 * pair
                     xt_ps = psum_mix.tile([P, 2, HALF], BF16, name="xt_ps", tag="xt")
@@ -168,24 +167,27 @@ def tile_rwkv_timemix_pa_kernel(
                         out=x_planes[:, first_plane : first_plane + 2, hf * SEQ_HALF : (hf + 1) * SEQ_HALF, LEAD:PITCH],
                         in_=xt_ps[:].rearrange("p k (s t) -> p k s t", s=SEQ_HALF),
                     )
-                    for k in range(2):
-                        chans = slice(g * 512 + 2 * pair + k, (g + 1) * 512, PACK)
-                        diff_ps = psum_mix.tile([P, SEQ_HALF, T], F32, name="diff_ps", tag="diff", bufs=6)
-                        for s in range(SEQ_HALF):
-                            acc = diff_ps[:, s, :]
-                            nc.tensor.matmul(
-                                acc, lhsT=x_half[hf][:, 2 * s, chans], rhs=minus_before[:, 0, :],
-                                start=True, stop=False,
-                            )
-                            nc.tensor.matmul(
-                                acc, lhsT=x_half[hf][:, 2 * s + 1, chans], rhs=minus_before[:, 1, :],
-                                start=False, stop=False,
-                            )
-                            nc.tensor.matmul(
-                                acc, lhsT=small_mix[:, chans], rhs=minus_prev0[:, hf * SEQ_HALF + s, :],
-                                start=False, stop=True,
-                            )
-                        banks.append(diff_ps)
+
+            def prepare_differences(hf, g):
+                banks = []
+                for t in range(PACK):
+                    chans = slice(g * 512 + t, (g + 1) * 512, PACK)
+                    diff_ps = psum_mix.tile([P, SEQ_HALF, T], F32, name="diff_ps", tag="diff", bufs=6)
+                    for s in range(SEQ_HALF):
+                        acc = diff_ps[:, s, :]
+                        nc.tensor.matmul(
+                            acc, lhsT=x_half[hf][:, 2 * s, chans], rhs=minus_before[:, 0, :],
+                            start=True, stop=False,
+                        )
+                        nc.tensor.matmul(
+                            acc, lhsT=x_half[hf][:, 2 * s + 1, chans], rhs=minus_before[:, 1, :],
+                            start=False, stop=False,
+                        )
+                        nc.tensor.matmul(
+                            acc, lhsT=small_mix[:, chans], rhs=minus_prev0[:, hf * SEQ_HALF + s, :],
+                            start=False, stop=True,
+                        )
+                    banks.append(diff_ps)
                 return banks
 
             def quantise_x(grouped, m, g, hf):
@@ -218,11 +220,15 @@ def tile_rwkv_timemix_pa_kernel(
             )
 
             steps_of_mix = [(hf, g) for hf in range(HALVES) for g in range(GROUPS)]
-            diff_banks = prepare(*steps_of_mix[0])
+            prepare_planes(*steps_of_mix[0])
+            diff_banks = prepare_differences(*steps_of_mix[0])
 
-            waiting = None
+            late = None
             for step, (hf, g) in enumerate(steps_of_mix):
                 seqs = slice(hf * SEQ_HALF, (hf + 1) * SEQ_HALF)
+                if step + 1 < len(steps_of_mix):
+                    prepare_planes(*steps_of_mix[step + 1])
+                regrouped = []
                 for m in (MIX_R, MIX_K, MIX_V):
                     mixed = mix.tile([P, PACK, HALF], BF16, name="mixed%d" % m)
                     for t in range(PACK):
@@ -232,21 +238,26 @@ def tile_rwkv_timemix_pa_kernel(
                             in1=x_planes[:, g * PACK + t, seqs, LEAD - 1 : PITCH - 1],
                             op0=ALU.mult, op1=ALU.add,
                         )
-                    grouped = mix.tile([P, HALF, PACK], BF16, name="grouped", bufs=3, align_bytes=64)
+                    grouped = mix.tile([P, HALF, PACK], BF16, name="grouped", bufs=5, align_bytes=64)
                     dst = grouped[:].rearrange("p (c i) t -> p c t i", i=4)
                     src = mixed[:].rearrange("p t (c i) -> p c t i", i=4)
                     if m == MIX_V:
-                        nc.vector.tensor_copy(out=dst, in_=src)
-                    else:
                         nc.scalar.copy(out=dst, in_=src)
-                    if waiting is not None:
-                        quantise_x(*waiting)
-                    waiting = (grouped, m, g, hf)
+                    else:
+                        nc.gpsimd.tensor_scalar(
+                            out=dst, in0=src, scalar1=1.0, scalar2=0.0, op0=ALU.mult, op1=ALU.add
+                        )
+                    regrouped.append(grouped)
+                if late is not None:
+                    quantise_x(*late)
+                quantise_x(regrouped[MIX_R], MIX_R, g, hf)
+                quantise_x(regrouped[MIX_K], MIX_K, g, hf)
+                late = (regrouped[MIX_V], MIX_V, g, hf)
                 if step + 1 < len(steps_of_mix):
-                    diff_banks = prepare(*steps_of_mix[step + 1])
+                    diff_banks = prepare_differences(*steps_of_mix[step + 1])
                 for j in range(3 * step, min(3 * step + 3, CH_TILES)):
                     log_of_bt(j)
-            quantise_x(*waiting)
+            quantise_x(*late)
 
             by_channel_tile(by_state, small_state)
             nc.vector.tensor_scalar_mul(out=neg_u[:], in0=by_state[:, :, ROW_U : ROW_U + 1], scalar1=-1.0)
@@ -256,7 +267,8 @@ def tile_rwkv_timemix_pa_kernel(
                 op0=ALU.mult, op1=ALU.mult,
             )
 
-        with tc.psum_pool(name="psum", bufs=2, reuse_waits="tile") as psum, tc.tile_pool(name="epi", bufs=2, reuse_waits="tile") as epi:
+        epi = ctx.enter_context(tc.tile_pool(name="epi", bufs=2, reuse_waits="tile"))
+        with tc.psum_pool(name="psum", bufs=2, reuse_waits="tile") as psum:
 
             def mx_product(acc, lhs_code, lhs_scale, lhs_cols, rhs_code, rhs_scale, rhs_cols):
                 for g in range(GROUPS):
@@ -346,18 +358,18 @@ def tile_rwkv_timemix_pa_kernel(
                 else:
                     nc.scalar.copy(out=dst, in_=src)
 
-            def regroup_h(hf, q, on_vector):
-                h_ps = psum.tile([P, PLANES, P], BF16, name="h_ps", tag="misc")
+            def regroup_h(hf, q, on_vector, banks):
+                h_ps = banks.tile([P, PLANES, P], BF16, name="h_ps", tag="misc")
                 for pl in range(PLANES):
                     g, t = divmod(pl, PACK)
                     nc.tensor.transpose(
                         h_ps[:, pl, :], h_half[hf][:, q, g * 512 + t : (g + 1) * 512 : PACK], ident_bf[:]
                     )
-                h_grouped = epi.tile([P, GROUPS, P, PACK], BF16, name="h_grouped", align_bytes=64)
+                h_grouped = epi.tile([P, GROUPS, P, PACK], BF16, name="h_grouped", bufs=TOK_TILES, align_bytes=64)
                 copy_out(on_vector, h_grouped[:], h_ps[:].rearrange("p (g t) n -> p g n t", g=GROUPS))
                 tiles[(hf, q)] = h_grouped
 
-            def project(hf, q, on_vector):
+            def project(hf, q, on_vector, banks):
                 h_code = epi.tile([P, GROUPS, P], U32, name="h_code", align_bytes=64)
                 h_scale = epi.tile([P, GROUPS, P], U8, name="h_scale", align_bytes=64)
                 nc.vector.quantize_mx(
@@ -365,10 +377,10 @@ def tile_rwkv_timemix_pa_kernel(
                     scales=h_scale[:].rearrange("p g n -> p (g n)"),
                     in_=tiles[(hf, q)][:].rearrange("p g n t -> p (g n t)"),
                 )
-                result = epi.tile([P, C], F32, name="result")
+                result = epi.tile([P, C], F32, name="result", bufs=TOK_TILES)
                 for nh in range(C // 512):
                     n_cols = slice(nh * 512, (nh + 1) * 512)
-                    out_ps = psum.tile([P, 512], F32, name="out_ps", tag="misc")
+                    out_ps = banks.tile([P, 512], F32, name="out_ps", tag="misc")
                     mx_product(out_ps[:], h_code, h_scale, slice(0, P), w_code[W_OUT], w_scale[:, W_OUT], n_cols)
                     copy_out(on_vector, result[:, n_cols], out_ps[:])
                 first = hf * HALF + q * P
@@ -391,12 +403,12 @@ def tile_rwkv_timemix_pa_kernel(
                     if hf + 1 < HALVES:
                         gate_piece(hf + 1, j)
                     if hf >= 1 and j % 2 == 0:
-                        regroup_h(hf - 1, j // 2, False)
+                        regroup_h(hf - 1, j // 2, False, psum)
                     if hf >= 1 and j % 2 == 1:
-                        project(hf - 1, j // 2, False)
-            last = HALVES - 1
-            regroup_h(last, 0, False)
+                        project(hf - 1, j // 2, False, psum)
+
+        with tc.psum_pool(name="psum_end", bufs=8, reuse_waits="tile") as psum_end:
             for q in range(TOK_TILES):
-                if q + 1 < TOK_TILES:
-                    regroup_h(last, q + 1, (q + 1) % 2 == 1)
-                project(last, q, q % 2 == 1)
+                regroup_h(HALVES - 1, q, q % 2 == 1, psum_end)
+            for q in range(TOK_TILES):
+                project(HALVES - 1, q, q % 2 == 1, psum_end)

@@ -79,10 +79,10 @@ def tile_rwkv_timemix_pa_kernel(
 
         ident_bf = keep.tile([P, P], BF16, name="ident_bf")
         make_identity(nc, ident_bf[:])
-        steps_int = keep.tile([P, T], I32, name="steps_int")
-        nc.gpsimd.iota(steps_int[:], pattern=[[1, T]], base=1, channel_multiplier=0)
         ident_f32 = keep.tile([P, P], F32, name="ident_f32")
         make_identity(nc, ident_f32[:])
+        steps_int = keep.tile([P, T], I32, name="steps_int")
+        nc.gpsimd.iota(steps_int[:], pattern=[[1, T]], base=1, channel_multiplier=0)
 
         w_scale = keep.tile([P, 4, GROUPS, C], U8, name="w_scale", align_bytes=64)
         nc.vector.memset(w_scale[:].rearrange("p a g n -> p (a g n)").bitcast(I32), 0)
@@ -154,18 +154,18 @@ def tile_rwkv_timemix_pa_kernel(
             )
 
             def prepare_planes(hf, g):
-                for pair in range(PACK // 2):
-                    first_plane = g * PACK + 2 * pair
-                    xt_ps = psum_mix.tile([P, 2, HALF], BF16, name="xt_ps", tag="xt")
-                    for k in range(2):
-                        chans = slice(g * 512 + 2 * pair + k, (g + 1) * 512, PACK)
-                        for q in range(TOK_TILES):
-                            nc.tensor.transpose(
-                                xt_ps[:, k, q * P : (q + 1) * P], x_half[hf][:, q, chans], ident_bf[:]
-                            )
+                for k in range(PACK // 2):
+                    first_plane = g * PACK + 2 * k
+                    xt_ps = psum_mix.tile([P, HALF], F32, name="xt_ps", tag="xt")
+                    for q in range(TOK_TILES):
+                        nc.tensor.transpose(
+                            xt_ps[:, q * P : (q + 1) * P],
+                            x_half[hf][:, q, :].bitcast(F32)[:, g * 256 + k : (g + 1) * 256 : 2],
+                            ident_f32[:],
+                        )
                     nc.scalar.copy(
                         out=x_planes[:, first_plane : first_plane + 2, hf * SEQ_HALF : (hf + 1) * SEQ_HALF, LEAD:PITCH],
-                        in_=xt_ps[:].rearrange("p k (s t) -> p k s t", s=SEQ_HALF),
+                        in_=xt_ps[:].bitcast(BF16).rearrange("p (s t e) -> p e s t", s=SEQ_HALF, e=2),
                     )
 
             def prepare_differences(hf, g):
@@ -295,7 +295,7 @@ def tile_rwkv_timemix_pa_kernel(
 
             h_half = []
             for hf in range(HALVES):
-                h_half.append(rows.tile([P, TOK_TILES, C], BF16, name="h_half%d" % hf, tag="rows"))
+                h_half.append(rows.tile([P, TOK_TILES, PLANES, P], BF16, name="h_half%d" % hf, tag="rows"))
 
             units = [(hf, j) for hf in range(HALVES) for j in range(CH_TILES)]
             tiles = {}
@@ -348,8 +348,14 @@ def tile_rwkv_timemix_pa_kernel(
             def gate_unit(n):
                 hf, j = units[n]
                 ch = slice(j * P, (j + 1) * P)
+                g, part = divmod(j, PACK)
                 nc.vector.tensor_tensor(
-                    out=h_half[hf][:, :, ch], in0=tiles[n][:], in1=gate[hf][:, :, ch], op=ALU.mult
+                    out=h_half[hf][:, :, g * PACK : (g + 1) * PACK, part * 32 : (part + 1) * 32].rearrange(
+                        "p q t a -> p q a t"
+                    ),
+                    in0=tiles[n][:].rearrange("p q (a t) -> p q a t", t=PACK),
+                    in1=gate[hf][:, :, ch].rearrange("p q (a t) -> p q a t", t=PACK),
+                    op=ALU.mult,
                 )
 
             def copy_out(on_vector, dst, src):
@@ -361,10 +367,7 @@ def tile_rwkv_timemix_pa_kernel(
             def regroup_h(hf, q, on_vector, banks):
                 h_ps = banks.tile([P, PLANES, P], BF16, name="h_ps", tag="misc")
                 for pl in range(PLANES):
-                    g, t = divmod(pl, PACK)
-                    nc.tensor.transpose(
-                        h_ps[:, pl, :], h_half[hf][:, q, g * 512 + t : (g + 1) * 512 : PACK], ident_bf[:]
-                    )
+                    nc.tensor.transpose(h_ps[:, pl, :], h_half[hf][:, q, pl, :], ident_bf[:])
                 h_grouped = epi.tile([P, GROUPS, P, PACK], BF16, name="h_grouped", bufs=TOK_TILES, align_bytes=64)
                 copy_out(on_vector, h_grouped[:], h_ps[:].rearrange("p (g t) n -> p g n t", g=GROUPS))
                 tiles[(hf, q)] = h_grouped
@@ -378,13 +381,13 @@ def tile_rwkv_timemix_pa_kernel(
                     in_=tiles[(hf, q)][:].rearrange("p g n t -> p (g n t)"),
                 )
                 result = epi.tile([P, C], F32, name="result", bufs=TOK_TILES)
+                first = hf * HALF + q * P
                 for nh in range(C // 512):
                     n_cols = slice(nh * 512, (nh + 1) * 512)
                     out_ps = banks.tile([P, 512], F32, name="out_ps", tag="misc")
                     mx_product(out_ps[:], h_code, h_scale, slice(0, P), w_code[W_OUT], w_scale[:, W_OUT], n_cols)
                     copy_out(on_vector, result[:, n_cols], out_ps[:])
-                first = hf * HALF + q * P
-                nc.sync.dma_start(out=out_rows[first : first + P, :], in_=result[:])
+                    nc.sync.dma_start(out=out_rows[first : first + P, n_cols], in_=result[:, n_cols])
 
             for piece in range(2 * TOK_TILES):
                 gate_piece(0, piece)

@@ -295,7 +295,7 @@ def tile_rwkv_timemix_pa_kernel(
 
             h_half = []
             for hf in range(HALVES):
-                h_half.append(rows.tile([P, TOK_TILES, PLANES, P], BF16, name="h_half%d" % hf, tag="rows"))
+                h_half.append(rows.tile([P, TOK_TILES, C], BF16, name="h_half%d" % hf, tag="rows"))
 
             units = [(hf, j) for hf in range(HALVES) for j in range(CH_TILES)]
             tiles = {}
@@ -348,14 +348,8 @@ def tile_rwkv_timemix_pa_kernel(
             def gate_unit(n):
                 hf, j = units[n]
                 ch = slice(j * P, (j + 1) * P)
-                g, part = divmod(j, PACK)
                 nc.vector.tensor_tensor(
-                    out=h_half[hf][:, :, g * PACK : (g + 1) * PACK, part * 32 : (part + 1) * 32].rearrange(
-                        "p q t a -> p q a t"
-                    ),
-                    in0=tiles[n][:].rearrange("p q (a t) -> p q a t", t=PACK),
-                    in1=gate[hf][:, :, ch].rearrange("p q (a t) -> p q a t", t=PACK),
-                    op=ALU.mult,
+                    out=h_half[hf][:, :, ch], in0=tiles[n][:], in1=gate[hf][:, :, ch], op=ALU.mult
                 )
 
             def copy_out(on_vector, dst, src):
@@ -365,11 +359,21 @@ def tile_rwkv_timemix_pa_kernel(
                     nc.scalar.copy(out=dst, in_=src)
 
             def regroup_h(hf, q, on_vector, banks):
-                h_ps = banks.tile([P, PLANES, P], BF16, name="h_ps", tag="misc")
-                for pl in range(PLANES):
-                    nc.tensor.transpose(h_ps[:, pl, :], h_half[hf][:, q, pl, :], ident_bf[:])
+                h_ps = banks.tile([P, GROUPS * 2, P], F32, name="h_ps", tag="misc")
+                words = h_half[hf][:, q, :].bitcast(F32)
+                for g in range(GROUPS):
+                    for k in range(2):
+                        nc.tensor.transpose(
+                            h_ps[:, g * 2 + k, :], words[:, g * 256 + k : (g + 1) * 256 : 2], ident_f32[:]
+                        )
                 h_grouped = epi.tile([P, GROUPS, P, PACK], BF16, name="h_grouped", bufs=TOK_TILES, align_bytes=64)
-                copy_out(on_vector, h_grouped[:], h_ps[:].rearrange("p (g t) n -> p g n t", g=GROUPS))
+                copy_out(
+                    on_vector,
+                    h_grouped[:].rearrange("p g n t -> p (g n t)").bitcast(F32).rearrange(
+                        "p (g n k) -> p g n k", g=GROUPS, k=2
+                    ),
+                    h_ps[:].rearrange("p (g k) n -> p g n k", k=2),
+                )
                 tiles[(hf, q)] = h_grouped
 
             def project(hf, q, on_vector, banks):

@@ -139,6 +139,29 @@ def tile_rwkv_timemix_pa_kernel(
         for hf in range(HALVES):
             gate.append(keep.tile([P, TOK_TILES, C], F32, name="gate%d" % hf))
 
+        def mx_product(acc, lhs_code, lhs_scale, lhs_cols, rhs_code, rhs_scale, rhs_cols):
+            for g in range(GROUPS):
+                nc.tensor.matmul_mx(
+                    out=acc,
+                    lhsT=lhs_code[:, g, lhs_cols].bitcast(FP8X4),
+                    lhsT_scale=lhs_scale[:, g, lhs_cols],
+                    rhs=rhs_code[:, g, rhs_cols].bitcast(FP8X4),
+                    rhs_scale=rhs_scale[:, g, rhs_cols],
+                    start=(g == 0),
+                    stop=(g == GROUPS - 1),
+                )
+
+        def gate_piece(hf, piece, banks):
+            q, nh = divmod(piece, C // 512)
+            first = hf * HALF + q * P
+            n_cols = slice(nh * 512, (nh + 1) * 512)
+            r_ps = banks.tile([P, 512], F32, name="r_ps", tag="misc")
+            mx_product(
+                r_ps[:], x_code[MIX_R], x_scale[MIX_R], slice(first, first + P),
+                w_code[MIX_R], w_scale[:, MIX_R], n_cols,
+            )
+            nc.scalar.activation(out=gate[hf][:, q, n_cols], in_=r_ps[:], func=ACT.Sigmoid)
+
         with tc.psum_pool(name="psum_mix", bufs=2) as psum_mix, tc.tile_pool(name="mix", bufs=2) as mix:
             by_plane_ps = psum_mix.tile([P, PLANES, P], BF16, name="by_plane_ps", tag="xt")
             for pl in range(PLANES):
@@ -172,7 +195,7 @@ def tile_rwkv_timemix_pa_kernel(
                 banks = []
                 for t in range(PACK):
                     chans = slice(g * 512 + t, (g + 1) * 512, PACK)
-                    diff_ps = psum_mix.tile([P, SEQ_HALF, T], F32, name="diff_ps", tag="diff", bufs=6)
+                    diff_ps = psum_mix.tile([P, SEQ_HALF, T], F32, name="diff_ps", tag="diff", bufs=4)
                     for s in range(SEQ_HALF):
                         acc = diff_ps[:, s, :]
                         nc.tensor.matmul(
@@ -223,41 +246,50 @@ def tile_rwkv_timemix_pa_kernel(
             prepare_planes(*steps_of_mix[0])
             diff_banks = prepare_differences(*steps_of_mix[0])
 
-            late = None
-            for step, (hf, g) in enumerate(steps_of_mix):
-                seqs = slice(hf * SEQ_HALF, (hf + 1) * SEQ_HALF)
-                if step + 1 < len(steps_of_mix):
-                    prepare_planes(*steps_of_mix[step + 1])
-                regrouped = []
-                for m in (MIX_R, MIX_K, MIX_V):
-                    mixed = mix.tile([P, PACK, HALF], BF16, name="mixed%d" % m)
-                    for t in range(PACK):
-                        nc.vector.scalar_tensor_tensor(
-                            out=mixed[:, t, :].rearrange("p (s t) -> p s t", s=SEQ_HALF),
-                            in0=diff_banks[t][:], scalar=mu_plane[:, g * PACK + t, m : m + 1],
-                            in1=x_planes[:, g * PACK + t, seqs, LEAD - 1 : PITCH - 1],
-                            op0=ALU.mult, op1=ALU.add,
-                        )
-                    grouped = mix.tile([P, HALF, PACK], BF16, name="grouped", bufs=5, align_bytes=64)
-                    dst = grouped[:].rearrange("p (c i) t -> p c t i", i=4)
-                    src = mixed[:].rearrange("p t (c i) -> p c t i", i=4)
-                    if m == MIX_V:
-                        nc.scalar.copy(out=dst, in_=src)
-                    else:
-                        nc.gpsimd.tensor_scalar(
-                            out=dst, in0=src, scalar1=1.0, scalar2=0.0, op0=ALU.mult, op1=ALU.add
-                        )
-                    regrouped.append(grouped)
-                if late is not None:
-                    quantise_x(*late)
-                quantise_x(regrouped[MIX_R], MIX_R, g, hf)
-                quantise_x(regrouped[MIX_K], MIX_K, g, hf)
-                late = (regrouped[MIX_V], MIX_V, g, hf)
+            mixed_before = None
+            for step in range(len(steps_of_mix) + 1):
+                mixing = step < len(steps_of_mix)
+                if mixing:
+                    hf, g = steps_of_mix[step]
+                    seqs = slice(hf * SEQ_HALF, (hf + 1) * SEQ_HALF)
+                    if step + 1 < len(steps_of_mix):
+                        prepare_planes(*steps_of_mix[step + 1])
+                    fresh = []
+                    for m in (MIX_R, MIX_K, MIX_V):
+                        mixed = mix.tile([P, PACK, HALF], BF16, name="mixed%d" % m)
+                        for t in range(PACK):
+                            nc.vector.scalar_tensor_tensor(
+                                out=mixed[:, t, :].rearrange("p (s t) -> p s t", s=SEQ_HALF),
+                                in0=diff_banks[t][:], scalar=mu_plane[:, g * PACK + t, m : m + 1],
+                                in1=x_planes[:, g * PACK + t, seqs, LEAD - 1 : PITCH - 1],
+                                op0=ALU.mult, op1=ALU.add,
+                            )
+                        fresh.append(mixed)
+                if mixed_before is not None:
+                    regrouped = []
+                    for m in (MIX_R, MIX_K, MIX_V):
+                        grouped = mix.tile([P, HALF, PACK], BF16, name="grouped%d" % m, bufs=1, align_bytes=64)
+                        dst = grouped[:].rearrange("p (c i) t -> p c t i", i=4)
+                        src = mixed_before[0][m][:].rearrange("p t (c i) -> p c t i", i=4)
+                        if m == MIX_V:
+                            nc.scalar.copy(out=dst, in_=src)
+                        elif mixing:
+                            nc.gpsimd.tensor_scalar(
+                                out=dst, in0=src, scalar1=1.0, scalar2=0.0, op0=ALU.mult, op1=ALU.add
+                            )
+                        else:
+                            nc.vector.tensor_copy(out=dst, in_=src)
+                        regrouped.append(grouped)
+                    for m in (MIX_V, MIX_K, MIX_R):
+                        quantise_x(regrouped[m], m, mixed_before[1], mixed_before[2])
+                mixed_before = (fresh, g, hf) if mixing else None
                 if step + 1 < len(steps_of_mix):
                     diff_banks = prepare_differences(*steps_of_mix[step + 1])
                 for j in range(3 * step, min(3 * step + 3, CH_TILES)):
                     log_of_bt(j)
-            quantise_x(*late)
+                if step >= len(steps_of_mix) - 1:
+                    for piece in range(TOK_TILES):
+                        gate_piece(0, (step - len(steps_of_mix) + 1) * TOK_TILES + piece, psum_mix)
 
             by_channel_tile(by_state, small_state)
             nc.vector.tensor_scalar_mul(out=neg_u[:], in0=by_state[:, :, ROW_U : ROW_U + 1], scalar1=-1.0)
@@ -269,29 +301,6 @@ def tile_rwkv_timemix_pa_kernel(
 
         epi = ctx.enter_context(tc.tile_pool(name="epi", bufs=2, reuse_waits="tile"))
         with tc.psum_pool(name="psum", bufs=2, reuse_waits="tile") as psum:
-
-            def mx_product(acc, lhs_code, lhs_scale, lhs_cols, rhs_code, rhs_scale, rhs_cols):
-                for g in range(GROUPS):
-                    nc.tensor.matmul_mx(
-                        out=acc,
-                        lhsT=lhs_code[:, g, lhs_cols].bitcast(FP8X4),
-                        lhsT_scale=lhs_scale[:, g, lhs_cols],
-                        rhs=rhs_code[:, g, rhs_cols].bitcast(FP8X4),
-                        rhs_scale=rhs_scale[:, g, rhs_cols],
-                        start=(g == 0),
-                        stop=(g == GROUPS - 1),
-                    )
-
-            def gate_piece(hf, piece):
-                q, nh = divmod(piece, C // 512)
-                first = hf * HALF + q * P
-                n_cols = slice(nh * 512, (nh + 1) * 512)
-                r_ps = psum.tile([P, 512], F32, name="r_ps", tag="misc")
-                mx_product(
-                    r_ps[:], x_code[MIX_R], x_scale[MIX_R], slice(first, first + P),
-                    w_code[MIX_R], w_scale[:, MIX_R], n_cols,
-                )
-                nc.scalar.activation(out=gate[hf][:, q, n_cols], in_=r_ps[:], func=ACT.Sigmoid)
 
             h_half = []
             for hf in range(HALVES):
@@ -393,8 +402,6 @@ def tile_rwkv_timemix_pa_kernel(
                     copy_out(on_vector, result[:, n_cols], out_ps[:])
                     nc.sync.dma_start(out=out_rows[first : first + P, n_cols], in_=result[:, n_cols])
 
-            for piece in range(2 * TOK_TILES):
-                gate_piece(0, piece)
             start_unit(0)
             for n in range(len(units) + 2):
                 if n < len(units):
@@ -408,7 +415,7 @@ def tile_rwkv_timemix_pa_kernel(
                 if n >= 2:
                     hf, j = units[n - 2]
                     if hf + 1 < HALVES:
-                        gate_piece(hf + 1, j)
+                        gate_piece(hf + 1, j, psum)
                     if hf >= 1 and j % 2 == 0:
                         regroup_h(hf - 1, j // 2, False, psum)
                     if hf >= 1 and j % 2 == 1:

@@ -31,6 +31,8 @@ ROW_W, ROW_B0 = 0, 1
 ROW_U, ROW_A0 = 0, 1
 ROWS = 1 + B
 MIX_R, MIX_K, MIX_V, W_OUT = 0, 1, 2, 3
+BOTH, LOWER, UPPER = (0, 1), (0,), (1,)
+H_BUFS = 5
 
 FLOPS = 4 * 2 * B * T * C * C
 
@@ -49,169 +51,109 @@ def tile_rwkv_timemix_pa_kernel(
     with ExitStack() as ctx:
         keep = ctx.enter_context(tc.tile_pool(name="keep", bufs=1))
         rows = ctx.enter_context(tc.tile_pool(name="rows", bufs=HALVES))
+        carry = ctx.enter_context(tc.tile_pool(name="carry", bufs=2))
         ctx.enter_context(tc.manual_schedule())
 
-        small_mix = keep.tile([P, C], BF16, name="small_mix")
-        nc.vector.memset(small_mix[:].bitcast(I32), 0)
-        small_decay = keep.tile([P, C], BF16, name="small_decay")
-        nc.vector.memset(small_decay[:].bitcast(I32), 0)
-        small_state = keep.tile([P, C], BF16, name="small_state")
-        nc.vector.memset(small_state[:].bitcast(I32), 0)
-        x_half = []
-        for hf in range(HALVES):
-            x_half.append(rows.tile([P, TOK_TILES, C], BF16, name="x_half%d" % hf, tag="rows"))
+        with tc.tile_pool(name="early", bufs=1) as early:
+            small_mix = early.tile([P, C], BF16, name="small_mix")
+            nc.vector.memset(small_mix[:].bitcast(I32), 0)
+            small_decay = early.tile([P, C], BF16, name="small_decay")
+            nc.vector.memset(small_decay[:].bitcast(I32), 0)
+            small_state = early.tile([P, C], BF16, name="small_state")
+            nc.vector.memset(small_state[:].bitcast(I32), 0)
+            x_half = []
+            for hf in range(HALVES):
+                x_half.append(rows.tile([P, TOK_TILES, C], BF16, name="x_half%d" % hf, tag="rows"))
 
-        def load_x(hf):
-            nc.sync.dma_start(
-                out=x_half[hf][:],
-                in_=x_rows[hf * HALF : (hf + 1) * HALF, :].rearrange("(q p) c -> p q c", p=P),
-            )
+            def load_x(hf):
+                for q in range(TOK_TILES):
+                    first = hf * HALF + q * P
+                    nc.sync.dma_start(out=x_half[hf][:, q, :], in_=x_rows[first : first + P, :])
 
-        load_x(0)
-        nc.scalar.dma_start(out=small_mix[ROW_XPREV : ROW_XPREV + B, :], in_=x_prev0)
-        for m, mu in enumerate((mu_r, mu_k, mu_v)):
-            nc.scalar.dma_start(out=small_mix[ROW_MU + m : ROW_MU + m + 1, :], in_=mu.unsqueeze(0))
-        nc.scalar.dma_start(out=small_decay[ROW_W : ROW_W + 1, :], in_=w.unsqueeze(0))
-        nc.scalar.dma_start(out=small_decay[ROW_B0 : ROW_B0 + B, :], in_=b0)
-        nc.scalar.dma_start(out=small_state[ROW_U : ROW_U + 1, :], in_=u.unsqueeze(0))
-        nc.scalar.dma_start(out=small_state[ROW_A0 : ROW_A0 + B, :], in_=a0)
-        load_x(1)
+            load_x(0)
+            nc.scalar.dma_start(out=small_mix[ROW_XPREV : ROW_XPREV + B, :], in_=x_prev0)
+            for m, mu in enumerate((mu_r, mu_k, mu_v)):
+                nc.scalar.dma_start(out=small_mix[ROW_MU + m : ROW_MU + m + 1, :], in_=mu.unsqueeze(0))
+            nc.scalar.dma_start(out=small_decay[ROW_W : ROW_W + 1, :], in_=w.unsqueeze(0))
+            nc.scalar.dma_start(out=small_decay[ROW_B0 : ROW_B0 + B, :], in_=b0)
+            nc.scalar.dma_start(out=small_state[ROW_U : ROW_U + 1, :], in_=u.unsqueeze(0))
+            nc.scalar.dma_start(out=small_state[ROW_A0 : ROW_A0 + B, :], in_=a0)
+            load_x(1)
 
-        ident_bf = keep.tile([P, P], BF16, name="ident_bf")
-        make_identity(nc, ident_bf[:])
-        ident_f32 = keep.tile([P, P], F32, name="ident_f32")
-        make_identity(nc, ident_f32[:])
-        steps_int = keep.tile([P, T], I32, name="steps_int")
-        nc.gpsimd.iota(steps_int[:], pattern=[[1, T]], base=1, channel_multiplier=0)
+            ident_bf = early.tile([P, P], BF16, name="ident_bf")
+            make_identity(nc, ident_bf[:])
+            ident_f32 = keep.tile([P, P], F32, name="ident_f32")
+            make_identity(nc, ident_f32[:])
+            steps_int = early.tile([P, T], I32, name="steps_int")
+            nc.gpsimd.iota(steps_int[:], pattern=[[1, T]], base=1, channel_multiplier=0)
 
-        w_scale = keep.tile([P, 4, GROUPS, C], U8, name="w_scale", align_bytes=64)
-        nc.vector.memset(w_scale[:].rearrange("p a g n -> p (a g n)").bitcast(I32), 0)
-        for wi in (MIX_R, MIX_K, MIX_V, W_OUT):
-            by_row = weight_scales[wi].rearrange("g (q r) n -> r q g n", r=4)
-            for r in range(4):
-                nc.sync.dma_start(
-                    out=w_scale[r:P:32, wi, :, :].bitcast(I32), in_=by_row[r].bitcast(I32)
-                )
-        w_code = []
-        for wi in range(4):
-            w_code.append(keep.tile([P, GROUPS, C], U32, name="w_code%d" % wi, align_bytes=64))
-        for wi in (MIX_R, MIX_K, MIX_V, W_OUT):
-            for g in range(GROUPS):
-                nc.sync.dma_start(
-                    out=w_code[wi][:, g, :].bitcast(I32),
-                    in_=weight_words[wi][g].rearrange("p n t -> p (n t)").bitcast(I32),
-                )
-
-        minus_before = keep.tile([P, 2, T], BF16, name="minus_before")
-        nc.vector.memset(minus_before[:].rearrange("p a n -> p (a n)").bitcast(I32), 0)
-        minus_prev0 = keep.tile([P, B, T], BF16, name="minus_prev0")
-        nc.vector.memset(minus_prev0[:].rearrange("p a n -> p (a n)").bitcast(I32), 0)
-        for a in range(2):
-            own = minus_before[:, a, a * P : (a + 1) * P]
-            nc.vector.tensor_copy(out=own, in_=ident_bf[:])
-            width = min(P, T - a * P - 1)
-            nxt = minus_before[:, a, a * P + 1 : a * P + 1 + width]
-            nc.vector.tensor_tensor(out=nxt, in0=nxt, in1=ident_bf[:, 0:width], op=ALU.subtract)
-        for b in range(B):
-            nc.vector.tensor_scalar_mul(
-                out=minus_prev0[:, b, 0:1], in0=ident_bf[:, ROW_XPREV + b : ROW_XPREV + b + 1], scalar1=-1.0
-            )
-        steps = keep.tile([P, T], F32, name="steps")
-        nc.vector.tensor_copy(out=steps[:], in_=steps_int[:])
-        eps_col = keep.tile([P, 1], F32, name="eps_col")
-        nc.vector.memset(eps_col[:], EPS)
-
-        x_code, x_scale = [], []
-        for m in range(3):
-            x_code.append(keep.tile([P, GROUPS, B * T], U32, name="x_code%d" % m, align_bytes=64))
-            x_scale.append(keep.tile([P, GROUPS, B * T], U8, name="x_scale%d" % m, align_bytes=64))
-        by_decay = keep.tile([P, CH_TILES, ROWS], F32, name="by_decay")
-        by_state = keep.tile([P, CH_TILES, ROWS], F32, name="by_state")
-        mu_plane = keep.tile([P, PLANES, 3], F32, name="mu_plane")
-        neg_w = keep.tile([P, CH_TILES, 1], F32, name="neg_w")
-        neg_u = keep.tile([P, CH_TILES, 1], F32, name="neg_u")
-        inv_b0 = keep.tile([P, CH_TILES, B], F32, name="inv_b0")
-        neg_ratio = keep.tile([P, CH_TILES, B], F32, name="neg_ratio")
-        decay = keep.tile([P, CH_TILES, T], F32, name="decay")
-        ln_b0_eps = keep.tile([P, CH_TILES, B], F32, name="ln_b0_eps")
-        ln_bt = keep.tile([P, CH_TILES, B, T], F32, name="ln_bt")
-        gate = []
-        for hf in range(HALVES):
-            gate.append(keep.tile([P, TOK_TILES, C], F32, name="gate%d" % hf))
-
-        def mx_product(acc, lhs_code, lhs_scale, lhs_cols, rhs_code, rhs_scale, rhs_cols):
-            for g in range(GROUPS):
-                nc.tensor.matmul_mx(
-                    out=acc,
-                    lhsT=lhs_code[:, g, lhs_cols].bitcast(FP8X4),
-                    lhsT_scale=lhs_scale[:, g, lhs_cols],
-                    rhs=rhs_code[:, g, rhs_cols].bitcast(FP8X4),
-                    rhs_scale=rhs_scale[:, g, rhs_cols],
-                    start=(g == 0),
-                    stop=(g == GROUPS - 1),
-                )
-
-        def gate_piece(hf, piece, banks):
-            q, nh = divmod(piece, C // 512)
-            first = hf * HALF + q * P
-            n_cols = slice(nh * 512, (nh + 1) * 512)
-            r_ps = banks.tile([P, 512], F32, name="r_ps", tag="misc")
-            mx_product(
-                r_ps[:], x_code[MIX_R], x_scale[MIX_R], slice(first, first + P),
-                w_code[MIX_R], w_scale[:, MIX_R], n_cols,
-            )
-            nc.scalar.activation(out=gate[hf][:, q, n_cols], in_=r_ps[:], func=ACT.Sigmoid)
-
-        with tc.psum_pool(name="psum_mix", bufs=2) as psum_mix, tc.tile_pool(name="mix", bufs=2) as mix:
-            by_plane_ps = psum_mix.tile([P, PLANES, P], BF16, name="by_plane_ps", tag="xt")
-            for pl in range(PLANES):
-                g, t = divmod(pl, PACK)
-                nc.tensor.transpose(
-                    by_plane_ps[:, pl, :], small_mix[:, g * 512 + t : (g + 1) * 512 : PACK], ident_bf[:]
-                )
-            nc.vector.tensor_copy(out=mu_plane[:], in_=by_plane_ps[:, :, ROW_MU : ROW_MU + 3])
-            x_planes = mix.tile([P, PLANES, B, PITCH], BF16, name="x_planes", bufs=1)
-            nc.vector.tensor_copy(
-                out=x_planes[:, :, :, LEAD - 1 : LEAD],
-                in_=by_plane_ps[:, :, ROW_XPREV : ROW_XPREV + B].unsqueeze(3),
-            )
-
-            def prepare_planes(hf, g):
-                for k in range(PACK // 2):
-                    first_plane = g * PACK + 2 * k
-                    xt_ps = psum_mix.tile([P, HALF], F32, name="xt_ps", tag="xt")
-                    for q in range(TOK_TILES):
-                        nc.tensor.transpose(
-                            xt_ps[:, q * P : (q + 1) * P],
-                            x_half[hf][:, q, :].bitcast(F32)[:, g * 256 + k : (g + 1) * 256 : 2],
-                            ident_f32[:],
-                        )
-                    nc.scalar.copy(
-                        out=x_planes[:, first_plane : first_plane + 2, hf * SEQ_HALF : (hf + 1) * SEQ_HALF, LEAD:PITCH],
-                        in_=xt_ps[:].bitcast(BF16).rearrange("p (s t e) -> p e s t", s=SEQ_HALF, e=2),
+            w_scale = keep.tile([P, 4, GROUPS, C], U8, name="w_scale", align_bytes=64)
+            nc.vector.memset(w_scale[:].rearrange("p a g n -> p (a g n)").bitcast(I32), 0)
+            for wi in (MIX_R, MIX_K, MIX_V, W_OUT):
+                by_row = weight_scales[wi].rearrange("g (q r) n -> r q g n", r=4)
+                for r in range(4):
+                    nc.sync.dma_start(
+                        out=w_scale[r:P:32, wi, :, :].bitcast(I32), in_=by_row[r].bitcast(I32)
+                    )
+            w_code = []
+            for wi in range(4):
+                w_code.append(keep.tile([P, GROUPS, C], U32, name="w_code%d" % wi, align_bytes=64))
+            for wi in (MIX_R, MIX_K, MIX_V, W_OUT):
+                for g in range(GROUPS):
+                    nc.sync.dma_start(
+                        out=w_code[wi][:, g, :].bitcast(I32),
+                        in_=weight_words[wi][g].rearrange("p n t -> p (n t)").bitcast(I32),
                     )
 
-            def prepare_differences(hf, g):
-                banks = []
-                for t in range(PACK):
-                    chans = slice(g * 512 + t, (g + 1) * 512, PACK)
-                    diff_ps = psum_mix.tile([P, SEQ_HALF, T], F32, name="diff_ps", tag="diff", bufs=4)
-                    for s in range(SEQ_HALF):
-                        acc = diff_ps[:, s, :]
-                        nc.tensor.matmul(
-                            acc, lhsT=x_half[hf][:, 2 * s, chans], rhs=minus_before[:, 0, :],
-                            start=True, stop=False,
-                        )
-                        nc.tensor.matmul(
-                            acc, lhsT=x_half[hf][:, 2 * s + 1, chans], rhs=minus_before[:, 1, :],
-                            start=False, stop=False,
-                        )
-                        nc.tensor.matmul(
-                            acc, lhsT=small_mix[:, chans], rhs=minus_prev0[:, hf * SEQ_HALF + s, :],
-                            start=False, stop=True,
-                        )
-                    banks.append(diff_ps)
-                return banks
+            minus_before = early.tile([P, 2, T], BF16, name="minus_before")
+            nc.vector.memset(minus_before[:].rearrange("p a n -> p (a n)").bitcast(I32), 0)
+            minus_prev0 = early.tile([P, B, T], BF16, name="minus_prev0")
+            nc.vector.memset(minus_prev0[:].rearrange("p a n -> p (a n)").bitcast(I32), 0)
+            for a in range(2):
+                own = minus_before[:, a, a * P : (a + 1) * P]
+                nc.vector.tensor_copy(out=own, in_=ident_bf[:])
+                width = min(P, T - a * P - 1)
+                nxt = minus_before[:, a, a * P + 1 : a * P + 1 + width]
+                nc.vector.tensor_tensor(out=nxt, in0=nxt, in1=ident_bf[:, 0:width], op=ALU.subtract)
+            for b in range(B):
+                nc.vector.tensor_scalar_mul(
+                    out=minus_prev0[:, b, 0:1], in0=ident_bf[:, ROW_XPREV + b : ROW_XPREV + b + 1], scalar1=-1.0
+                )
+            steps = keep.tile([P, T], F32, name="steps")
+            nc.vector.tensor_copy(out=steps[:], in_=steps_int[:])
+            eps_col = keep.tile([P, 1], F32, name="eps_col")
+            nc.vector.memset(eps_col[:], EPS)
+
+            x_code, x_scale = [], []
+            for m in range(3):
+                x_code.append(keep.tile([P, GROUPS, B * T], U32, name="x_code%d" % m, align_bytes=64))
+                x_scale.append(keep.tile([P, GROUPS, B * T], U8, name="x_scale%d" % m, align_bytes=64))
+            by_decay = early.tile([P, CH_TILES, ROWS], F32, name="by_decay")
+            by_state = keep.tile([P, CH_TILES, ROWS], F32, name="by_state")
+            mu_plane = keep.tile([P, PLANES, 3], F32, name="mu_plane")
+            neg_w = keep.tile([P, CH_TILES, 1], F32, name="neg_w")
+            neg_u = keep.tile([P, CH_TILES, 1], F32, name="neg_u")
+            inv_b0 = keep.tile([P, CH_TILES, B], F32, name="inv_b0")
+            neg_ratio = keep.tile([P, CH_TILES, B], F32, name="neg_ratio")
+            decay = keep.tile([P, CH_TILES, T], F32, name="decay")
+            ln_b0_eps = keep.tile([P, CH_TILES, B], F32, name="ln_b0_eps")
+            ln_bt = keep.tile([P, CH_TILES, B, T], F32, name="ln_bt")
+            gate = []
+            for hf in range(HALVES):
+                gate.append(keep.tile([P, TOK_TILES, C], F32, name="gate%d" % hf))
+
+            def new_grouped(m):
+                return carry.tile([P, HALF, PACK], BF16, name="grouped%d" % m, bufs=1, align_bytes=64)
+
+            def regroup(m, grouped, mixed, tok):
+                dst = grouped[:, tok, :].rearrange("p (c i) t -> p c t i", i=4)
+                src = mixed[:, :, tok].rearrange("p t (c i) -> p c t i", i=4)
+                if m == MIX_V:
+                    nc.scalar.copy(out=dst, in_=src)
+                else:
+                    nc.gpsimd.tensor_scalar(
+                        out=dst, in0=src, scalar1=1.0, scalar2=0.0, op0=ALU.mult, op1=ALU.add
+                    )
 
             def quantise_x(grouped, m, g, hf):
                 cols = slice(hf * HALF, (hf + 1) * HALF)
@@ -221,83 +163,148 @@ def tile_rwkv_timemix_pa_kernel(
                     in_=grouped[:].rearrange("p n t -> p (n t)"),
                 )
 
-            def log_of_bt(j):
-                for b in range(B):
-                    nc.scalar.activation(
-                        out=ln_bt[:, j, b, :], in_=decay[:, j, :], func=ACT.Ln,
-                        scale=by_decay[:, j, ROW_B0 + b : ROW_B0 + b + 1], bias=eps_col[:],
+            def mx_product(acc, lhs_code, lhs_scale, lhs_cols, rhs_code, rhs_scale, rhs_cols):
+                for g in range(GROUPS):
+                    nc.tensor.matmul_mx(
+                        out=acc,
+                        lhsT=lhs_code[:, g, lhs_cols].bitcast(FP8X4),
+                        lhsT_scale=lhs_scale[:, g, lhs_cols],
+                        rhs=rhs_code[:, g, rhs_cols].bitcast(FP8X4),
+                        rhs_scale=rhs_scale[:, g, rhs_cols],
+                        start=(g == 0),
+                        stop=(g == GROUPS - 1),
                     )
 
-            def by_channel_tile(dst, small):
-                small_ps = psum_mix.tile([P, CH_TILES, P], BF16, name="small_ps", tag="xt")
-                for j in range(CH_TILES):
-                    nc.tensor.transpose(small_ps[:, j, :], small[:, j * P : (j + 1) * P], ident_bf[:])
-                nc.vector.tensor_copy(out=dst[:], in_=small_ps[:, :, 0:ROWS])
+            def gate_piece(hf, piece, banks):
+                nh, q = divmod(piece, TOK_TILES)
+                first = hf * HALF + q * P
+                n_cols = slice(nh * 512, (nh + 1) * 512)
+                r_ps = banks.tile([P, 512], F32, name="r_ps", tag="misc")
+                mx_product(
+                    r_ps[:], x_code[MIX_R], x_scale[MIX_R], slice(first, first + P),
+                    w_code[MIX_R], w_scale[:, MIX_R], n_cols,
+                )
+                nc.scalar.activation(out=gate[hf][:, q, n_cols], in_=r_ps[:], func=ACT.Sigmoid)
 
-            by_channel_tile(by_decay, small_decay)
-            nc.vector.tensor_scalar_mul(out=neg_w[:], in0=by_decay[:, :, ROW_W : ROW_W + 1], scalar1=-1.0)
-            for j in range(CH_TILES):
-                nc.scalar.activation(out=decay[:, j, :], in_=steps[:], func=ACT.Exp, scale=neg_w[:, j, :])
-            nc.scalar.activation(
-                out=ln_b0_eps[:], in_=by_decay[:, :, ROW_B0 : ROW_B0 + B], func=ACT.Ln, scale=1.0 / EPS
-            )
+            with tc.psum_pool(name="psum_mix", bufs=2) as psum_mix:
+                by_plane_ps = psum_mix.tile([P, PLANES, P], BF16, name="by_plane_ps", tag="xt")
+                for pl in range(PLANES):
+                    g, t = divmod(pl, PACK)
+                    nc.tensor.transpose(
+                        by_plane_ps[:, pl, :], small_mix[:, g * 512 + t : (g + 1) * 512 : PACK], ident_bf[:]
+                    )
+                nc.vector.tensor_copy(out=mu_plane[:], in_=by_plane_ps[:, :, ROW_MU : ROW_MU + 3])
+                x_pairs = early.tile([P, PLANES // 2, B, PITCH, 2], BF16, name="x_pairs")
+                nc.vector.tensor_copy(
+                    out=x_pairs[:, :, :, LEAD - 1, :],
+                    in_=by_plane_ps[:, :, ROW_XPREV : ROW_XPREV + B].rearrange("p (r e) b -> p r b e", e=2),
+                )
 
-            steps_of_mix = [(hf, g) for hf in range(HALVES) for g in range(GROUPS)]
-            prepare_planes(*steps_of_mix[0])
-            diff_banks = prepare_differences(*steps_of_mix[0])
+                def before_of(plane, seqs):
+                    return x_pairs[:, plane // 2, seqs, LEAD - 1 : PITCH - 1, plane % 2]
 
-            mixed_before = None
-            for step in range(len(steps_of_mix) + 1):
-                mixing = step < len(steps_of_mix)
-                if mixing:
-                    hf, g = steps_of_mix[step]
+                def prepare_planes(hf, g):
+                    for k in range(PACK // 2):
+                        xt_ps = psum_mix.tile([P, HALF], F32, name="xt_ps", tag="xt")
+                        for q in range(TOK_TILES):
+                            nc.tensor.transpose(
+                                xt_ps[:, q * P : (q + 1) * P],
+                                x_half[hf][:, q, :].bitcast(F32)[:, g * 256 + k : (g + 1) * 256 : 2],
+                                ident_f32[:],
+                            )
+                        nc.scalar.copy(
+                            out=x_pairs[:, g * 2 + k, hf * SEQ_HALF : (hf + 1) * SEQ_HALF, LEAD:PITCH, :]
+                            .rearrange("p s t e -> p s (t e)")
+                            .bitcast(F32),
+                            in_=xt_ps[:].rearrange("p (s t) -> p s t", s=SEQ_HALF),
+                        )
+
+                def prepare_differences(hf, g):
+                    banks = []
+                    for t in range(PACK):
+                        chans = slice(g * 512 + t, (g + 1) * 512, PACK)
+                        diff_ps = psum_mix.tile([P, SEQ_HALF, T], F32, name="diff_ps", tag="diff", bufs=4)
+                        for s in range(SEQ_HALF):
+                            acc = diff_ps[:, s, :]
+                            nc.tensor.matmul(
+                                acc, lhsT=x_half[hf][:, 2 * s, chans], rhs=minus_before[:, 0, :],
+                                start=True, stop=False,
+                            )
+                            nc.tensor.matmul(
+                                acc[:, P:T], lhsT=x_half[hf][:, 2 * s + 1, chans], rhs=minus_before[:, 1, P:T],
+                                start=False, stop=False,
+                            )
+                            nc.tensor.matmul(
+                                acc[:, 0:2], lhsT=small_mix[:, chans], rhs=minus_prev0[:, hf * SEQ_HALF + s, 0:2],
+                                start=False, stop=True,
+                            )
+                        banks.append(diff_ps)
+                    return banks
+
+                def log_of_bt(j):
+                    for b in range(B):
+                        nc.scalar.activation(
+                            out=ln_bt[:, j, b, :], in_=decay[:, j, :], func=ACT.Ln,
+                            scale=by_decay[:, j, ROW_B0 + b : ROW_B0 + b + 1], bias=eps_col[:],
+                        )
+
+                def by_channel_tile(dst, small):
+                    small_ps = psum_mix.tile([P, CH_TILES, P], BF16, name="small_ps", tag="xt")
+                    for j in range(CH_TILES):
+                        nc.tensor.transpose(small_ps[:, j, :], small[:, j * P : (j + 1) * P], ident_bf[:])
+                    nc.vector.tensor_copy(out=dst[:], in_=small_ps[:, :, 0:ROWS])
+
+                def per_channel_constants():
+                    by_channel_tile(by_decay, small_decay)
+                    nc.vector.tensor_scalar_mul(out=neg_w[:], in0=by_decay[:, :, ROW_W : ROW_W + 1], scalar1=-1.0)
+                    for j in range(CH_TILES):
+                        nc.scalar.activation(out=decay[:, j, :], in_=steps[:], func=ACT.Exp, scale=neg_w[:, j, :])
+                    nc.scalar.activation(
+                        out=ln_b0_eps[:], in_=by_decay[:, :, ROW_B0 : ROW_B0 + B], func=ACT.Ln, scale=1.0 / EPS
+                    )
+                    by_channel_tile(by_state, small_state)
+                    nc.vector.tensor_scalar_mul(out=neg_u[:], in0=by_state[:, :, ROW_U : ROW_U + 1], scalar1=-1.0)
+                    nc.vector.reciprocal(out=inv_b0[:], in_=by_decay[:, :, ROW_B0 : ROW_B0 + B])
+                    nc.vector.scalar_tensor_tensor(
+                        out=neg_ratio[:], in0=by_state[:, :, ROW_A0 : ROW_A0 + B], scalar=-1.0, in1=inv_b0[:],
+                        op0=ALU.mult, op1=ALU.mult,
+                    )
+
+                steps_of_mix = [(hf, g) for hf in range(HALVES) for g in range(GROUPS)]
+                prepare_planes(*steps_of_mix[0])
+                diff_banks = prepare_differences(*steps_of_mix[0])
+
+                mixed_before = None
+                for step, (hf, g) in enumerate(steps_of_mix):
                     seqs = slice(hf * SEQ_HALF, (hf + 1) * SEQ_HALF)
                     if step + 1 < len(steps_of_mix):
                         prepare_planes(*steps_of_mix[step + 1])
                     fresh = []
                     for m in (MIX_R, MIX_K, MIX_V):
-                        mixed = mix.tile([P, PACK, HALF], BF16, name="mixed%d" % m)
+                        mixed = carry.tile([P, PACK, HALF], BF16, name="mixed%d" % m, tag="slab%d" % m)
                         for t in range(PACK):
                             nc.vector.scalar_tensor_tensor(
                                 out=mixed[:, t, :].rearrange("p (s t) -> p s t", s=SEQ_HALF),
                                 in0=diff_banks[t][:], scalar=mu_plane[:, g * PACK + t, m : m + 1],
-                                in1=x_planes[:, g * PACK + t, seqs, LEAD - 1 : PITCH - 1],
+                                in1=before_of(g * PACK + t, seqs),
                                 op0=ALU.mult, op1=ALU.add,
                             )
                         fresh.append(mixed)
-                if mixed_before is not None:
-                    regrouped = []
-                    for m in (MIX_R, MIX_K, MIX_V):
-                        grouped = mix.tile([P, HALF, PACK], BF16, name="grouped%d" % m, bufs=1, align_bytes=64)
-                        dst = grouped[:].rearrange("p (c i) t -> p c t i", i=4)
-                        src = mixed_before[0][m][:].rearrange("p t (c i) -> p c t i", i=4)
-                        if m == MIX_V:
-                            nc.scalar.copy(out=dst, in_=src)
-                        elif mixing:
-                            nc.gpsimd.tensor_scalar(
-                                out=dst, in0=src, scalar1=1.0, scalar2=0.0, op0=ALU.mult, op1=ALU.add
-                            )
-                        else:
-                            nc.vector.tensor_copy(out=dst, in_=src)
-                        regrouped.append(grouped)
-                    for m in (MIX_V, MIX_K, MIX_R):
-                        quantise_x(regrouped[m], m, mixed_before[1], mixed_before[2])
-                mixed_before = (fresh, g, hf) if mixing else None
-                if step + 1 < len(steps_of_mix):
-                    diff_banks = prepare_differences(*steps_of_mix[step + 1])
-                for j in range(3 * step, min(3 * step + 3, CH_TILES)):
-                    log_of_bt(j)
-                if step >= len(steps_of_mix) - 1:
-                    for piece in range(TOK_TILES):
-                        gate_piece(0, (step - len(steps_of_mix) + 1) * TOK_TILES + piece, psum_mix)
-
-            by_channel_tile(by_state, small_state)
-            nc.vector.tensor_scalar_mul(out=neg_u[:], in0=by_state[:, :, ROW_U : ROW_U + 1], scalar1=-1.0)
-            nc.vector.reciprocal(out=inv_b0[:], in_=by_decay[:, :, ROW_B0 : ROW_B0 + B])
-            nc.vector.scalar_tensor_tensor(
-                out=neg_ratio[:], in0=by_state[:, :, ROW_A0 : ROW_A0 + B], scalar=-1.0, in1=inv_b0[:],
-                op0=ALU.mult, op1=ALU.mult,
-            )
+                        if step == 0 and m == MIX_R:
+                            per_channel_constants()
+                    if mixed_before is not None:
+                        regrouped = [new_grouped(m) for m in (MIX_R, MIX_K, MIX_V)]
+                        for m in (MIX_R, MIX_K, MIX_V):
+                            regroup(m, regrouped[m], mixed_before[0][m], slice(0, HALF))
+                        for m in (MIX_V, MIX_K, MIX_R):
+                            quantise_x(regrouped[m], m, mixed_before[1], mixed_before[2])
+                    mixed_before = (fresh, g, hf)
+                    if step + 1 < len(steps_of_mix):
+                        diff_banks = prepare_differences(*steps_of_mix[step + 1])
+                    for j in range(3 * step, min(3 * step + 3, CH_TILES)):
+                        log_of_bt(j)
+                for piece in range(2 * TOK_TILES):
+                    gate_piece(0, piece, psum_mix)
 
         epi = ctx.enter_context(tc.tile_pool(name="epi", bufs=2, reuse_waits="tile"))
         with tc.psum_pool(name="psum", bufs=2, reuse_waits="tile") as psum:
@@ -309,14 +316,16 @@ def tile_rwkv_timemix_pa_kernel(
             units = [(hf, j) for hf in range(HALVES) for j in range(CH_TILES)]
             tiles = {}
 
-            def start_unit(n):
+            def start_v(n):
                 hf, j = units[n]
                 ch = slice(j * P, (j + 1) * P)
                 tokens = slice(hf * HALF, (hf + 1) * HALF)
-                k_ps = psum.tile([P, HALF], F32, name="k_ps", tag="k", bufs=1)
-                mx_product(k_ps[:], w_code[MIX_K], w_scale[:, MIX_K], ch, x_code[MIX_K], x_scale[MIX_K], tokens)
                 v_ps = psum.tile([P, HALF], F32, name="v_ps", tag="v", bufs=3)
                 mx_product(v_ps[:], w_code[MIX_V], w_scale[:, MIX_V], ch, x_code[MIX_V], x_scale[MIX_V], tokens)
+                tiles[n] = (v_ps, tiles[n])
+
+            def start_rho(n):
+                hf, j = units[n]
                 rho = epi.tile([P, SEQ_HALF, T], F32, name="rho")
                 for s in range(SEQ_HALF):
                     b = hf * SEQ_HALF + s
@@ -324,7 +333,15 @@ def tile_rwkv_timemix_pa_kernel(
                         out=rho[:, s, :], in_=steps[:], func=ACT.Sigmoid,
                         scale=neg_w[:, j, :], bias=ln_b0_eps[:, j, b : b + 1],
                     )
-                tiles[n] = (k_ps, v_ps, rho)
+                tiles[n] = rho
+
+            def start_k(n):
+                hf, j = units[n]
+                ch = slice(j * P, (j + 1) * P)
+                tokens = slice(hf * HALF, (hf + 1) * HALF)
+                k_ps = psum.tile([P, HALF], F32, name="k_ps", tag="k", bufs=1)
+                mx_product(k_ps[:], w_code[MIX_K], w_scale[:, MIX_K], ch, x_code[MIX_K], x_scale[MIX_K], tokens)
+                tiles[n] = (k_ps, tiles[n][0], tiles[n][1])
 
             def weigh_unit(n):
                 hf, j = units[n]
@@ -367,33 +384,43 @@ def tile_rwkv_timemix_pa_kernel(
                 else:
                     nc.scalar.copy(out=dst, in_=src)
 
-            def regroup_h(hf, q, on_vector, banks):
-                h_ps = banks.tile([P, GROUPS * 2, P], F32, name="h_ps", tag="misc")
+            def regroup_h(hf, q, groups, on_vector, banks):
+                h_ps = banks.tile([P, len(groups) * 2, P], F32, name="h_ps", tag="misc")
                 words = h_half[hf][:, q, :].bitcast(F32)
-                for g in range(GROUPS):
+                for i, g in enumerate(groups):
                     for k in range(2):
                         nc.tensor.transpose(
-                            h_ps[:, g * 2 + k, :], words[:, g * 256 + k : (g + 1) * 256 : 2], ident_f32[:]
+                            h_ps[:, i * 2 + k, :], words[:, g * 256 + k : (g + 1) * 256 : 2], ident_f32[:]
                         )
-                h_grouped = epi.tile([P, GROUPS, P, PACK], BF16, name="h_grouped", bufs=TOK_TILES, align_bytes=64)
+                if (hf, q) not in tiles:
+                    h_grouped = epi.tile([P, GROUPS, P, PACK], BF16, name="h_grouped", bufs=H_BUFS, align_bytes=64)
+                    h_code = epi.tile([P, GROUPS, P], U32, name="h_code", bufs=H_BUFS, align_bytes=64)
+                    h_scale = epi.tile([P, GROUPS, P], U8, name="h_scale", bufs=H_BUFS, align_bytes=64)
+                    tiles[(hf, q)] = (h_grouped, h_code, h_scale)
+                span = slice(groups[0], groups[0] + len(groups))
                 copy_out(
                     on_vector,
-                    h_grouped[:].rearrange("p g n t -> p (g n t)").bitcast(F32).rearrange(
-                        "p (g n k) -> p g n k", g=GROUPS, k=2
+                    tiles[(hf, q)][0][:, span].rearrange("p g n t -> p (g n t)").bitcast(F32).rearrange(
+                        "p (g n k) -> p g n k", g=len(groups), k=2
                     ),
                     h_ps[:].rearrange("p (g k) n -> p g n k", k=2),
                 )
-                tiles[(hf, q)] = h_grouped
+
+            def quantise_h(hf, q, groups):
+                h_grouped, h_code, h_scale = tiles[(hf, q)]
+                span = slice(groups[0], groups[0] + len(groups))
+                nc.vector.quantize_mx(
+                    out=h_code[:, span].rearrange("p g n -> p (g n)").bitcast(FP8X4),
+                    scales=h_scale[:, span].rearrange("p g n -> p (g n)"),
+                    in_=h_grouped[:, span].rearrange("p g n t -> p (g n t)"),
+                )
+
+            def new_result(hf, q):
+                return carry.tile([P, C], F32, name="result", tag="slab%d" % ((hf * TOK_TILES + q) % 3))
 
             def project(hf, q, on_vector, banks):
-                h_code = epi.tile([P, GROUPS, P], U32, name="h_code", align_bytes=64)
-                h_scale = epi.tile([P, GROUPS, P], U8, name="h_scale", align_bytes=64)
-                nc.vector.quantize_mx(
-                    out=h_code[:].rearrange("p g n -> p (g n)").bitcast(FP8X4),
-                    scales=h_scale[:].rearrange("p g n -> p (g n)"),
-                    in_=tiles[(hf, q)][:].rearrange("p g n t -> p (g n t)"),
-                )
-                result = epi.tile([P, C], F32, name="result", bufs=TOK_TILES)
+                h_code, h_scale = tiles[(hf, q)][1], tiles[(hf, q)][2]
+                result = new_result(hf, q)
                 first = hf * HALF + q * P
                 for nh in range(C // 512):
                     n_cols = slice(nh * 512, (nh + 1) * 512)
@@ -402,27 +429,92 @@ def tile_rwkv_timemix_pa_kernel(
                     copy_out(on_vector, result[:, n_cols], out_ps[:])
                     nc.sync.dma_start(out=out_rows[first : first + P, n_cols], in_=result[:, n_cols])
 
-            start_unit(0)
+            last_mixed, last_g, last_hf = mixed_before
+            last_grouped = [new_grouped(m) for m in (MIX_R, MIX_K, MIX_V)]
+            quarters = [slice(i * P, (i + 1) * P) for i in range(TOK_TILES)]
+            early_from = len(units) - 2
+            start_rho(0)
+            start_v(0)
+            start_k(0)
             for n in range(len(units) + 2):
+                if n + 1 < len(units):
+                    start_rho(n + 1)
                 if n < len(units):
                     weigh_unit(n)
                 if n + 1 < len(units):
-                    start_unit(n + 1)
+                    start_v(n + 1)
+                if n == 2:
+                    quantise_x(last_grouped[MIX_V], MIX_V, last_g, last_hf)
+                    quantise_x(last_grouped[MIX_R], MIX_R, last_g, last_hf)
+                if n == 4:
+                    quantise_x(last_grouped[MIX_K], MIX_K, last_g, last_hf)
+                if 3 <= n < 3 + 2 * TOK_TILES:
+                    gate_piece(1, n - 3, psum)
+                before = units[n - 2] if n >= 2 else (0, 0)
+                if before[0] >= 1 and before[1] % 2 == 1:
+                    quantise_h(before[0] - 1, before[1] // 2, BOTH)
+                    project(before[0] - 1, before[1] // 2, False, psum)
+                if early_from < n <= early_from + TOK_TILES and n < len(units) + 2:
+                    quantise_h(HALVES - 1, n - early_from - 1, LOWER)
+                if n + 1 < len(units):
+                    start_k(n + 1)
+                if before[0] >= 1 and before[1] % 2 == 0:
+                    regroup_h(before[0] - 1, before[1] // 2, BOTH, False, psum)
+                if early_from <= n < early_from + TOK_TILES:
+                    regroup_h(HALVES - 1, n - early_from, LOWER, False, psum)
                 if 1 <= n <= len(units):
                     blend_unit(n - 1)
                 if n >= 2:
                     gate_unit(n - 2)
-                if n >= 2:
-                    hf, j = units[n - 2]
-                    if hf + 1 < HALVES:
-                        gate_piece(hf + 1, j, psum)
-                    if hf >= 1 and j % 2 == 0:
-                        regroup_h(hf - 1, j // 2, False, psum)
-                    if hf >= 1 and j % 2 == 1:
-                        project(hf - 1, j // 2, False, psum)
+                if n == 0:
+                    regroup(MIX_V, last_grouped[MIX_V], last_mixed[MIX_V], slice(0, HALF))
+                if n < 4:
+                    m = (MIX_R, MIX_K)[n // 2]
+                    for tok in quarters[2 * (n % 2) : 2 * (n % 2) + 2]:
+                        regroup(m, last_grouped[m], last_mixed[m], tok)
 
         with tc.psum_pool(name="psum_end", bufs=8, reuse_waits="tile") as psum_end:
+            last = HALVES - 1
+            banks = {}
+
+            def pass_over(g, q):
+                for nh in range(C // 512):
+                    if g == 0:
+                        out_ps = psum_end.tile([P, 512], F32, name="out_ps", tag="misc")
+                        banks[(q, nh)] = out_ps
+                    n_cols = slice(nh * 512, (nh + 1) * 512)
+                    nc.tensor.matmul_mx(
+                        out=banks[(q, nh)][:],
+                        lhsT=tiles[(last, q)][1][:, g, :].bitcast(FP8X4),
+                        lhsT_scale=tiles[(last, q)][2][:, g, :],
+                        rhs=w_code[W_OUT][:, g, n_cols].bitcast(FP8X4),
+                        rhs_scale=w_scale[:, W_OUT, g, n_cols],
+                        start=(g == 0),
+                        stop=(g == GROUPS - 1),
+                    )
+
+            def store(q):
+                result = new_result(last, q)
+                first = last * HALF + q * P
+                for nh in range(C // 512):
+                    n_cols = slice(nh * 512, (nh + 1) * 512)
+                    copy_out(nh == 1, result[:, n_cols], banks[(q, nh)][:])
+                    nc.sync.dma_start(out=out_rows[first : first + P, n_cols], in_=result[:, n_cols])
+
+            pass_over(0, 0)
+            pass_over(0, 1)
+            quantise_h(last, TOK_TILES - 1, LOWER)
             for q in range(TOK_TILES):
-                regroup_h(HALVES - 1, q, q % 2 == 1, psum_end)
+                regroup_h(last, q, UPPER, q % 2 == 1, psum_end)
             for q in range(TOK_TILES):
-                project(HALVES - 1, q, q % 2 == 1, psum_end)
+                quantise_h(last, q, UPPER)
+            pass_over(1, 0)
+            store(0)
+            pass_over(1, 1)
+            store(1)
+            pass_over(0, 2)
+            pass_over(0, 3)
+            pass_over(1, 2)
+            store(2)
+            pass_over(1, 3)
+            store(3)

@@ -352,6 +352,11 @@ def tile_rwkv_timemix_pa_kernel(
                     in1=ln_bt[:, j, hf * SEQ_HALF : (hf + 1) * SEQ_HALF, :].rearrange("p s t -> p (s t)"),
                 )
                 nc.scalar.activation(out=sb[:], in_=sb[:], func=ACT.Sigmoid, scale=-1.0, bias=neg_u[:, j, :])
+                tiles[n] = (v_ps, sb, rho)
+
+            def part_unit(n):
+                hf, j = units[n]
+                v_ps, sb, rho = tiles[n]
                 wkv = epi.tile([P, HALF], F32, name="wkv", bufs=3)
                 for s in range(SEQ_HALF):
                     b = hf * SEQ_HALF + s
@@ -441,21 +446,24 @@ def tile_rwkv_timemix_pa_kernel(
                     start_rho(n + 1)
                 if n < len(units):
                     weigh_unit(n)
-                if n + 1 < len(units):
-                    start_v(n + 1)
+                before = units[n - 2] if n >= 2 else (0, 0)
                 if n == 2:
                     quantise_x(last_grouped[MIX_V], MIX_V, last_g, last_hf)
                     quantise_x(last_grouped[MIX_R], MIX_R, last_g, last_hf)
                 if n == 4:
                     quantise_x(last_grouped[MIX_K], MIX_K, last_g, last_hf)
-                if 3 <= n < 3 + 2 * TOK_TILES:
-                    gate_piece(1, n - 3, psum)
-                before = units[n - 2] if n >= 2 else (0, 0)
                 if before[0] >= 1 and before[1] % 2 == 1:
                     quantise_h(before[0] - 1, before[1] // 2, BOTH)
-                    project(before[0] - 1, before[1] // 2, False, psum)
                 if early_from < n <= early_from + TOK_TILES and n < len(units) + 2:
                     quantise_h(HALVES - 1, n - early_from - 1, LOWER)
+                if n < len(units):
+                    part_unit(n)
+                if n + 1 < len(units):
+                    start_v(n + 1)
+                if 3 <= n < 3 + 2 * TOK_TILES:
+                    gate_piece(1, n - 3, psum)
+                if before[0] >= 1 and before[1] % 2 == 1:
+                    project(before[0] - 1, before[1] // 2, False, psum)
                 if n + 1 < len(units):
                     start_k(n + 1)
                 if before[0] >= 1 and before[1] % 2 == 0:

@@ -31,8 +31,10 @@ ROW_W, ROW_B0 = 0, 1
 ROW_U, ROW_A0 = 0, 1
 ROWS = 1 + B
 MIX_R, MIX_K, MIX_V, W_OUT = 0, 1, 2, 3
-BOTH, LOWER, UPPER = (0, 1), (0,), (1,)
-H_BUFS = 5
+PLANE_ROW = (0, 4, 8)
+GROUPED_BUFS = (1, 1, 2)
+VECTOR_TILES = (1, 3)
+TENSOR_GROUP = 1
 
 FLOPS = 4 * 2 * B * T * C * C
 
@@ -50,7 +52,6 @@ def tile_rwkv_timemix_pa_kernel(
 
     with ExitStack() as ctx:
         keep = ctx.enter_context(tc.tile_pool(name="keep", bufs=1))
-        rows = ctx.enter_context(tc.tile_pool(name="rows", bufs=HALVES))
         carry = ctx.enter_context(tc.tile_pool(name="carry", bufs=2))
         ctx.enter_context(tc.manual_schedule())
 
@@ -63,22 +64,27 @@ def tile_rwkv_timemix_pa_kernel(
             nc.vector.memset(small_state[:].bitcast(I32), 0)
             x_half = []
             for hf in range(HALVES):
-                x_half.append(rows.tile([P, TOK_TILES, C], BF16, name="x_half%d" % hf, tag="rows"))
+                x_half.append(early.tile([P, TOK_TILES, C], BF16, name="x_half%d" % hf))
 
-            def load_x(hf):
+            def load_x(hf, chans):
                 for q in range(TOK_TILES):
                     first = hf * HALF + q * P
-                    nc.sync.dma_start(out=x_half[hf][:, q, :], in_=x_rows[first : first + P, :])
+                    nc.sync.dma_start(out=x_half[hf][:, q, chans], in_=x_rows[first : first + P, chans])
 
-            load_x(0)
-            nc.scalar.dma_start(out=small_mix[ROW_XPREV : ROW_XPREV + B, :], in_=x_prev0)
+            eps_col = keep.tile([P, 1], F32, name="eps_col")
+            nc.vector.memset(eps_col[:], EPS)
+            table_first = early.tile([P, 1], F32, name="table_first")
+            nc.scalar.activation(out=table_first[:], in_=eps_col[:], func=ACT.Exp)
+            load_x(0, slice(0, C // 2))
             for m, mu in enumerate((mu_r, mu_k, mu_v)):
-                nc.scalar.dma_start(out=small_mix[ROW_MU + m : ROW_MU + m + 1, :], in_=mu.unsqueeze(0))
-            nc.scalar.dma_start(out=small_decay[ROW_W : ROW_W + 1, :], in_=w.unsqueeze(0))
-            nc.scalar.dma_start(out=small_decay[ROW_B0 : ROW_B0 + B, :], in_=b0)
-            nc.scalar.dma_start(out=small_state[ROW_U : ROW_U + 1, :], in_=u.unsqueeze(0))
-            nc.scalar.dma_start(out=small_state[ROW_A0 : ROW_A0 + B, :], in_=a0)
-            load_x(1)
+                nc.sync.dma_start(out=small_mix[ROW_MU + m : ROW_MU + m + 1, :], in_=mu.unsqueeze(0))
+            nc.sync.dma_start(out=small_mix[ROW_XPREV : ROW_XPREV + B, :], in_=x_prev0)
+            nc.sync.dma_start(out=small_decay[ROW_W : ROW_W + 1, :], in_=w.unsqueeze(0))
+            nc.sync.dma_start(out=small_decay[ROW_B0 : ROW_B0 + B, :], in_=b0)
+            load_x(0, slice(C // 2, C))
+            nc.sync.dma_start(out=small_state[ROW_U : ROW_U + 1, :], in_=u.unsqueeze(0))
+            nc.sync.dma_start(out=small_state[ROW_A0 : ROW_A0 + B, :], in_=a0)
+            load_x(1, slice(0, C))
 
             ident_bf = early.tile([P, P], BF16, name="ident_bf")
             make_identity(nc, ident_bf[:])
@@ -87,23 +93,52 @@ def tile_rwkv_timemix_pa_kernel(
             steps_int = early.tile([P, T], I32, name="steps_int")
             nc.gpsimd.iota(steps_int[:], pattern=[[1, T]], base=1, channel_multiplier=0)
 
-            w_scale = keep.tile([P, 4, GROUPS, C], U8, name="w_scale", align_bytes=64)
-            nc.vector.memset(w_scale[:].rearrange("p a g n -> p (a g n)").bitcast(I32), 0)
-            for wi in (MIX_R, MIX_K, MIX_V, W_OUT):
-                by_row = weight_scales[wi].rearrange("g (q r) n -> r q g n", r=4)
+            scale_raw = early.tile([P, GROUPS, C], U8, name="scale_raw", align_bytes=64)
+            nc.vector.memset(scale_raw[:].rearrange("p g n -> p (g n)").bitcast(I32), 0)
+            out_scale = keep.tile([P, GROUPS, C], U8, name="out_scale", align_bytes=64)
+            nc.vector.memset(out_scale[:].rearrange("p g n -> p (g n)").bitcast(I32), 0)
+
+            def load_scales(tile, first, scales):
+                by_row = scales.rearrange("g (q r) n -> r q g n", r=4)
                 for r in range(4):
                     nc.sync.dma_start(
-                        out=w_scale[r:P:32, wi, :, :].bitcast(I32), in_=by_row[r].bitcast(I32)
+                        out=tile[first + r : P : 32, :, :].bitcast(I32), in_=by_row[r].bitcast(I32)
                     )
-            w_code = []
-            for wi in range(4):
-                w_code.append(keep.tile([P, GROUPS, C], U32, name="w_code%d" % wi, align_bytes=64))
-            for wi in (MIX_R, MIX_K, MIX_V, W_OUT):
+
+            def load_words(tile, words):
                 for g in range(GROUPS):
                     nc.sync.dma_start(
-                        out=w_code[wi][:, g, :].bitcast(I32),
-                        in_=weight_words[wi][g].rearrange("p n t -> p (n t)").bitcast(I32),
+                        out=tile[:, g, :], in_=words[g].rearrange("p n t -> p (n t)").bitcast(I32)
                     )
+
+            def load_raw(wi):
+                tile = early.tile([P, GROUPS, C], I32, name="raw%d" % wi, tag="raw", bufs=2, align_bytes=64)
+                load_words(tile, weight_words[wi])
+                return tile
+
+            w_scale = keep.tile([P, GROUPS, C], U8, name="w_scale", align_bytes=64)
+            w_code = []
+            for wi in range(4):
+                w_code.append(keep.tile([P, GROUPS, C], I32, name="w_code%d" % wi, align_bytes=64))
+            for wi in (MIX_R, MIX_K, MIX_V):
+                load_scales(scale_raw, PLANE_ROW[wi], weight_scales[wi])
+            load_scales(out_scale, 0, weight_scales[W_OUT])
+            raw = {MIX_R: load_raw(MIX_R), MIX_V: load_raw(MIX_V)}
+            load_words(w_code[W_OUT], weight_words[W_OUT])
+
+            def sorted_columns(tile):
+                return tile[:].rearrange("p g (b t m) -> p (g b) t m", b=GROUPS, t=PACK)
+
+            def raw_columns(tile):
+                return tile[:].rearrange("p g (b m t) -> p (g b) t m", b=GROUPS, t=PACK)
+
+            def sort_codes(wi):
+                nc.vector.tensor_copy(out=sorted_columns(w_code[wi]), in_=raw_columns(raw[wi]))
+
+            def sort_scales(piece):
+                nc.gpsimd.tensor_copy(
+                    out=sorted_columns(w_scale)[:, piece], in_=raw_columns(scale_raw)[:, piece]
+                )
 
             minus_before = early.tile([P, 2, T], BF16, name="minus_before")
             nc.vector.memset(minus_before[:].rearrange("p a n -> p (a n)").bitcast(I32), 0)
@@ -121,13 +156,12 @@ def tile_rwkv_timemix_pa_kernel(
                 )
             steps = keep.tile([P, T], F32, name="steps")
             nc.vector.tensor_copy(out=steps[:], in_=steps_int[:])
-            eps_col = keep.tile([P, 1], F32, name="eps_col")
-            nc.vector.memset(eps_col[:], EPS)
 
             x_code, x_scale = [], []
             for m in range(3):
                 x_code.append(keep.tile([P, GROUPS, B * T], U32, name="x_code%d" % m, align_bytes=64))
                 x_scale.append(keep.tile([P, GROUPS, B * T], U8, name="x_scale%d" % m, align_bytes=64))
+            diag = early.tile([P, PACK, 2, P], BF16, name="diag")
             by_decay = early.tile([P, CH_TILES, ROWS], F32, name="by_decay")
             by_state = keep.tile([P, CH_TILES, ROWS], F32, name="by_state")
             mu_plane = keep.tile([P, PLANES, 3], F32, name="mu_plane")
@@ -135,20 +169,19 @@ def tile_rwkv_timemix_pa_kernel(
             neg_u = keep.tile([P, CH_TILES, 1], F32, name="neg_u")
             inv_b0 = keep.tile([P, CH_TILES, B], F32, name="inv_b0")
             neg_ratio = keep.tile([P, CH_TILES, B], F32, name="neg_ratio")
-            decay = keep.tile([P, CH_TILES, T], F32, name="decay")
+            decay = early.tile([P, CH_TILES, T], F32, name="decay")
             ln_b0_eps = keep.tile([P, CH_TILES, B], F32, name="ln_b0_eps")
             ln_bt = keep.tile([P, CH_TILES, B, T], F32, name="ln_bt")
-            gate = []
-            for hf in range(HALVES):
-                gate.append(keep.tile([P, TOK_TILES, C], F32, name="gate%d" % hf))
 
             def new_grouped(m):
-                return carry.tile([P, HALF, PACK], BF16, name="grouped%d" % m, bufs=1, align_bytes=64)
+                return carry.tile([P, HALF, PACK], BF16, name="grouped%d" % m, bufs=GROUPED_BUFS[m], align_bytes=64)
 
-            def regroup(m, grouped, mixed, tok):
+            def regroup(m, grouped, mixed, tok, on_vector=False):
                 dst = grouped[:, tok, :].rearrange("p (c i) t -> p c t i", i=4)
                 src = mixed[:, :, tok].rearrange("p t (c i) -> p c t i", i=4)
-                if m == MIX_V:
+                if on_vector:
+                    nc.vector.tensor_copy(out=dst, in_=src)
+                elif m == MIX_V:
                     nc.scalar.copy(out=dst, in_=src)
                 else:
                     nc.gpsimd.tensor_scalar(
@@ -163,83 +196,98 @@ def tile_rwkv_timemix_pa_kernel(
                     in_=grouped[:].rearrange("p n t -> p (n t)"),
                 )
 
-            def mx_product(acc, lhs_code, lhs_scale, lhs_cols, rhs_code, rhs_scale, rhs_cols):
+            def channel_product(acc, wi, hf, j, tok_of_half):
+                ch = slice(j * P, (j + 1) * P)
+                tok = slice(hf * HALF + tok_of_half.start, hf * HALF + tok_of_half.stop)
                 for g in range(GROUPS):
                     nc.tensor.matmul_mx(
                         out=acc,
-                        lhsT=lhs_code[:, g, lhs_cols].bitcast(FP8X4),
-                        lhsT_scale=lhs_scale[:, g, lhs_cols],
-                        rhs=rhs_code[:, g, rhs_cols].bitcast(FP8X4),
-                        rhs_scale=rhs_scale[:, g, rhs_cols],
+                        lhsT=w_code[wi][:, g, ch].bitcast(FP8X4),
+                        lhsT_scale=w_scale[PLANE_ROW[wi] : P, g, ch],
+                        rhs=x_code[wi][:, g, tok].bitcast(FP8X4),
+                        rhs_scale=x_scale[wi][:, g, tok],
                         start=(g == 0),
                         stop=(g == GROUPS - 1),
                     )
 
-            def gate_piece(hf, piece, banks):
-                nh, q = divmod(piece, TOK_TILES)
-                first = hf * HALF + q * P
-                n_cols = slice(nh * 512, (nh + 1) * 512)
-                r_ps = banks.tile([P, 512], F32, name="r_ps", tag="misc")
-                mx_product(
-                    r_ps[:], x_code[MIX_R], x_scale[MIX_R], slice(first, first + P),
-                    w_code[MIX_R], w_scale[:, MIX_R], n_cols,
-                )
-                nc.scalar.activation(out=gate[hf][:, q, n_cols], in_=r_ps[:], func=ACT.Sigmoid)
-
             with tc.psum_pool(name="psum_mix", bufs=2) as psum_mix:
-                by_plane_ps = psum_mix.tile([P, PLANES, P], BF16, name="by_plane_ps", tag="xt")
-                for pl in range(PLANES):
-                    g, t = divmod(pl, PACK)
-                    nc.tensor.transpose(
-                        by_plane_ps[:, pl, :], small_mix[:, g * 512 + t : (g + 1) * 512 : PACK], ident_bf[:]
-                    )
-                nc.vector.tensor_copy(out=mu_plane[:], in_=by_plane_ps[:, :, ROW_MU : ROW_MU + 3])
                 x_pairs = early.tile([P, PLANES // 2, B, PITCH, 2], BF16, name="x_pairs")
-                nc.vector.tensor_copy(
-                    out=x_pairs[:, :, :, LEAD - 1, :],
-                    in_=by_plane_ps[:, :, ROW_XPREV : ROW_XPREV + B].rearrange("p (r e) b -> p r b e", e=2),
-                )
+
+                def small_planes(g):
+                    by_plane_ps = psum_mix.tile([P, PACK, P], BF16, name="by_plane_ps", tag="xt")
+                    for t in range(PACK):
+                        nc.tensor.transpose(
+                            by_plane_ps[:, t, :], small_mix[:, g * 512 + t : (g + 1) * 512 : PACK], ident_bf[:]
+                        )
+                    nc.vector.tensor_copy(
+                        out=mu_plane[:, g * PACK : (g + 1) * PACK, :], in_=by_plane_ps[:, :, ROW_MU : ROW_MU + 3]
+                    )
+                    nc.vector.tensor_copy(
+                        out=x_pairs[:, g * 2 : (g + 1) * 2, :, LEAD - 1, :],
+                        in_=by_plane_ps[:, :, ROW_XPREV : ROW_XPREV + B].rearrange("p (r e) b -> p r b e", e=2),
+                    )
+
+                def make_diagonals():
+                    for t in range(PACK):
+                        for i, sign in enumerate((1.0, -1.0)):
+                            nc.gpsimd.tensor_scalar(
+                                out=diag[:, t, i, :], in0=ident_bf[:], op0=ALU.mult, op1=ALU.mult,
+                                scalar1=mu_plane[:, TENSOR_GROUP * PACK + t, MIX_V : MIX_V + 1], scalar2=sign,
+                            )
+
+                def mix_by_tensor(hf, grouped):
+                    for q in range(TOK_TILES):
+                        b, a = hf * SEQ_HALF + q // 2, q % 2
+                        mix_ps = psum_mix.tile([P, PACK, P], F32, name="mix_ps", tag="misc")
+                        for t in range(PACK):
+                            plane = TENSOR_GROUP * PACK + t
+                            pair = x_pairs[:, plane // 2, b, :, plane % 2]
+                            now = pair[:, LEAD + a * P : LEAD + (a + 1) * P]
+                            before = pair[:, LEAD - 1 + a * P : LEAD - 1 + (a + 1) * P]
+                            acc = mix_ps[:, t, :]
+                            nc.tensor.matmul(acc, lhsT=diag[:, t, 0, :], rhs=now, start=True, stop=False)
+                            nc.tensor.matmul(acc, lhsT=diag[:, t, 1, :], rhs=before, start=False, stop=False)
+                            nc.tensor.matmul(acc, lhsT=ident_bf[:], rhs=before, start=False, stop=True)
+                        nc.scalar.copy(
+                            out=grouped[:, q * P : (q + 1) * P, :], in_=mix_ps[:].rearrange("p t n -> p n t")
+                        )
 
                 def before_of(plane, seqs):
                     return x_pairs[:, plane // 2, seqs, LEAD - 1 : PITCH - 1, plane % 2]
 
-                def prepare_planes(hf, g):
-                    for k in range(PACK // 2):
-                        xt_ps = psum_mix.tile([P, HALF], F32, name="xt_ps", tag="xt")
-                        for q in range(TOK_TILES):
-                            nc.tensor.transpose(
-                                xt_ps[:, q * P : (q + 1) * P],
-                                x_half[hf][:, q, :].bitcast(F32)[:, g * 256 + k : (g + 1) * 256 : 2],
-                                ident_f32[:],
-                            )
-                        nc.scalar.copy(
-                            out=x_pairs[:, g * 2 + k, hf * SEQ_HALF : (hf + 1) * SEQ_HALF, LEAD:PITCH, :]
-                            .rearrange("p s t e -> p s (t e)")
-                            .bitcast(F32),
-                            in_=xt_ps[:].rearrange("p (s t) -> p s t", s=SEQ_HALF),
+                def prepare_pair(hf, g, k):
+                    xt_ps = psum_mix.tile([P, HALF], F32, name="xt_ps", tag="xt")
+                    for q in range(TOK_TILES):
+                        nc.tensor.transpose(
+                            xt_ps[:, q * P : (q + 1) * P],
+                            x_half[hf][:, q, :].bitcast(F32)[:, g * 256 + k : (g + 1) * 256 : 2],
+                            ident_f32[:],
                         )
+                    nc.scalar.copy(
+                        out=x_pairs[:, g * 2 + k, hf * SEQ_HALF : (hf + 1) * SEQ_HALF, LEAD:PITCH, :]
+                        .rearrange("p s t e -> p s (t e)")
+                        .bitcast(F32),
+                        in_=xt_ps[:].rearrange("p (s t) -> p s t", s=SEQ_HALF),
+                    )
 
-                def prepare_differences(hf, g):
-                    banks = []
-                    for t in range(PACK):
-                        chans = slice(g * 512 + t, (g + 1) * 512, PACK)
-                        diff_ps = psum_mix.tile([P, SEQ_HALF, T], F32, name="diff_ps", tag="diff", bufs=4)
-                        for s in range(SEQ_HALF):
-                            acc = diff_ps[:, s, :]
-                            nc.tensor.matmul(
-                                acc, lhsT=x_half[hf][:, 2 * s, chans], rhs=minus_before[:, 0, :],
-                                start=True, stop=False,
-                            )
-                            nc.tensor.matmul(
-                                acc[:, P:T], lhsT=x_half[hf][:, 2 * s + 1, chans], rhs=minus_before[:, 1, P:T],
-                                start=False, stop=False,
-                            )
-                            nc.tensor.matmul(
-                                acc[:, 0:2], lhsT=small_mix[:, chans], rhs=minus_prev0[:, hf * SEQ_HALF + s, 0:2],
-                                start=False, stop=True,
-                            )
-                        banks.append(diff_ps)
-                    return banks
+                def prepare_difference(hf, g, t):
+                    chans = slice(g * 512 + t, (g + 1) * 512, PACK)
+                    diff_ps = psum_mix.tile([P, SEQ_HALF, T], F32, name="diff_ps", tag="diff", bufs=4)
+                    for s in range(SEQ_HALF):
+                        acc = diff_ps[:, s, :]
+                        nc.tensor.matmul(
+                            acc, lhsT=x_half[hf][:, 2 * s, chans], rhs=minus_before[:, 0, :],
+                            start=True, stop=False,
+                        )
+                        nc.tensor.matmul(
+                            acc[:, P:T], lhsT=x_half[hf][:, 2 * s + 1, chans], rhs=minus_before[:, 1, P:T],
+                            start=False, stop=False,
+                        )
+                        nc.tensor.matmul(
+                            acc[:, 0:2], lhsT=small_mix[:, chans], rhs=minus_prev0[:, hf * SEQ_HALF + s, 0:2],
+                            start=False, stop=True,
+                        )
+                    return diff_ps
 
                 def log_of_bt(j):
                     for b in range(B):
@@ -248,21 +296,29 @@ def tile_rwkv_timemix_pa_kernel(
                             scale=by_decay[:, j, ROW_B0 + b : ROW_B0 + b + 1], bias=eps_col[:],
                         )
 
-                def by_channel_tile(dst, small):
+                def by_channel_tile(small):
                     small_ps = psum_mix.tile([P, CH_TILES, P], BF16, name="small_ps", tag="xt")
                     for j in range(CH_TILES):
-                        nc.tensor.transpose(small_ps[:, j, :], small[:, j * P : (j + 1) * P], ident_bf[:])
-                    nc.vector.tensor_copy(out=dst[:], in_=small_ps[:, :, 0:ROWS])
+                        g, t = divmod(j, PACK)
+                        nc.tensor.transpose(
+                            small_ps[:, j, :], small[:, g * 512 + t : (g + 1) * 512 : PACK], ident_bf[:]
+                        )
+                    return small_ps
 
-                def per_channel_constants():
-                    by_channel_tile(by_decay, small_decay)
-                    nc.vector.tensor_scalar_mul(out=neg_w[:], in0=by_decay[:, :, ROW_W : ROW_W + 1], scalar1=-1.0)
+                def decay_constants():
+                    small_ps = by_channel_tile(small_decay)
+                    nc.scalar.activation(
+                        out=neg_w[:], in_=small_ps[:, :, ROW_W : ROW_W + 1], func=ACT.Copy, scale=-1.0
+                    )
+                    nc.scalar.copy(out=by_decay[:], in_=small_ps[:, :, 0:ROWS])
                     for j in range(CH_TILES):
                         nc.scalar.activation(out=decay[:, j, :], in_=steps[:], func=ACT.Exp, scale=neg_w[:, j, :])
+
+                def state_constants():
                     nc.scalar.activation(
                         out=ln_b0_eps[:], in_=by_decay[:, :, ROW_B0 : ROW_B0 + B], func=ACT.Ln, scale=1.0 / EPS
                     )
-                    by_channel_tile(by_state, small_state)
+                    nc.vector.tensor_copy(out=by_state[:], in_=by_channel_tile(small_state)[:, :, 0:ROWS])
                     nc.vector.tensor_scalar_mul(out=neg_u[:], in0=by_state[:, :, ROW_U : ROW_U + 1], scalar1=-1.0)
                     nc.vector.reciprocal(out=inv_b0[:], in_=by_decay[:, :, ROW_B0 : ROW_B0 + B])
                     nc.vector.scalar_tensor_tensor(
@@ -271,16 +327,24 @@ def tile_rwkv_timemix_pa_kernel(
                     )
 
                 steps_of_mix = [(hf, g) for hf in range(HALVES) for g in range(GROUPS)]
-                prepare_planes(*steps_of_mix[0])
-                diff_banks = prepare_differences(*steps_of_mix[0])
+                prepare_pair(0, 0, 0)
+                small_planes(0)
+                diff_banks = [prepare_difference(0, 0, t) for t in (0, 1)]
+                prepare_pair(0, 0, 1)
+                decay_constants()
+                diff_banks += [prepare_difference(0, 0, t) for t in (2, 3)]
 
+                logs_of_step = ((), (0, 1), (2, 3, 4), (5, 6, 7))
                 mixed_before = None
                 for step, (hf, g) in enumerate(steps_of_mix):
                     seqs = slice(hf * SEQ_HALF, (hf + 1) * SEQ_HALF)
                     if step + 1 < len(steps_of_mix):
-                        prepare_planes(*steps_of_mix[step + 1])
+                        for k in range(PACK // 2):
+                            prepare_pair(*steps_of_mix[step + 1], k)
                     fresh = []
                     for m in (MIX_R, MIX_K, MIX_V):
+                        if m == MIX_V and g == TENSOR_GROUP:
+                            continue
                         mixed = carry.tile([P, PACK, HALF], BF16, name="mixed%d" % m, tag="slab%d" % m)
                         for t in range(PACK):
                             nc.vector.scalar_tensor_tensor(
@@ -290,97 +354,138 @@ def tile_rwkv_timemix_pa_kernel(
                                 op0=ALU.mult, op1=ALU.add,
                             )
                         fresh.append(mixed)
-                        if step == 0 and m == MIX_R:
-                            per_channel_constants()
+                        if step == 0 and m == MIX_K:
+                            small_planes(1)
+                            make_diagonals()
+                            sort_scales(0)
+                            state_constants()
+                    if step == 1:
+                        sort_codes(MIX_R)
+                        raw[MIX_K] = load_raw(MIX_K)
+                    if step == 2:
+                        sort_codes(MIX_V)
+                    if step == 3:
+                        sort_codes(MIX_K)
                     if mixed_before is not None:
                         regrouped = [new_grouped(m) for m in (MIX_R, MIX_K, MIX_V)]
                         for m in (MIX_R, MIX_K, MIX_V):
-                            regroup(m, regrouped[m], mixed_before[0][m], slice(0, HALF))
+                            if m == MIX_V and mixed_before[1] == TENSOR_GROUP:
+                                mix_by_tensor(mixed_before[2], regrouped[m])
+                            else:
+                                regroup(m, regrouped[m], mixed_before[0][m], slice(0, HALF))
+                        if step < 3:
+                            for piece in ((), (1, 2), (3,))[step]:
+                                sort_scales(piece)
                         for m in (MIX_V, MIX_K, MIX_R):
                             quantise_x(regrouped[m], m, mixed_before[1], mixed_before[2])
                     mixed_before = (fresh, g, hf)
                     if step + 1 < len(steps_of_mix):
-                        diff_banks = prepare_differences(*steps_of_mix[step + 1])
-                    for j in range(3 * step, min(3 * step + 3, CH_TILES)):
+                        diff_banks = [prepare_difference(*steps_of_mix[step + 1], t) for t in range(PACK)]
+                    for j in logs_of_step[step]:
                         log_of_bt(j)
-                for piece in range(2 * TOK_TILES):
-                    gate_piece(0, piece, psum_mix)
+                last_grouped_v = new_grouped(MIX_V)
+                mix_by_tensor(mixed_before[2], last_grouped_v)
 
         epi = ctx.enter_context(tc.tile_pool(name="epi", bufs=2, reuse_waits="tile"))
+        r_half = []
+        for hf in range(HALVES):
+            r_half.append(epi.tile([P, CH_TILES, HALF], F32, name="r_half%d" % hf, bufs=1))
         with tc.psum_pool(name="psum", bufs=2, reuse_waits="tile") as psum:
+            whole = tuple(range(SEQ_HALF))
+            units = [(0, j, whole) for j in range(CH_TILES)] + [(1, j, whole) for j in range(PACK)]
+            units += [(1, j, (s,)) for s in whole for j in range(PACK, CH_TILES)]
 
-            h_half = []
-            for hf in range(HALVES):
-                h_half.append(rows.tile([P, TOK_TILES, C], BF16, name="h_half%d" % hf, tag="rows"))
+            def tokens(seqs):
+                return slice(seqs[0] * T, (seqs[-1] + 1) * T)
 
-            units = [(hf, j) for hf in range(HALVES) for j in range(CH_TILES)]
-            tiles = {}
+            def width(seqs):
+                return len(seqs) * T
 
-            def start_v(n):
-                hf, j = units[n]
-                ch = slice(j * P, (j + 1) * P)
-                tokens = slice(hf * HALF, (hf + 1) * HALF)
-                v_ps = psum.tile([P, HALF], F32, name="v_ps", tag="v", bufs=3)
-                mx_product(v_ps[:], w_code[MIX_V], w_scale[:, MIX_V], ch, x_code[MIX_V], x_scale[MIX_V], tokens)
-                tiles[n] = (v_ps, tiles[n])
+            rho, k_bank, v_bank, sb, part = {}, {}, {}, {}, {}
+            wkv, h = {}, {}
 
             def start_rho(n):
-                hf, j = units[n]
-                rho = epi.tile([P, SEQ_HALF, T], F32, name="rho")
-                for s in range(SEQ_HALF):
+                hf, j, seqs = units[n]
+                rho[n] = epi.tile([P, SEQ_HALF, T], F32, name="rho")
+                for i, s in enumerate(seqs):
                     b = hf * SEQ_HALF + s
                     nc.scalar.activation(
-                        out=rho[:, s, :], in_=steps[:], func=ACT.Sigmoid,
+                        out=rho[n][:, i, :], in_=steps[:], func=ACT.Sigmoid,
                         scale=neg_w[:, j, :], bias=ln_b0_eps[:, j, b : b + 1],
                     )
-                tiles[n] = rho
 
             def start_k(n):
-                hf, j = units[n]
-                ch = slice(j * P, (j + 1) * P)
-                tokens = slice(hf * HALF, (hf + 1) * HALF)
-                k_ps = psum.tile([P, HALF], F32, name="k_ps", tag="k", bufs=1)
-                mx_product(k_ps[:], w_code[MIX_K], w_scale[:, MIX_K], ch, x_code[MIX_K], x_scale[MIX_K], tokens)
-                tiles[n] = (k_ps, tiles[n][0], tiles[n][1])
+                k_ps = psum.tile([P, HALF], F32, name="k_ps", tag="k")
+                hf, j, seqs = units[n]
+                channel_product(k_ps[:, 0 : width(seqs)], MIX_K, hf, j, tokens(seqs))
+                k_bank[n] = k_ps
+
+            def start_v(n):
+                v_ps = psum.tile([P, HALF], F32, name="v_ps", tag="v", bufs=3)
+                hf, j, seqs = units[n]
+                channel_product(v_ps[:, 0 : width(seqs)], MIX_V, hf, j, tokens(seqs))
+                v_bank[n] = v_ps
+
+            def make_r(hf, j):
+                r_ps = psum.tile([P, HALF], F32, name="r_ps", tag="misc", bufs=3)
+                channel_product(r_ps[:], MIX_R, hf, j, slice(0, HALF))
+                nc.scalar.activation(out=r_half[hf][:, j, :], in_=r_ps[:], func=ACT.Sigmoid)
 
             def weigh_unit(n):
-                hf, j = units[n]
-                k_ps, v_ps, rho = tiles[n]
-                sb = epi.tile([P, HALF], F32, name="sb")
+                hf, j, seqs = units[n]
+                sb[n] = epi.tile([P, HALF], F32, name="sb")
+                own = sb[n][:, 0 : width(seqs)]
+                first = hf * SEQ_HALF + seqs[0]
                 nc.vector.tensor_tensor(
-                    out=sb[:], in0=k_ps[:], op=ALU.subtract,
-                    in1=ln_bt[:, j, hf * SEQ_HALF : (hf + 1) * SEQ_HALF, :].rearrange("p s t -> p (s t)"),
+                    out=own, in0=k_bank[n][:, 0 : width(seqs)], op=ALU.subtract,
+                    in1=ln_bt[:, j, first : first + len(seqs), :].rearrange("p s t -> p (s t)"),
                 )
-                nc.scalar.activation(out=sb[:], in_=sb[:], func=ACT.Sigmoid, scale=-1.0, bias=neg_u[:, j, :])
-                tiles[n] = (v_ps, sb, rho)
+                nc.scalar.activation(out=own, in_=own, func=ACT.Sigmoid, scale=-1.0, bias=neg_u[:, j, :])
 
             def part_unit(n):
-                hf, j = units[n]
-                v_ps, sb, rho = tiles[n]
-                wkv = epi.tile([P, HALF], F32, name="wkv", bufs=3)
-                for s in range(SEQ_HALF):
+                hf, j, seqs = units[n]
+                part[n] = epi.tile([P, HALF], F32, name="part", bufs=3)
+                for i, s in enumerate(seqs):
                     b = hf * SEQ_HALF + s
                     nc.vector.scalar_tensor_tensor(
-                        out=wkv[:, s * T : (s + 1) * T], in0=rho[:, s, :],
-                        scalar=neg_ratio[:, j, b : b + 1], in1=v_ps[:, s * T : (s + 1) * T],
+                        out=part[n][:, i * T : (i + 1) * T], in0=rho[n][:, i, :],
+                        scalar=neg_ratio[:, j, b : b + 1], in1=v_bank[n][:, i * T : (i + 1) * T],
                         op0=ALU.mult, op1=ALU.add,
                     )
-                tiles[n] = (v_ps, sb, wkv)
 
             def blend_unit(n):
-                v_ps, sb, wkv = tiles[n]
-                nc.gpsimd.tensor_tensor(out=wkv[:], in0=wkv[:], in1=sb[:], op=ALU.mult)
-                nc.vector.tensor_tensor(out=wkv[:], in0=v_ps[:], in1=wkv[:], op=ALU.subtract)
-                wkv_ps = psum.tile([P, TOK_TILES, P], F32, name="wkv_ps", tag="wkv")
-                for q in range(TOK_TILES):
-                    nc.tensor.transpose(wkv_ps[:, q, :], wkv[:, q * P : (q + 1) * P], ident_f32[:])
-                tiles[n] = wkv_ps
-
-            def gate_unit(n):
-                hf, j = units[n]
-                ch = slice(j * P, (j + 1) * P)
+                hf, j, seqs = units[n]
+                g, t = divmod(j, PACK)
+                if (hf, g) not in wkv:
+                    wkv_tile = epi.tile([P, PACK, HALF], F32, name="wkv")
+                    wkv[(hf, g)] = wkv_tile
+                own = part[n][:, 0 : width(seqs)]
+                nc.gpsimd.tensor_tensor(out=own, in0=own, in1=sb[n][:, 0 : width(seqs)], op=ALU.mult)
                 nc.vector.tensor_tensor(
-                    out=h_half[hf][:, :, ch], in0=tiles[n][:], in1=gate[hf][:, :, ch], op=ALU.mult
+                    out=wkv[(hf, g)][:, t, tokens(seqs)], in0=v_bank[n][:, 0 : width(seqs)], in1=own, op=ALU.subtract
+                )
+
+            def gate_tokens(engine, hf, g, q):
+                if q == 0:
+                    h_grouped = epi.tile([P, HALF, PACK], BF16, name="h_grouped", align_bytes=64)
+                    h_code = epi.tile([P, HALF], U32, name="h_code", bufs=4, align_bytes=64)
+                    h_scale = epi.tile([P, HALF], U8, name="h_scale", bufs=4, align_bytes=64)
+                    h[(hf, g)] = (h_grouped, h_code, h_scale)
+                tok = slice(q * P, (q + 1) * P)
+                engine.tensor_tensor(
+                    out=h[(hf, g)][0][:, tok, :].rearrange("p (c i) t -> p c t i", i=4),
+                    in0=wkv[(hf, g)][:, :, tok].rearrange("p t (c i) -> p c t i", i=4),
+                    in1=r_half[hf][:, g * PACK : (g + 1) * PACK, tok].rearrange("p t (c i) -> p c t i", i=4),
+                    op=ALU.mult,
+                )
+
+            def quantise_h(hf, g, first, last):
+                h_grouped, h_code, h_scale = h[(hf, g)]
+                tok = slice(first * P, last * P)
+                nc.vector.quantize_mx(
+                    out=h_code[:, tok].bitcast(FP8X4),
+                    scales=h_scale[:, tok],
+                    in_=h_grouped[:, tok, :].rearrange("p n t -> p (n t)"),
                 )
 
             def copy_out(on_vector, dst, src):
@@ -389,140 +494,98 @@ def tile_rwkv_timemix_pa_kernel(
                 else:
                     nc.scalar.copy(out=dst, in_=src)
 
-            def regroup_h(hf, q, groups, on_vector, banks):
-                h_ps = banks.tile([P, len(groups) * 2, P], F32, name="h_ps", tag="misc")
-                words = h_half[hf][:, q, :].bitcast(F32)
-                for i, g in enumerate(groups):
-                    for k in range(2):
-                        nc.tensor.transpose(
-                            h_ps[:, i * 2 + k, :], words[:, g * 256 + k : (g + 1) * 256 : 2], ident_f32[:]
-                        )
-                if (hf, q) not in tiles:
-                    h_grouped = epi.tile([P, GROUPS, P, PACK], BF16, name="h_grouped", bufs=H_BUFS, align_bytes=64)
-                    h_code = epi.tile([P, GROUPS, P], U32, name="h_code", bufs=H_BUFS, align_bytes=64)
-                    h_scale = epi.tile([P, GROUPS, P], U8, name="h_scale", bufs=H_BUFS, align_bytes=64)
-                    tiles[(hf, q)] = (h_grouped, h_code, h_scale)
-                span = slice(groups[0], groups[0] + len(groups))
-                copy_out(
-                    on_vector,
-                    tiles[(hf, q)][0][:, span].rearrange("p g n t -> p (g n t)").bitcast(F32).rearrange(
-                        "p (g n k) -> p g n k", g=len(groups), k=2
-                    ),
-                    h_ps[:].rearrange("p (g k) n -> p g n k", k=2),
-                )
-
-            def quantise_h(hf, q, groups):
-                h_grouped, h_code, h_scale = tiles[(hf, q)]
-                span = slice(groups[0], groups[0] + len(groups))
-                nc.vector.quantize_mx(
-                    out=h_code[:, span].rearrange("p g n -> p (g n)").bitcast(FP8X4),
-                    scales=h_scale[:, span].rearrange("p g n -> p (g n)"),
-                    in_=h_grouped[:, span].rearrange("p g n t -> p (g n t)"),
-                )
-
             def new_result(hf, q):
                 return carry.tile([P, C], F32, name="result", tag="slab%d" % ((hf * TOK_TILES + q) % 3))
 
-            def project(hf, q, on_vector, banks):
-                h_code, h_scale = tiles[(hf, q)][1], tiles[(hf, q)][2]
+            def pass_over(out_ps, hf, q, g, nh):
+                tok, n_cols = slice(q * P, (q + 1) * P), slice(nh * 512, (nh + 1) * 512)
+                nc.tensor.matmul_mx(
+                    out=out_ps,
+                    lhsT=h[(hf, g)][1][:, tok].bitcast(FP8X4),
+                    lhsT_scale=h[(hf, g)][2][:, tok],
+                    rhs=w_code[W_OUT][:, g, n_cols].bitcast(FP8X4),
+                    rhs_scale=out_scale[:, g, n_cols],
+                    start=(g == 0),
+                    stop=(g == GROUPS - 1),
+                )
+
+            def store(hf, q, banks, vector_half):
                 result = new_result(hf, q)
                 first = hf * HALF + q * P
                 for nh in range(C // 512):
                     n_cols = slice(nh * 512, (nh + 1) * 512)
-                    out_ps = banks.tile([P, 512], F32, name="out_ps", tag="misc")
-                    mx_product(out_ps[:], h_code, h_scale, slice(0, P), w_code[W_OUT], w_scale[:, W_OUT], n_cols)
-                    copy_out(on_vector, result[:, n_cols], out_ps[:])
+                    copy_out(nh == vector_half, result[:, n_cols], banks[nh][:])
                     nc.sync.dma_start(out=out_rows[first : first + P, n_cols], in_=result[:, n_cols])
 
+            def project(hf, q):
+                banks = []
+                for nh in range(C // 512):
+                    out_ps = psum.tile([P, 512], F32, name="out_ps", tag="misc", bufs=3)
+                    for g in range(GROUPS):
+                        pass_over(out_ps[:], hf, q, g, nh)
+                    banks.append(out_ps)
+                store(hf, q, banks, None)
+
             last_mixed, last_g, last_hf = mixed_before
-            last_grouped = [new_grouped(m) for m in (MIX_R, MIX_K, MIX_V)]
+            last_grouped = [new_grouped(MIX_R), new_grouped(MIX_K), last_grouped_v]
             quarters = [slice(i * P, (i + 1) * P) for i in range(TOK_TILES)]
-            early_from = len(units) - 2
+            r_turns = {n: ((0, 2 * n), (0, 2 * n + 1)) for n in range(PACK)}
+            for j, n in enumerate((4, 5, 6, 7, 8, 9, 13, 15)):
+                r_turns[n] = ((1, j),)
+            gate_turns = {5 + 4 * i + q: (i // GROUPS, i % GROUPS, q) for i in range(3) for q in range(TOK_TILES)}
+            gate_turns[17] = (1, 1, 0)
+            gate_turns[18] = (1, 1, 1)
+            quantise_turns = {
+                9: (0, 0, 0, 4), 10: (0, 1, 0, 1), 11: (0, 1, 1, 2), 12: (0, 1, 2, 3), 13: (0, 1, 3, 4),
+                15: (1, 0, 0, 2), 17: (1, 0, 2, 4), 18: (1, 1, 0, 1), 19: (1, 1, 1, 2),
+            }
+            project_turns = {10: (0, 0), 11: (0, 1), 12: (0, 2), 14: (0, 3), 18: (1, 0), 19: (1, 1)}
             start_rho(0)
-            start_v(0)
             start_k(0)
-            for n in range(len(units) + 2):
+            start_v(0)
+            for n in range(len(units)):
                 if n + 1 < len(units):
                     start_rho(n + 1)
-                if n < len(units):
-                    weigh_unit(n)
-                before = units[n - 2] if n >= 2 else (0, 0)
+                weigh_unit(n)
                 if n == 2:
                     quantise_x(last_grouped[MIX_V], MIX_V, last_g, last_hf)
                     quantise_x(last_grouped[MIX_R], MIX_R, last_g, last_hf)
                 if n == 4:
                     quantise_x(last_grouped[MIX_K], MIX_K, last_g, last_hf)
-                if before[0] >= 1 and before[1] % 2 == 1:
-                    quantise_h(before[0] - 1, before[1] // 2, BOTH)
-                if early_from < n <= early_from + TOK_TILES and n < len(units) + 2:
-                    quantise_h(HALVES - 1, n - early_from - 1, LOWER)
-                if n < len(units):
-                    part_unit(n)
-                if n + 1 < len(units):
-                    start_v(n + 1)
-                if 3 <= n < 3 + 2 * TOK_TILES:
-                    gate_piece(1, n - 3, psum)
-                if before[0] >= 1 and before[1] % 2 == 1:
-                    project(before[0] - 1, before[1] // 2, False, psum)
+                if n in quantise_turns:
+                    quantise_h(*quantise_turns[n])
+                part_unit(n)
                 if n + 1 < len(units):
                     start_k(n + 1)
-                if before[0] >= 1 and before[1] % 2 == 0:
-                    regroup_h(before[0] - 1, before[1] // 2, BOTH, False, psum)
-                if early_from <= n < early_from + TOK_TILES:
-                    regroup_h(HALVES - 1, n - early_from, LOWER, False, psum)
-                if 1 <= n <= len(units):
+                    start_v(n + 1)
+                for hf, j in r_turns.get(n, ()):
+                    make_r(hf, j)
+                if n in project_turns:
+                    project(*project_turns[n])
+                if n >= 1:
                     blend_unit(n - 1)
-                if n >= 2:
-                    gate_unit(n - 2)
-                if n == 0:
-                    regroup(MIX_V, last_grouped[MIX_V], last_mixed[MIX_V], slice(0, HALF))
+                if n in gate_turns:
+                    hf, g, q = gate_turns[n]
+                    gate_tokens(nc.vector if q in VECTOR_TILES else nc.gpsimd, hf, g, q)
                 if n < 4:
                     m = (MIX_R, MIX_K)[n // 2]
-                    for tok in quarters[2 * (n % 2) : 2 * (n % 2) + 2]:
-                        regroup(m, last_grouped[m], last_mixed[m], tok)
+                    for i in (2 * (n % 2), 2 * (n % 2) + 1):
+                        regroup(m, last_grouped[m], last_mixed[m], quarters[i], on_vector=i % 2 == 1)
+            blend_unit(len(units) - 1)
 
-        with tc.psum_pool(name="psum_end", bufs=8, reuse_waits="tile") as psum_end:
-            last = HALVES - 1
+        with tc.psum_pool(name="psum_end", bufs=4, reuse_waits="tile") as psum_end:
+            hf = HALVES - 1
             banks = {}
-
-            def pass_over(g, q):
-                for nh in range(C // 512):
-                    if g == 0:
-                        out_ps = psum_end.tile([P, 512], F32, name="out_ps", tag="misc")
-                        banks[(q, nh)] = out_ps
-                    n_cols = slice(nh * 512, (nh + 1) * 512)
-                    nc.tensor.matmul_mx(
-                        out=banks[(q, nh)][:],
-                        lhsT=tiles[(last, q)][1][:, g, :].bitcast(FP8X4),
-                        lhsT_scale=tiles[(last, q)][2][:, g, :],
-                        rhs=w_code[W_OUT][:, g, n_cols].bitcast(FP8X4),
-                        rhs_scale=w_scale[:, W_OUT, g, n_cols],
-                        start=(g == 0),
-                        stop=(g == GROUPS - 1),
-                    )
-
-            def store(q):
-                result = new_result(last, q)
-                first = last * HALF + q * P
-                for nh in range(C // 512):
-                    n_cols = slice(nh * 512, (nh + 1) * 512)
-                    copy_out(nh == 1, result[:, n_cols], banks[(q, nh)][:])
-                    nc.sync.dma_start(out=out_rows[first : first + P, n_cols], in_=result[:, n_cols])
-
-            pass_over(0, 0)
-            pass_over(0, 1)
-            quantise_h(last, TOK_TILES - 1, LOWER)
-            for q in range(TOK_TILES):
-                regroup_h(last, q, UPPER, q % 2 == 1, psum_end)
-            for q in range(TOK_TILES):
-                quantise_h(last, q, UPPER)
-            pass_over(1, 0)
-            store(0)
-            pass_over(1, 1)
-            store(1)
-            pass_over(0, 2)
-            pass_over(0, 3)
-            pass_over(1, 2)
-            store(2)
-            pass_over(1, 3)
-            store(3)
+            gate_tokens(nc.vector, hf, 1, 2)
+            gate_tokens(nc.vector, hf, 1, 3)
+            quantise_h(hf, 1, 2, 3)
+            quantise_h(hf, 1, 3, 4)
+            for g in range(GROUPS):
+                for q in (2, 3):
+                    for nh in range(C // 512):
+                        if g == 0:
+                            out_ps = psum_end.tile([P, 512], F32, name="out_ps", tag="misc")
+                            banks[(q, nh)] = out_ps
+                        pass_over(banks[(q, nh)][:], hf, q, g, nh)
+                    if g == GROUPS - 1:
+                        store(hf, q, (banks[(q, 0)], banks[(q, 1)]), 1)

@@ -135,10 +135,8 @@ def tile_rwkv_timemix_pa_kernel(
             def sort_codes(wi):
                 nc.vector.tensor_copy(out=sorted_columns(w_code[wi]), in_=raw_columns(raw[wi]))
 
-            def sort_scales(piece):
-                nc.gpsimd.tensor_copy(
-                    out=sorted_columns(w_scale)[:, piece], in_=raw_columns(scale_raw)[:, piece]
-                )
+            def sort_scales():
+                nc.vector.tensor_copy(out=sorted_columns(w_scale), in_=raw_columns(scale_raw))
 
             minus_before = early.tile([P, 2, T], BF16, name="minus_before")
             nc.vector.memset(minus_before[:].rearrange("p a n -> p (a n)").bitcast(I32), 0)
@@ -357,13 +355,13 @@ def tile_rwkv_timemix_pa_kernel(
                         if step == 0 and m == MIX_K:
                             small_planes(1)
                             make_diagonals()
-                            sort_scales(0)
                             state_constants()
                     if step == 1:
                         sort_codes(MIX_R)
                         raw[MIX_K] = load_raw(MIX_K)
                     if step == 2:
                         sort_codes(MIX_V)
+                        sort_scales()
                     if step == 3:
                         sort_codes(MIX_K)
                     if mixed_before is not None:
@@ -373,9 +371,6 @@ def tile_rwkv_timemix_pa_kernel(
                                 mix_by_tensor(mixed_before[2], regrouped[m])
                             else:
                                 regroup(m, regrouped[m], mixed_before[0][m], slice(0, HALF))
-                        if step < 3:
-                            for piece in ((), (1, 2), (3,))[step]:
-                                sort_scales(piece)
                         for m in (MIX_V, MIX_K, MIX_R):
                             quantise_x(regrouped[m], m, mixed_before[1], mixed_before[2])
                     mixed_before = (fresh, g, hf)

@@ -33,7 +33,6 @@ ROWS = 1 + B
 MIX_R, MIX_K, MIX_V, W_OUT = 0, 1, 2, 3
 PLANE_ROW = (0, 4, 8)
 GROUPED_BUFS = (1, 1, 2)
-VECTOR_TILES = (1, 3)
 TENSOR_GROUP = 1
 
 FLOPS = 4 * 2 * B * T * C * C
@@ -174,12 +173,10 @@ def tile_rwkv_timemix_pa_kernel(
             def new_grouped(m):
                 return carry.tile([P, HALF, PACK], BF16, name="grouped%d" % m, bufs=GROUPED_BUFS[m], align_bytes=64)
 
-            def regroup(m, grouped, mixed, tok, on_vector=False):
+            def regroup(m, grouped, mixed, tok, on_scalar):
                 dst = grouped[:, tok, :].rearrange("p (c i) t -> p c t i", i=4)
                 src = mixed[:, :, tok].rearrange("p t (c i) -> p c t i", i=4)
-                if on_vector:
-                    nc.vector.tensor_copy(out=dst, in_=src)
-                elif m == MIX_V:
+                if on_scalar:
                     nc.scalar.copy(out=dst, in_=src)
                 else:
                     nc.gpsimd.tensor_scalar(
@@ -370,7 +367,7 @@ def tile_rwkv_timemix_pa_kernel(
                             if m == MIX_V and mixed_before[1] == TENSOR_GROUP:
                                 mix_by_tensor(mixed_before[2], regrouped[m])
                             else:
-                                regroup(m, regrouped[m], mixed_before[0][m], slice(0, HALF))
+                                regroup(m, regrouped[m], mixed_before[0][m], slice(0, HALF), m == MIX_V)
                         for m in (MIX_V, MIX_K, MIX_R):
                             quantise_x(regrouped[m], m, mixed_before[1], mixed_before[2])
                     mixed_before = (fresh, g, hf)
@@ -387,8 +384,9 @@ def tile_rwkv_timemix_pa_kernel(
             r_half.append(epi.tile([P, CH_TILES, HALF], F32, name="r_half%d" % hf, bufs=1))
         with tc.psum_pool(name="psum", bufs=2, reuse_waits="tile") as psum:
             whole = tuple(range(SEQ_HALF))
-            units = [(0, j, whole) for j in range(CH_TILES)] + [(1, j, whole) for j in range(PACK)]
-            units += [(1, j, (s,)) for s in whole for j in range(PACK, CH_TILES)]
+            tiles = [(hf, j) for hf in range(HALVES) for j in range(CH_TILES)]
+            units = [(hf, j, whole) for hf, j in tiles[:-2]]
+            units += [(hf, j, (s,)) for s in whole for hf, j in tiles[-2:]]
 
             def tokens(seqs):
                 return slice(seqs[0] * T, (seqs[-1] + 1) * T)
@@ -524,17 +522,16 @@ def tile_rwkv_timemix_pa_kernel(
             last_mixed, last_g, last_hf = mixed_before
             last_grouped = [new_grouped(MIX_R), new_grouped(MIX_K), last_grouped_v]
             quarters = [slice(i * P, (i + 1) * P) for i in range(TOK_TILES)]
-            r_turns = {n: ((0, 2 * n), (0, 2 * n + 1)) for n in range(PACK)}
-            for j, n in enumerate((4, 5, 6, 7, 8, 9, 13, 15)):
-                r_turns[n] = ((1, j),)
-            gate_turns = {5 + 4 * i + q: (i // GROUPS, i % GROUPS, q) for i in range(3) for q in range(TOK_TILES)}
-            gate_turns[17] = (1, 1, 0)
-            gate_turns[18] = (1, 1, 1)
-            quantise_turns = {
-                9: (0, 0, 0, 4), 10: (0, 1, 0, 1), 11: (0, 1, 1, 2), 12: (0, 1, 2, 3), 13: (0, 1, 3, 4),
-                15: (1, 0, 0, 2), 17: (1, 0, 2, 4), 18: (1, 1, 0, 1), 19: (1, 1, 1, 2),
+            gpsimd_gates = {5: (0, 0, 0), 7: (0, 0, 2), 9: (0, 1, 0), 11: (0, 1, 2)}
+            vector_gates = {
+                6: ((0, 0, 1),), 8: ((0, 0, 3),), 10: ((0, 1, 1),), 12: ((0, 1, 3),), 13: ((1, 0, 0),), 14: ((1, 0, 1),),
+                15: ((1, 0, 2),), 16: ((1, 0, 3),), 17: ((1, 1, 0), (1, 1, 1)),
             }
-            project_turns = {10: (0, 0), 11: (0, 1), 12: (0, 2), 14: (0, 3), 18: (1, 0), 19: (1, 1)}
+            quantise_turns = {
+                10: ((0, 0, 0, 4),), 11: ((0, 1, 0, 1),), 12: ((0, 1, 1, 2),), 13: ((0, 1, 2, 3),),
+                14: ((0, 1, 3, 4),), 16: ((1, 0, 0, 2),), 17: ((1, 0, 2, 4), (1, 1, 0, 2)),
+            }
+            project_turns = {11: ((0, 0),), 12: ((0, 1),), 13: ((0, 2),), 15: ((0, 3),), 17: ((1, 0), (1, 1))}
             start_rho(0)
             start_k(0)
             start_v(0)
@@ -542,30 +539,30 @@ def tile_rwkv_timemix_pa_kernel(
                 if n + 1 < len(units):
                     start_rho(n + 1)
                 weigh_unit(n)
+                part_unit(n)
                 if n == 2:
                     quantise_x(last_grouped[MIX_V], MIX_V, last_g, last_hf)
-                    quantise_x(last_grouped[MIX_R], MIX_R, last_g, last_hf)
                 if n == 4:
+                    quantise_x(last_grouped[MIX_R], MIX_R, last_g, last_hf)
                     quantise_x(last_grouped[MIX_K], MIX_K, last_g, last_hf)
-                if n in quantise_turns:
-                    quantise_h(*quantise_turns[n])
-                part_unit(n)
+                for piece in vector_gates.get(n, ()):
+                    gate_tokens(nc.vector, *piece)
+                for piece in quantise_turns.get(n, ()):
+                    quantise_h(*piece)
                 if n + 1 < len(units):
                     start_k(n + 1)
                     start_v(n + 1)
-                for hf, j in r_turns.get(n, ()):
-                    make_r(hf, j)
-                if n in project_turns:
-                    project(*project_turns[n])
+                if n < len(tiles):
+                    make_r(*tiles[n])
+                for piece in project_turns.get(n, ()):
+                    project(*piece)
                 if n >= 1:
                     blend_unit(n - 1)
-                if n in gate_turns:
-                    hf, g, q = gate_turns[n]
-                    gate_tokens(nc.vector if q in VECTOR_TILES else nc.gpsimd, hf, g, q)
+                if n in gpsimd_gates:
+                    gate_tokens(nc.gpsimd, *gpsimd_gates[n])
                 if n < 4:
-                    m = (MIX_R, MIX_K)[n // 2]
-                    for i in (2 * (n % 2), 2 * (n % 2) + 1):
-                        regroup(m, last_grouped[m], last_mixed[m], quarters[i], on_vector=i % 2 == 1)
+                    regroup(MIX_R, last_grouped[MIX_R], last_mixed[MIX_R], quarters[n], True)
+                    regroup(MIX_K, last_grouped[MIX_K], last_mixed[MIX_K], quarters[n], False)
             blend_unit(len(units) - 1)
 
         with tc.psum_pool(name="psum_end", bufs=4, reuse_waits="tile") as psum_end:

@@ -33,7 +33,7 @@ ROWS = 1 + B
 MIX_R, MIX_K, MIX_V, W_OUT = 0, 1, 2, 3
 PLANE_ROW = (0, 4, 8)
 GROUPED_BUFS = (1, 1, 2)
-TENSOR_GROUP = 1
+TENSOR_SEQ = 1
 
 FLOPS = 4 * 2 * B * T * C * C
 
@@ -158,9 +158,8 @@ def tile_rwkv_timemix_pa_kernel(
             for m in range(3):
                 x_code.append(keep.tile([P, GROUPS, B * T], U32, name="x_code%d" % m, align_bytes=64))
                 x_scale.append(keep.tile([P, GROUPS, B * T], U8, name="x_scale%d" % m, align_bytes=64))
-            diag = early.tile([P, PACK, 2, P], BF16, name="diag")
+            diag = early.tile([P, PLANES, 2, P], BF16, name="diag")
             by_decay = early.tile([P, CH_TILES, ROWS], F32, name="by_decay")
-            by_state = keep.tile([P, CH_TILES, ROWS], F32, name="by_state")
             mu_plane = keep.tile([P, PLANES, 3], F32, name="mu_plane")
             neg_w = keep.tile([P, CH_TILES, 1], F32, name="neg_w")
             neg_u = keep.tile([P, CH_TILES, 1], F32, name="neg_u")
@@ -172,6 +171,22 @@ def tile_rwkv_timemix_pa_kernel(
 
             def new_grouped(m):
                 return carry.tile([P, HALF, PACK], BF16, name="grouped%d" % m, bufs=GROUPED_BUFS[m], align_bytes=64)
+
+            whole = tuple(range(SEQ_HALF))
+            tiles = [(hf, j) for hf in range(HALVES) for j in range(CH_TILES)]
+            units = [(hf, j, whole) for hf, j in tiles[:-2]]
+            units += [(hf, j, (s,)) for s in whole for hf, j in tiles[-2:]]
+            rho = {}
+
+            def start_rho(n):
+                hf, j, seqs = units[n]
+                rho[n] = carry.tile([P, SEQ_HALF, T], F32, name="rho")
+                for i, s in enumerate(seqs):
+                    b = hf * SEQ_HALF + s
+                    nc.scalar.activation(
+                        out=rho[n][:, i, :], in_=steps[:], func=ACT.Sigmoid,
+                        scale=neg_w[:, j, :], bias=ln_b0_eps[:, j, b : b + 1],
+                    )
 
             def regroup(m, grouped, mixed, tok, on_scalar):
                 dst = grouped[:, tok, :].rearrange("p (c i) t -> p c t i", i=4)
@@ -222,29 +237,30 @@ def tile_rwkv_timemix_pa_kernel(
                         in_=by_plane_ps[:, :, ROW_XPREV : ROW_XPREV + B].rearrange("p (r e) b -> p r b e", e=2),
                     )
 
-                def make_diagonals():
-                    for t in range(PACK):
+                def make_diagonals(g):
+                    for plane in range(g * PACK, (g + 1) * PACK):
                         for i, sign in enumerate((1.0, -1.0)):
                             nc.gpsimd.tensor_scalar(
-                                out=diag[:, t, i, :], in0=ident_bf[:], op0=ALU.mult, op1=ALU.mult,
-                                scalar1=mu_plane[:, TENSOR_GROUP * PACK + t, MIX_V : MIX_V + 1], scalar2=sign,
+                                out=diag[:, plane, i, :], in0=ident_bf[:], op0=ALU.mult, op1=ALU.mult,
+                                scalar1=mu_plane[:, plane, MIX_V : MIX_V + 1], scalar2=sign,
                             )
 
-                def mix_by_tensor(hf, grouped):
-                    for q in range(TOK_TILES):
-                        b, a = hf * SEQ_HALF + q // 2, q % 2
+                def mix_by_tensor(hf, g, grouped):
+                    b = hf * SEQ_HALF + TENSOR_SEQ
+                    for a in range(T // P):
                         mix_ps = psum_mix.tile([P, PACK, P], F32, name="mix_ps", tag="misc")
                         for t in range(PACK):
-                            plane = TENSOR_GROUP * PACK + t
+                            plane = g * PACK + t
                             pair = x_pairs[:, plane // 2, b, :, plane % 2]
                             now = pair[:, LEAD + a * P : LEAD + (a + 1) * P]
                             before = pair[:, LEAD - 1 + a * P : LEAD - 1 + (a + 1) * P]
                             acc = mix_ps[:, t, :]
-                            nc.tensor.matmul(acc, lhsT=diag[:, t, 0, :], rhs=now, start=True, stop=False)
-                            nc.tensor.matmul(acc, lhsT=diag[:, t, 1, :], rhs=before, start=False, stop=False)
+                            nc.tensor.matmul(acc, lhsT=diag[:, plane, 0, :], rhs=now, start=True, stop=False)
+                            nc.tensor.matmul(acc, lhsT=diag[:, plane, 1, :], rhs=before, start=False, stop=False)
                             nc.tensor.matmul(acc, lhsT=ident_bf[:], rhs=before, start=False, stop=True)
+                        first = TENSOR_SEQ * T + a * P
                         nc.scalar.copy(
-                            out=grouped[:, q * P : (q + 1) * P, :], in_=mix_ps[:].rearrange("p t n -> p n t")
+                            out=grouped[:, first : first + P, :], in_=mix_ps[:].rearrange("p t n -> p n t")
                         )
 
                 def before_of(plane, seqs):
@@ -310,49 +326,69 @@ def tile_rwkv_timemix_pa_kernel(
                         nc.scalar.activation(out=decay[:, j, :], in_=steps[:], func=ACT.Exp, scale=neg_w[:, j, :])
 
                 def state_constants():
-                    nc.scalar.activation(
-                        out=ln_b0_eps[:], in_=by_decay[:, :, ROW_B0 : ROW_B0 + B], func=ACT.Ln, scale=1.0 / EPS
-                    )
-                    nc.vector.tensor_copy(out=by_state[:], in_=by_channel_tile(small_state)[:, :, 0:ROWS])
-                    nc.vector.tensor_scalar_mul(out=neg_u[:], in0=by_state[:, :, ROW_U : ROW_U + 1], scalar1=-1.0)
-                    nc.vector.reciprocal(out=inv_b0[:], in_=by_decay[:, :, ROW_B0 : ROW_B0 + B])
+                    small_ps = by_channel_tile(small_state)
+                    nc.vector.tensor_scalar_mul(out=neg_u[:], in0=small_ps[:, :, ROW_U : ROW_U + 1], scalar1=-1.0)
                     nc.vector.scalar_tensor_tensor(
-                        out=neg_ratio[:], in0=by_state[:, :, ROW_A0 : ROW_A0 + B], scalar=-1.0, in1=inv_b0[:],
+                        out=neg_ratio[:], in0=small_ps[:, :, ROW_A0 : ROW_A0 + B], scalar=-1.0, in1=inv_b0[:],
                         op0=ALU.mult, op1=ALU.mult,
                     )
+
+                def invert_b0():
+                    nc.vector.reciprocal(out=inv_b0[:], in_=by_decay[:, :, ROW_B0 : ROW_B0 + B])
+
+                first_step_extras = {
+                    (1, MIX_V): lambda: (small_planes(1), make_diagonals(1)),
+                    (2, MIX_R): invert_b0,
+                    (2, MIX_V): state_constants,
+                }
 
                 steps_of_mix = [(hf, g) for hf in range(HALVES) for g in range(GROUPS)]
                 prepare_pair(0, 0, 0)
                 small_planes(0)
+                make_diagonals(0)
                 diff_banks = [prepare_difference(0, 0, t) for t in (0, 1)]
                 prepare_pair(0, 0, 1)
                 decay_constants()
                 diff_banks += [prepare_difference(0, 0, t) for t in (2, 3)]
 
                 logs_of_step = ((), (0, 1), (2, 3, 4), (5, 6, 7))
+                def regroup_step(grouped, mixed, g, hf):
+                    regroup(MIX_R, grouped[MIX_R], mixed[MIX_R], slice(0, HALF), False)
+                    regroup(MIX_K, grouped[MIX_K], mixed[MIX_K], slice(0, HALF), False)
+                    regroup(MIX_V, grouped[MIX_V], mixed[MIX_V], slice(0, TENSOR_SEQ * T), True)
+                    mix_by_tensor(hf, g, grouped[MIX_V])
+
                 mixed_before = None
                 for step, (hf, g) in enumerate(steps_of_mix):
                     seqs = slice(hf * SEQ_HALF, (hf + 1) * SEQ_HALF)
-                    if step + 1 < len(steps_of_mix):
-                        for k in range(PACK // 2):
-                            prepare_pair(*steps_of_mix[step + 1], k)
-                    fresh = []
+                    def prepare_next():
+                        if step + 1 < len(steps_of_mix):
+                            for k in range(PACK // 2):
+                                prepare_pair(*steps_of_mix[step + 1], k)
+
+                    if step > 0:
+                        prepare_next()
+                    fresh, counts = [], []
                     for m in (MIX_R, MIX_K, MIX_V):
-                        if m == MIX_V and g == TENSOR_GROUP:
-                            continue
-                        mixed = carry.tile([P, PACK, HALF], BF16, name="mixed%d" % m, tag="slab%d" % m)
-                        for t in range(PACK):
+                        counts.append(TENSOR_SEQ if m == MIX_V else SEQ_HALF)
+                        mixed = carry.tile([P, PACK, counts[m] * T], BF16, name="mixed%d" % m, tag="slab%d" % m)
+                        fresh.append(mixed)
+                    for t in range(PACK):
+                        for m in (MIX_R, MIX_K, MIX_V):
                             nc.vector.scalar_tensor_tensor(
-                                out=mixed[:, t, :].rearrange("p (s t) -> p s t", s=SEQ_HALF),
-                                in0=diff_banks[t][:], scalar=mu_plane[:, g * PACK + t, m : m + 1],
-                                in1=before_of(g * PACK + t, seqs),
+                                out=fresh[m][:, t, :].rearrange("p (s t) -> p s t", s=counts[m]),
+                                in0=diff_banks[t][:, 0 : counts[m], :],
+                                scalar=mu_plane[:, g * PACK + t, m : m + 1],
+                                in1=before_of(g * PACK + t, slice(seqs.start, seqs.start + counts[m])),
                                 op0=ALU.mult, op1=ALU.add,
                             )
-                        fresh.append(mixed)
-                        if step == 0 and m == MIX_K:
-                            small_planes(1)
-                            make_diagonals()
-                            state_constants()
+                            if step == 0 and (t, m) in first_step_extras:
+                                first_step_extras[(t, m)]()
+                    if step == 0:
+                        prepare_next()
+                        nc.scalar.activation(
+                            out=ln_b0_eps[:], in_=by_decay[:, :, ROW_B0 : ROW_B0 + B], func=ACT.Ln, scale=1.0 / EPS
+                        )
                     if step == 1:
                         sort_codes(MIX_R)
                         raw[MIX_K] = load_raw(MIX_K)
@@ -363,11 +399,7 @@ def tile_rwkv_timemix_pa_kernel(
                         sort_codes(MIX_K)
                     if mixed_before is not None:
                         regrouped = [new_grouped(m) for m in (MIX_R, MIX_K, MIX_V)]
-                        for m in (MIX_R, MIX_K, MIX_V):
-                            if m == MIX_V and mixed_before[1] == TENSOR_GROUP:
-                                mix_by_tensor(mixed_before[2], regrouped[m])
-                            else:
-                                regroup(m, regrouped[m], mixed_before[0][m], slice(0, HALF), m == MIX_V)
+                        regroup_step(regrouped, *mixed_before)
                         for m in (MIX_V, MIX_K, MIX_R):
                             quantise_x(regrouped[m], m, mixed_before[1], mixed_before[2])
                     mixed_before = (fresh, g, hf)
@@ -375,37 +407,25 @@ def tile_rwkv_timemix_pa_kernel(
                         diff_banks = [prepare_difference(*steps_of_mix[step + 1], t) for t in range(PACK)]
                     for j in logs_of_step[step]:
                         log_of_bt(j)
+                start_rho(0)
+                last_mixed, last_g, last_hf = mixed_before
                 last_grouped_v = new_grouped(MIX_V)
-                mix_by_tensor(mixed_before[2], last_grouped_v)
+                regroup(MIX_V, last_grouped_v, last_mixed[MIX_V], slice(0, TENSOR_SEQ * T), True)
+                mix_by_tensor(last_hf, last_g, last_grouped_v)
 
         epi = ctx.enter_context(tc.tile_pool(name="epi", bufs=2, reuse_waits="tile"))
         r_half = []
         for hf in range(HALVES):
             r_half.append(epi.tile([P, CH_TILES, HALF], F32, name="r_half%d" % hf, bufs=1))
         with tc.psum_pool(name="psum", bufs=2, reuse_waits="tile") as psum:
-            whole = tuple(range(SEQ_HALF))
-            tiles = [(hf, j) for hf in range(HALVES) for j in range(CH_TILES)]
-            units = [(hf, j, whole) for hf, j in tiles[:-2]]
-            units += [(hf, j, (s,)) for s in whole for hf, j in tiles[-2:]]
-
             def tokens(seqs):
                 return slice(seqs[0] * T, (seqs[-1] + 1) * T)
 
             def width(seqs):
                 return len(seqs) * T
 
-            rho, k_bank, v_bank, sb, part = {}, {}, {}, {}, {}
+            k_bank, v_bank, sb, part = {}, {}, {}, {}
             wkv, h = {}, {}
-
-            def start_rho(n):
-                hf, j, seqs = units[n]
-                rho[n] = epi.tile([P, SEQ_HALF, T], F32, name="rho")
-                for i, s in enumerate(seqs):
-                    b = hf * SEQ_HALF + s
-                    nc.scalar.activation(
-                        out=rho[n][:, i, :], in_=steps[:], func=ACT.Sigmoid,
-                        scale=neg_w[:, j, :], bias=ln_b0_eps[:, j, b : b + 1],
-                    )
 
             def start_k(n):
                 k_ps = psum.tile([P, HALF], F32, name="k_ps", tag="k")
@@ -519,7 +539,6 @@ def tile_rwkv_timemix_pa_kernel(
                     banks.append(out_ps)
                 store(hf, q, banks, None)
 
-            last_mixed, last_g, last_hf = mixed_before
             last_grouped = [new_grouped(MIX_R), new_grouped(MIX_K), last_grouped_v]
             quarters = [slice(i * P, (i + 1) * P) for i in range(TOK_TILES)]
             gpsimd_gates = {5: (0, 0, 0), 7: (0, 0, 2), 9: (0, 1, 0), 11: (0, 1, 2)}
@@ -532,7 +551,6 @@ def tile_rwkv_timemix_pa_kernel(
                 14: ((0, 1, 3, 4),), 16: ((1, 0, 0, 2),), 17: ((1, 0, 2, 4), (1, 1, 0, 2)),
             }
             project_turns = {11: ((0, 0),), 12: ((0, 1),), 13: ((0, 2),), 15: ((0, 3),), 17: ((1, 0), (1, 1))}
-            start_rho(0)
             start_k(0)
             start_v(0)
             for n in range(len(units)):

@@ -60,7 +60,6 @@ def tile_rwkv_timemix_pa_kernel(
             small_decay = early.tile([P, C], BF16, name="small_decay")
             nc.vector.memset(small_decay[:].bitcast(I32), 0)
             small_state = early.tile([P, C], BF16, name="small_state")
-            nc.vector.memset(small_state[:].bitcast(I32), 0)
             x_half = []
             for hf in range(HALVES):
                 x_half.append(early.tile([P, TOK_TILES, C], BF16, name="x_half%d" % hf))
@@ -74,13 +73,26 @@ def tile_rwkv_timemix_pa_kernel(
             nc.vector.memset(eps_col[:], EPS)
             table_first = early.tile([P, 1], F32, name="table_first")
             nc.scalar.activation(out=table_first[:], in_=eps_col[:], func=ACT.Exp)
+            def load_words(tile, words):
+                for g in range(GROUPS):
+                    nc.sync.dma_start(
+                        out=tile[:, g, :], in_=words[g].rearrange("p n t -> p (n t)").bitcast(I32)
+                    )
+
+            def load_raw(wi):
+                tile = early.tile([P, GROUPS, C], I32, name="raw%d" % wi, tag="raw", bufs=2, align_bytes=64)
+                load_words(tile, weight_words[wi])
+                return tile
+
             load_x(0, slice(0, C // 2))
             for m, mu in enumerate((mu_r, mu_k, mu_v)):
                 nc.sync.dma_start(out=small_mix[ROW_MU + m : ROW_MU + m + 1, :], in_=mu.unsqueeze(0))
             nc.sync.dma_start(out=small_mix[ROW_XPREV : ROW_XPREV + B, :], in_=x_prev0)
             nc.sync.dma_start(out=small_decay[ROW_W : ROW_W + 1, :], in_=w.unsqueeze(0))
             nc.sync.dma_start(out=small_decay[ROW_B0 : ROW_B0 + B, :], in_=b0)
+            raw = {MIX_R: load_raw(MIX_R)}
             load_x(0, slice(C // 2, C))
+            nc.vector.memset(small_state[:].bitcast(I32), 0)
             nc.sync.dma_start(out=small_state[ROW_U : ROW_U + 1, :], in_=u.unsqueeze(0))
             nc.sync.dma_start(out=small_state[ROW_A0 : ROW_A0 + B, :], in_=a0)
             load_x(1, slice(0, C))
@@ -93,9 +105,9 @@ def tile_rwkv_timemix_pa_kernel(
             nc.gpsimd.iota(steps_int[:], pattern=[[1, T]], base=1, channel_multiplier=0)
 
             scale_raw = early.tile([P, GROUPS, C], U8, name="scale_raw", align_bytes=64)
-            nc.vector.memset(scale_raw[:].rearrange("p g n -> p (g n)").bitcast(I32), 0)
+            nc.gpsimd.memset(scale_raw[:].rearrange("p g n -> p (g n)").bitcast(I32), 0)
             out_scale = keep.tile([P, GROUPS, C], U8, name="out_scale", align_bytes=64)
-            nc.vector.memset(out_scale[:].rearrange("p g n -> p (g n)").bitcast(I32), 0)
+            nc.gpsimd.memset(out_scale[:].rearrange("p g n -> p (g n)").bitcast(I32), 0)
 
             def load_scales(tile, first, scales):
                 by_row = scales.rearrange("g (q r) n -> r q g n", r=4)
@@ -104,17 +116,6 @@ def tile_rwkv_timemix_pa_kernel(
                         out=tile[first + r : P : 32, :, :].bitcast(I32), in_=by_row[r].bitcast(I32)
                     )
 
-            def load_words(tile, words):
-                for g in range(GROUPS):
-                    nc.sync.dma_start(
-                        out=tile[:, g, :], in_=words[g].rearrange("p n t -> p (n t)").bitcast(I32)
-                    )
-
-            def load_raw(wi):
-                tile = early.tile([P, GROUPS, C], I32, name="raw%d" % wi, tag="raw", bufs=2, align_bytes=64)
-                load_words(tile, weight_words[wi])
-                return tile
-
             w_scale = keep.tile([P, GROUPS, C], U8, name="w_scale", align_bytes=64)
             w_code = []
             for wi in range(4):
@@ -122,7 +123,7 @@ def tile_rwkv_timemix_pa_kernel(
             for wi in (MIX_R, MIX_K, MIX_V):
                 load_scales(scale_raw, PLANE_ROW[wi], weight_scales[wi])
             load_scales(out_scale, 0, weight_scales[W_OUT])
-            raw = {MIX_R: load_raw(MIX_R), MIX_V: load_raw(MIX_V)}
+            raw[MIX_V] = load_raw(MIX_V)
             load_words(w_code[W_OUT], weight_words[W_OUT])
 
             def sorted_columns(tile):
@@ -139,7 +140,7 @@ def tile_rwkv_timemix_pa_kernel(
 
             minus_before = early.tile([P, 2, T], BF16, name="minus_before")
             nc.vector.memset(minus_before[:].rearrange("p a n -> p (a n)").bitcast(I32), 0)
-            minus_prev0 = early.tile([P, B, T], BF16, name="minus_prev0")
+            minus_prev0 = early.tile([P, B, 2], BF16, name="minus_prev0")
             nc.vector.memset(minus_prev0[:].rearrange("p a n -> p (a n)").bitcast(I32), 0)
             for a in range(2):
                 own = minus_before[:, a, a * P : (a + 1) * P]
@@ -295,7 +296,7 @@ def tile_rwkv_timemix_pa_kernel(
                             start=False, stop=False,
                         )
                         nc.tensor.matmul(
-                            acc[:, 0:2], lhsT=small_mix[:, chans], rhs=minus_prev0[:, hf * SEQ_HALF + s, 0:2],
+                            acc[:, 0:2], lhsT=small_mix[:, chans], rhs=minus_prev0[:, hf * SEQ_HALF + s, :],
                             start=False, stop=True,
                         )
                     return diff_ps
@@ -337,6 +338,7 @@ def tile_rwkv_timemix_pa_kernel(
                     nc.vector.reciprocal(out=inv_b0[:], in_=by_decay[:, :, ROW_B0 : ROW_B0 + B])
 
                 first_step_extras = {
+                    (1, MIX_K): lambda: sort_codes(MIX_R),
                     (1, MIX_V): lambda: (small_planes(1), make_diagonals(1)),
                     (2, MIX_R): invert_b0,
                     (2, MIX_V): state_constants,
@@ -389,8 +391,7 @@ def tile_rwkv_timemix_pa_kernel(
                         nc.scalar.activation(
                             out=ln_b0_eps[:], in_=by_decay[:, :, ROW_B0 : ROW_B0 + B], func=ACT.Ln, scale=1.0 / EPS
                         )
-                    if step == 1:
-                        sort_codes(MIX_R)
+                    if step == 0:
                         raw[MIX_K] = load_raw(MIX_K)
                     if step == 2:
                         sort_codes(MIX_V)
@@ -544,11 +545,12 @@ def tile_rwkv_timemix_pa_kernel(
             gpsimd_gates = {5: (0, 0, 0), 7: (0, 0, 2), 9: (0, 1, 0), 11: (0, 1, 2)}
             vector_gates = {
                 6: ((0, 0, 1),), 8: ((0, 0, 3),), 10: ((0, 1, 1),), 12: ((0, 1, 3),), 13: ((1, 0, 0),), 14: ((1, 0, 1),),
-                15: ((1, 0, 2),), 16: ((1, 0, 3),), 17: ((1, 1, 0), (1, 1, 1)),
+                15: ((1, 0, 2),), 16: ((1, 0, 3),),
             }
+            late_gates = {16: ((1, 1, 0), (1, 1, 1))}
             quantise_turns = {
                 10: ((0, 0, 0, 4),), 11: ((0, 1, 0, 1),), 12: ((0, 1, 1, 2),), 13: ((0, 1, 2, 3),),
-                14: ((0, 1, 3, 4),), 16: ((1, 0, 0, 2),), 17: ((1, 0, 2, 4), (1, 1, 0, 2)),
+                14: ((0, 1, 3, 4),), 16: ((1, 0, 0, 2),), 17: ((1, 1, 0, 2), (1, 0, 2, 4)),
             }
             project_turns = {11: ((0, 0),), 12: ((0, 1),), 13: ((0, 2),), 15: ((0, 3),), 17: ((1, 0), (1, 1))}
             start_k(0)
@@ -578,6 +580,8 @@ def tile_rwkv_timemix_pa_kernel(
                     blend_unit(n - 1)
                 if n in gpsimd_gates:
                     gate_tokens(nc.gpsimd, *gpsimd_gates[n])
+                for piece in late_gates.get(n, ()):
+                    gate_tokens(nc.vector, *piece)
                 if n < 4:
                     regroup(MIX_R, last_grouped[MIX_R], last_mixed[MIX_R], quarters[n], True)
                     regroup(MIX_K, last_grouped[MIX_K], last_mixed[MIX_K], quarters[n], False)

@@ -357,7 +357,7 @@ def tile_rwkv_timemix_pa_kernel(
                 def regroup_step(grouped, mixed, g, hf):
                     regroup(MIX_R, grouped[MIX_R], mixed[MIX_R], slice(0, HALF), False)
                     regroup(MIX_K, grouped[MIX_K], mixed[MIX_K], slice(0, HALF), False)
-                    regroup(MIX_V, grouped[MIX_V], mixed[MIX_V], slice(0, TENSOR_SEQ * T), True)
+                    regroup(MIX_V, grouped[MIX_V], mixed[MIX_V], slice(0, TENSOR_SEQ * T), (hf, g) != (0, 0))
                     mix_by_tensor(hf, g, grouped[MIX_V])
 
                 mixed_before = None
@@ -583,7 +583,7 @@ def tile_rwkv_timemix_pa_kernel(
                 for piece in late_gates.get(n, ()):
                     gate_tokens(nc.vector, *piece)
                 if n < 4:
-                    regroup(MIX_R, last_grouped[MIX_R], last_mixed[MIX_R], quarters[n], True)
+                    regroup(MIX_R, last_grouped[MIX_R], last_mixed[MIX_R], quarters[n], n in (2, 3))
                     regroup(MIX_K, last_grouped[MIX_K], last_mixed[MIX_K], quarters[n], False)
             blend_unit(len(units) - 1)
 

@@ -133,7 +133,10 @@ def tile_rwkv_timemix_pa_kernel(
                 return tile[:].rearrange("p g (b m t) -> p (g b) t m", b=GROUPS, t=PACK)
 
             def sort_codes(wi):
-                nc.vector.tensor_copy(out=sorted_columns(w_code[wi]), in_=raw_columns(raw[wi]))
+                nc.vector.tensor_copy(
+                    out=sorted_columns(w_code[wi]).rearrange("p x t (c i) -> p x c t i", i=4),
+                    in_=raw_columns(raw[wi]).rearrange("p x t (c i) -> p x c t i", i=4),
+                )
 
             def sort_scales():
                 nc.vector.tensor_copy(out=sorted_columns(w_scale), in_=raw_columns(scale_raw))

from contextlib import ExitStack

import concourse.mybir as mybir
from concourse.masks import make_identity

F32 = mybir.dt.float32
BF16 = mybir.dt.bfloat16
I32 = mybir.dt.int32
U32 = mybir.dt.uint32
U8 = mybir.dt.uint8
FP8X4 = mybir.dt.float8_e4m3fn_x4
ALU = mybir.AluOpType
ACT = mybir.ActivationFunctionType

P = 128
B, T, C = 4, 256, 1024
EPS = 1e-8
PACK = 4
GROUPS = C // (P * PACK)
PLANES = GROUPS * PACK
CH_TILES = C // P
HALVES = 2
HALF = B * T // HALVES
SEQ_HALF = B // HALVES
TOK_TILES = HALF // P
LEAD = 16
PITCH = LEAD + T

ROW_XPREV, ROW_MU = 0, 4
ROW_W, ROW_B0 = 0, 1
ROW_U, ROW_A0 = 0, 1
ROWS = 1 + B
MIX_R, MIX_K, MIX_V, W_OUT = 0, 1, 2, 3
PLANE_ROW = (0, 4, 8)
GROUPED_BUFS = (1, 1, 2)
TENSOR_SEQ = 1

FLOPS = 4 * 2 * B * T * C * C


def tile_rwkv_timemix_pa_kernel(
    tc, x, a0, b0, x_prev0, w, u, mu_r, mu_k, mu_v,
    W_r_words, W_r_scales, W_k_words, W_k_scales, W_v_words, W_v_scales,
    W_out_words, W_out_scales, out,
):
    nc = tc.nc
    x_rows = x.flatten_outer_dims()
    out_rows = out.flatten_outer_dims()
    weight_words = (W_r_words, W_k_words, W_v_words, W_out_words)
    weight_scales = (W_r_scales, W_k_scales, W_v_scales, W_out_scales)

    with ExitStack() as ctx:
        keep = ctx.enter_context(tc.tile_pool(name="keep", bufs=1))
        carry = ctx.enter_context(tc.tile_pool(name="carry", bufs=2))
        ctx.enter_context(tc.manual_schedule())

        with tc.tile_pool(name="early", bufs=1) as early:
            small_mix = early.tile([P, C], BF16, name="small_mix")
            nc.vector.memset(small_mix[:].bitcast(I32), 0)
            small_decay = early.tile([P, C], BF16, name="small_decay")
            nc.vector.memset(small_decay[:].bitcast(I32), 0)
            small_state = early.tile([P, C], BF16, name="small_state")
            x_half = []
            for hf in range(HALVES):
                x_half.append(early.tile([P, TOK_TILES, C], BF16, name="x_half%d" % hf))

            def load_x(hf, chans):
                for q in range(TOK_TILES):
                    first = hf * HALF + q * P
                    nc.sync.dma_start(out=x_half[hf][:, q, chans], in_=x_rows[first : first + P, chans])

            eps_col = keep.tile([P, 1], F32, name="eps_col")
            nc.vector.memset(eps_col[:], EPS)
            table_first = early.tile([P, 1], F32, name="table_first")
            nc.scalar.activation(out=table_first[:], in_=eps_col[:], func=ACT.Exp)
            def load_words(tile, words):
                for g in range(GROUPS):
                    nc.sync.dma_start(
                        out=tile[:, g, :], in_=words[g].rearrange("p n t -> p (n t)").bitcast(I32)
                    )

            def load_raw(wi):
                tile = early.tile([P, GROUPS, C], I32, name="raw%d" % wi, tag="raw", bufs=2, align_bytes=64)
                load_words(tile, weight_words[wi])
                return tile

            load_x(0, slice(0, C // 2))
            for m, mu in enumerate((mu_r, mu_k, mu_v)):
                nc.sync.dma_start(out=small_mix[ROW_MU + m : ROW_MU + m + 1, :], in_=mu.unsqueeze(0))
            nc.sync.dma_start(out=small_mix[ROW_XPREV : ROW_XPREV + B, :], in_=x_prev0)
            nc.sync.dma_start(out=small_decay[ROW_W : ROW_W + 1, :], in_=w.unsqueeze(0))
            nc.sync.dma_start(out=small_decay[ROW_B0 : ROW_B0 + B, :], in_=b0)
            raw = {MIX_R: load_raw(MIX_R)}
            load_x(0, slice(C // 2, C))
            nc.vector.memset(small_state[:].bitcast(I32), 0)
            nc.sync.dma_start(out=small_state[ROW_U : ROW_U + 1, :], in_=u.unsqueeze(0))
            nc.sync.dma_start(out=small_state[ROW_A0 : ROW_A0 + B, :], in_=a0)
            load_x(1, slice(0, C))

            ident_bf = early.tile([P, P], BF16, name="ident_bf")
            make_identity(nc, ident_bf[:])
            ident_f32 = keep.tile([P, P], F32, name="ident_f32")
            make_identity(nc, ident_f32[:])
            steps_int = early.tile([P, T], I32, name="steps_int")
            nc.gpsimd.iota(steps_int[:], pattern=[[1, T]], base=1, channel_multiplier=0)

            scale_raw = early.tile([P, GROUPS, C], U8, name="scale_raw", align_bytes=64)
            nc.gpsimd.memset(scale_raw[:].rearrange("p g n -> p (g n)").bitcast(I32), 0)
            out_scale = keep.tile([P, GROUPS, C], U8, name="out_scale", align_bytes=64)
            nc.gpsimd.memset(out_scale[:].rearrange("p g n -> p (g n)").bitcast(I32), 0)

            def load_scales(tile, first, scales):
                by_row = scales.rearrange("g (q r) n -> r q g n", r=4)
                for r in range(4):
                    nc.sync.dma_start(
                        out=tile[first + r : P : 32, :, :].bitcast(I32), in_=by_row[r].bitcast(I32)
                    )

            w_scale = keep.tile([P, GROUPS, C], U8, name="w_scale", align_bytes=64)
            w_code = []
            for wi in range(4):
                w_code.append(keep.tile([P, GROUPS, C], I32, name="w_code%d" % wi, align_bytes=64))
            for wi in (MIX_R, MIX_K, MIX_V):
                load_scales(scale_raw, PLANE_ROW[wi], weight_scales[wi])
            load_scales(out_scale, 0, weight_scales[W_OUT])
            raw[MIX_V] = load_raw(MIX_V)
            load_words(w_code[W_OUT], weight_words[W_OUT])

            def sorted_columns(tile):
                return tile[:].rearrange("p g (b t m) -> p (g b) t m", b=GROUPS, t=PACK)

            def raw_columns(tile):
                return tile[:].rearrange("p g (b m t) -> p (g b) t m", b=GROUPS, t=PACK)

            def sort_codes(wi):
                nc.vector.tensor_copy(
                    out=sorted_columns(w_code[wi]).rearrange("p x t (c i) -> p x c t i", i=4),
                    in_=raw_columns(raw[wi]).rearrange("p x t (c i) -> p x c t i", i=4),
                )

            def sort_scales():
                nc.vector.tensor_copy(out=sorted_columns(w_scale), in_=raw_columns(scale_raw))

            minus_before = early.tile([P, 2, T], BF16, name="minus_before")
            nc.vector.memset(minus_before[:].rearrange("p a n -> p (a n)").bitcast(I32), 0)
            minus_prev0 = early.tile([P, B, 2], BF16, name="minus_prev0")
            nc.vector.memset(minus_prev0[:].rearrange("p a n -> p (a n)").bitcast(I32), 0)
            for a in range(2):
                own = minus_before[:, a, a * P : (a + 1) * P]
                nc.vector.tensor_copy(out=own, in_=ident_bf[:])
                width = min(P, T - a * P - 1)
                nxt = minus_before[:, a, a * P + 1 : a * P + 1 + width]
                nc.vector.tensor_tensor(out=nxt, in0=nxt, in1=ident_bf[:, 0:width], op=ALU.subtract)
            for b in range(B):
                nc.vector.tensor_scalar_mul(
                    out=minus_prev0[:, b, 0:1], in0=ident_bf[:, ROW_XPREV + b : ROW_XPREV + b + 1], scalar1=-1.0
                )
            steps = keep.tile([P, T], F32, name="steps")
            nc.vector.tensor_copy(out=steps[:], in_=steps_int[:])

            x_code, x_scale = [], []
            for m in range(3):
                x_code.append(keep.tile([P, GROUPS, B * T], U32, name="x_code%d" % m, align_bytes=64))
                x_scale.append(keep.tile([P, GROUPS, B * T], U8, name="x_scale%d" % m, align_bytes=64))
            diag = early.tile([P, PLANES, 2, P], BF16, name="diag")
            by_decay = early.tile([P, CH_TILES, ROWS], F32, name="by_decay")
            mu_plane = keep.tile([P, PLANES, 3], F32, name="mu_plane")
            neg_w = keep.tile([P, CH_TILES, 1], F32, name="neg_w")
            neg_u = keep.tile([P, CH_TILES, 1], F32, name="neg_u")
            inv_b0 = keep.tile([P, CH_TILES, B], F32, name="inv_b0")
            neg_ratio = keep.tile([P, CH_TILES, B], F32, name="neg_ratio")
            decay = early.tile([P, CH_TILES, T], F32, name="decay")
            ln_b0_eps = keep.tile([P, CH_TILES, B], F32, name="ln_b0_eps")
            ln_bt = keep.tile([P, CH_TILES, B, T], F32, name="ln_bt")

            def new_grouped(m):
                return carry.tile([P, HALF, PACK], BF16, name="grouped%d" % m, bufs=GROUPED_BUFS[m], align_bytes=64)

            whole = tuple(range(SEQ_HALF))
            tiles = [(hf, j) for hf in range(HALVES) for j in range(CH_TILES)]
            units = [(hf, j, whole) for hf, j in tiles[:-2]]
            units += [(hf, j, (s,)) for s in whole for hf, j in tiles[-2:]]
            rho = {}

            def start_rho(n):
                hf, j, seqs = units[n]
                rho[n] = carry.tile([P, SEQ_HALF, T], F32, name="rho")
                for i, s in enumerate(seqs):
                    b = hf * SEQ_HALF + s
                    nc.scalar.activation(
                        out=rho[n][:, i, :], in_=steps[:], func=ACT.Sigmoid,
                        scale=neg_w[:, j, :], bias=ln_b0_eps[:, j, b : b + 1],
                    )

            def regroup(m, grouped, mixed, tok, on_scalar):
                dst = grouped[:, tok, :].rearrange("p (c i) t -> p c t i", i=4)
                src = mixed[:, :, tok].rearrange("p t (c i) -> p c t i", i=4)
                if on_scalar:
                    nc.scalar.copy(out=dst, in_=src)
                else:
                    nc.gpsimd.tensor_scalar(
                        out=dst, in0=src, scalar1=1.0, scalar2=0.0, op0=ALU.mult, op1=ALU.add
                    )

            def quantise_x(grouped, m, g, hf):
                cols = slice(hf * HALF, (hf + 1) * HALF)
                nc.vector.quantize_mx(
                    out=x_code[m][:, g, cols].bitcast(FP8X4),
                    scales=x_scale[m][:, g, cols],
                    in_=grouped[:].rearrange("p n t -> p (n t)"),
                )

            def channel_product(acc, wi, hf, j, tok_of_half):
                ch = slice(j * P, (j + 1) * P)
                tok = slice(hf * HALF + tok_of_half.start, hf * HALF + tok_of_half.stop)
                for g in range(GROUPS):
                    nc.tensor.matmul_mx(
                        out=acc,
                        lhsT=w_code[wi][:, g, ch].bitcast(FP8X4),
                        lhsT_scale=w_scale[PLANE_ROW[wi] : P, g, ch],
                        rhs=x_code[wi][:, g, tok].bitcast(FP8X4),
                        rhs_scale=x_scale[wi][:, g, tok],
                        start=(g == 0),
                        stop=(g == GROUPS - 1),
                    )

            with tc.psum_pool(name="psum_mix", bufs=2) as psum_mix:
                x_pairs = early.tile([P, PLANES // 2, B, PITCH, 2], BF16, name="x_pairs")

                def small_planes(g):
                    by_plane_ps = psum_mix.tile([P, PACK, P], BF16, name="by_plane_ps", tag="xt")
                    for t in range(PACK):
                        nc.tensor.transpose(
                            by_plane_ps[:, t, :], small_mix[:, g * 512 + t : (g + 1) * 512 : PACK], ident_bf[:]
                        )
                    nc.vector.tensor_copy(
                        out=mu_plane[:, g * PACK : (g + 1) * PACK, :], in_=by_plane_ps[:, :, ROW_MU : ROW_MU + 3]
                    )
                    nc.vector.tensor_copy(
                        out=x_pairs[:, g * 2 : (g + 1) * 2, :, LEAD - 1, :],
                        in_=by_plane_ps[:, :, ROW_XPREV : ROW_XPREV + B].rearrange("p (r e) b -> p r b e", e=2),
                    )

                def make_diagonals(g):
                    for plane in range(g * PACK, (g + 1) * PACK):
                        for i, sign in enumerate((1.0, -1.0)):
                            nc.gpsimd.tensor_scalar(
                                out=diag[:, plane, i, :], in0=ident_bf[:], op0=ALU.mult, op1=ALU.mult,
                                scalar1=mu_plane[:, plane, MIX_V : MIX_V + 1], scalar2=sign,
                            )

                def mix_by_tensor(hf, g, grouped):
                    b = hf * SEQ_HALF + TENSOR_SEQ
                    for a in range(T // P):
                        mix_ps = psum_mix.tile([P, PACK, P], F32, name="mix_ps", tag="misc")
                        for t in range(PACK):
                            plane = g * PACK + t
                            pair = x_pairs[:, plane // 2, b, :, plane % 2]
                            now = pair[:, LEAD + a * P : LEAD + (a + 1) * P]
                            before = pair[:, LEAD - 1 + a * P : LEAD - 1 + (a + 1) * P]
                            acc = mix_ps[:, t, :]
                            nc.tensor.matmul(acc, lhsT=diag[:, plane, 0, :], rhs=now, start=True, stop=False)
                            nc.tensor.matmul(acc, lhsT=diag[:, plane, 1, :], rhs=before, start=False, stop=False)
                            nc.tensor.matmul(acc, lhsT=ident_bf[:], rhs=before, start=False, stop=True)
                        first = TENSOR_SEQ * T + a * P
                        nc.scalar.copy(
                            out=grouped[:, first : first + P, :], in_=mix_ps[:].rearrange("p t n -> p n t")
                        )

                def before_of(plane, seqs):
                    return x_pairs[:, plane // 2, seqs, LEAD - 1 : PITCH - 1, plane % 2]

                def prepare_pair(hf, g, k):
                    xt_ps = psum_mix.tile([P, HALF], F32, name="xt_ps", tag="xt")
                    for q in range(TOK_TILES):
                        nc.tensor.transpose(
                            xt_ps[:, q * P : (q + 1) * P],
                            x_half[hf][:, q, :].bitcast(F32)[:, g * 256 + k : (g + 1) * 256 : 2],
                            ident_f32[:],
                        )
                    nc.scalar.copy(
                        out=x_pairs[:, g * 2 + k, hf * SEQ_HALF : (hf + 1) * SEQ_HALF, LEAD:PITCH, :]
                        .rearrange("p s t e -> p s (t e)")
                        .bitcast(F32),
                        in_=xt_ps[:].rearrange("p (s t) -> p s t", s=SEQ_HALF),
                    )

                def prepare_difference(hf, g, t):
                    chans = slice(g * 512 + t, (g + 1) * 512, PACK)
                    diff_ps = psum_mix.tile([P, SEQ_HALF, T], F32, name="diff_ps", tag="diff", bufs=4)
                    for s in range(SEQ_HALF):
                        acc = diff_ps[:, s, :]
                        nc.tensor.matmul(
                            acc, lhsT=x_half[hf][:, 2 * s, chans], rhs=minus_before[:, 0, :],
                            start=True, stop=False,
                        )
                        nc.tensor.matmul(
                            acc[:, P:T], lhsT=x_half[hf][:, 2 * s + 1, chans], rhs=minus_before[:, 1, P:T],
                            start=False, stop=False,
                        )
                        nc.tensor.matmul(
                            acc[:, 0:2], lhsT=small_mix[:, chans], rhs=minus_prev0[:, hf * SEQ_HALF + s, :],
                            start=False, stop=True,
                        )
                    return diff_ps

                def log_of_bt(j):
                    for b in range(B):
                        nc.scalar.activation(
                            out=ln_bt[:, j, b, :], in_=decay[:, j, :], func=ACT.Ln,
                            scale=by_decay[:, j, ROW_B0 + b : ROW_B0 + b + 1], bias=eps_col[:],
                        )

                def by_channel_tile(small):
                    small_ps = psum_mix.tile([P, CH_TILES, P], BF16, name="small_ps", tag="xt")
                    for j in range(CH_TILES):
                        g, t = divmod(j, PACK)
                        nc.tensor.transpose(
                            small_ps[:, j, :], small[:, g * 512 + t : (g + 1) * 512 : PACK], ident_bf[:]
                        )
                    return small_ps

                def decay_constants():
                    small_ps = by_channel_tile(small_decay)
                    nc.scalar.activation(
                        out=neg_w[:], in_=small_ps[:, :, ROW_W : ROW_W + 1], func=ACT.Copy, scale=-1.0
                    )
                    nc.scalar.copy(out=by_decay[:], in_=small_ps[:, :, 0:ROWS])
                    for j in range(CH_TILES):
                        nc.scalar.activation(out=decay[:, j, :], in_=steps[:], func=ACT.Exp, scale=neg_w[:, j, :])

                def state_constants():
                    small_ps = by_channel_tile(small_state)
                    nc.vector.tensor_scalar_mul(out=neg_u[:], in0=small_ps[:, :, ROW_U : ROW_U + 1], scalar1=-1.0)
                    nc.vector.scalar_tensor_tensor(
                        out=neg_ratio[:], in0=small_ps[:, :, ROW_A0 : ROW_A0 + B], scalar=-1.0, in1=inv_b0[:],
                        op0=ALU.mult, op1=ALU.mult,
                    )

                def invert_b0():
                    nc.vector.reciprocal(out=inv_b0[:], in_=by_decay[:, :, ROW_B0 : ROW_B0 + B])

                first_step_extras = {
                    (1, MIX_K): lambda: sort_codes(MIX_R),
                    (1, MIX_V): lambda: (small_planes(1), make_diagonals(1)),
                    (2, MIX_R): invert_b0,
                    (2, MIX_V): state_constants,
                }

                steps_of_mix = [(hf, g) for hf in range(HALVES) for g in range(GROUPS)]
                prepare_pair(0, 0, 0)
                small_planes(0)
                make_diagonals(0)
                diff_banks = [prepare_difference(0, 0, t) for t in (0, 1)]
                prepare_pair(0, 0, 1)
                decay_constants()
                diff_banks += [prepare_difference(0, 0, t) for t in (2, 3)]

                logs_of_step = ((), (0, 1), (2, 3, 4), (5, 6, 7))
                def regroup_step(grouped, mixed, g, hf):
                    regroup(MIX_R, grouped[MIX_R], mixed[MIX_R], slice(0, HALF), False)
                    regroup(MIX_K, grouped[MIX_K], mixed[MIX_K], slice(0, HALF), False)
                    regroup(MIX_V, grouped[MIX_V], mixed[MIX_V], slice(0, TENSOR_SEQ * T), (hf, g) != (0, 0))
                    mix_by_tensor(hf, g, grouped[MIX_V])

                mixed_before = None
                for step, (hf, g) in enumerate(steps_of_mix):
                    seqs = slice(hf * SEQ_HALF, (hf + 1) * SEQ_HALF)
                    def prepare_next():
                        if step + 1 < len(steps_of_mix):
                            for k in range(PACK // 2):
                                prepare_pair(*steps_of_mix[step + 1], k)

                    if step > 0:
                        prepare_next()
                    fresh, counts = [], []
                    for m in (MIX_R, MIX_K, MIX_V):
                        counts.append(TENSOR_SEQ if m == MIX_V else SEQ_HALF)
                        mixed = carry.tile([P, PACK, counts[m] * T], BF16, name="mixed%d" % m, tag="slab%d" % m)
                        fresh.append(mixed)
                    for t in range(PACK):
                        for m in (MIX_R, MIX_K, MIX_V):
                            nc.vector.scalar_tensor_tensor(
                                out=fresh[m][:, t, :].rearrange("p (s t) -> p s t", s=counts[m]),
                                in0=diff_banks[t][:, 0 : counts[m], :],
                                scalar=mu_plane[:, g * PACK + t, m : m + 1],
                                in1=before_of(g * PACK + t, slice(seqs.start, seqs.start + counts[m])),
                                op0=ALU.mult, op1=ALU.add,
                            )
                            if step == 0 and (t, m) in first_step_extras:
                                first_step_extras[(t, m)]()
                    if step == 0:
                        prepare_next()
                        nc.scalar.activation(
                            out=ln_b0_eps[:], in_=by_decay[:, :, ROW_B0 : ROW_B0 + B], func=ACT.Ln, scale=1.0 / EPS
                        )
                    if step == 0:
                        raw[MIX_K] = load_raw(MIX_K)
                    if step == 2:
                        sort_codes(MIX_V)
                        sort_scales()
                    if step == 3:
                        sort_codes(MIX_K)
                    if mixed_before is not None:
                        regrouped = [new_grouped(m) for m in (MIX_R, MIX_K, MIX_V)]
                        regroup_step(regrouped, *mixed_before)
                        for m in (MIX_V, MIX_K, MIX_R):
                            quantise_x(regrouped[m], m, mixed_before[1], mixed_before[2])
                    mixed_before = (fresh, g, hf)
                    if step + 1 < len(steps_of_mix):
                        diff_banks = [prepare_difference(*steps_of_mix[step + 1], t) for t in range(PACK)]
                    for j in logs_of_step[step]:
                        log_of_bt(j)
                start_rho(0)
                last_mixed, last_g, last_hf = mixed_before
                last_grouped_v = new_grouped(MIX_V)
                regroup(MIX_V, last_grouped_v, last_mixed[MIX_V], slice(0, TENSOR_SEQ * T), True)
                mix_by_tensor(last_hf, last_g, last_grouped_v)

        epi = ctx.enter_context(tc.tile_pool(name="epi", bufs=2, reuse_waits="tile"))
        r_half = []
        for hf in range(HALVES):
            r_half.append(epi.tile([P, CH_TILES, HALF], F32, name="r_half%d" % hf, bufs=1))
        with tc.psum_pool(name="psum", bufs=2, reuse_waits="tile") as psum:
            def tokens(seqs):
                return slice(seqs[0] * T, (seqs[-1] + 1) * T)

            def width(seqs):
                return len(seqs) * T

            k_bank, v_bank, sb, part = {}, {}, {}, {}
            wkv, h = {}, {}

            def start_k(n):
                k_ps = psum.tile([P, HALF], F32, name="k_ps", tag="k")
                hf, j, seqs = units[n]
                channel_product(k_ps[:, 0 : width(seqs)], MIX_K, hf, j, tokens(seqs))
                k_bank[n] = k_ps

            def start_v(n):
                v_ps = psum.tile([P, HALF], F32, name="v_ps", tag="v", bufs=3)
                hf, j, seqs = units[n]
                channel_product(v_ps[:, 0 : width(seqs)], MIX_V, hf, j, tokens(seqs))
                v_bank[n] = v_ps

            def make_r(hf, j):
                r_ps = psum.tile([P, HALF], F32, name="r_ps", tag="misc", bufs=3)
                channel_product(r_ps[:], MIX_R, hf, j, slice(0, HALF))
                nc.scalar.activation(out=r_half[hf][:, j, :], in_=r_ps[:], func=ACT.Sigmoid)

            def weigh_unit(n):
                hf, j, seqs = units[n]
                sb[n] = epi.tile([P, HALF], F32, name="sb")
                own = sb[n][:, 0 : width(seqs)]
                first = hf * SEQ_HALF + seqs[0]
                nc.vector.tensor_tensor(
                    out=own, in0=k_bank[n][:, 0 : width(seqs)], op=ALU.subtract,
                    in1=ln_bt[:, j, first : first + len(seqs), :].rearrange("p s t -> p (s t)"),
                )
                nc.scalar.activation(out=own, in_=own, func=ACT.Sigmoid, scale=-1.0, bias=neg_u[:, j, :])

            def part_unit(n):
                hf, j, seqs = units[n]
                part[n] = epi.tile([P, HALF], F32, name="part", bufs=3)
                for i, s in enumerate(seqs):
                    b = hf * SEQ_HALF + s
                    nc.vector.scalar_tensor_tensor(
                        out=part[n][:, i * T : (i + 1) * T], in0=rho[n][:, i, :],
                        scalar=neg_ratio[:, j, b : b + 1], in1=v_bank[n][:, i * T : (i + 1) * T],
                        op0=ALU.mult, op1=ALU.add,
                    )

            def blend_unit(n):
                hf, j, seqs = units[n]
                g, t = divmod(j, PACK)
                if (hf, g) not in wkv:
                    wkv_tile = epi.tile([P, PACK, HALF], F32, name="wkv")
                    wkv[(hf, g)] = wkv_tile
                own = part[n][:, 0 : width(seqs)]
                nc.gpsimd.tensor_tensor(out=own, in0=own, in1=sb[n][:, 0 : width(seqs)], op=ALU.mult)
                nc.vector.tensor_tensor(
                    out=wkv[(hf, g)][:, t, tokens(seqs)], in0=v_bank[n][:, 0 : width(seqs)], in1=own, op=ALU.subtract
                )

            def gate_tokens(engine, hf, g, q):
                if q == 0:
                    h_grouped = epi.tile([P, HALF, PACK], BF16, name="h_grouped", align_bytes=64)
                    h_code = epi.tile([P, HALF], U32, name="h_code", bufs=4, align_bytes=64)
                    h_scale = epi.tile([P, HALF], U8, name="h_scale", bufs=4, align_bytes=64)
                    h[(hf, g)] = (h_grouped, h_code, h_scale)
                tok = slice(q * P, (q + 1) * P)
                engine.tensor_tensor(
                    out=h[(hf, g)][0][:, tok, :].rearrange("p (c i) t -> p c t i", i=4),
                    in0=wkv[(hf, g)][:, :, tok].rearrange("p t (c i) -> p c t i", i=4),
                    in1=r_half[hf][:, g * PACK : (g + 1) * PACK, tok].rearrange("p t (c i) -> p c t i", i=4),
                    op=ALU.mult,
                )

            def quantise_h(hf, g, first, last):
                h_grouped, h_code, h_scale = h[(hf, g)]
                tok = slice(first * P, last * P)
                nc.vector.quantize_mx(
                    out=h_code[:, tok].bitcast(FP8X4),
                    scales=h_scale[:, tok],
                    in_=h_grouped[:, tok, :].rearrange("p n t -> p (n t)"),
                )

            def copy_out(on_vector, dst, src):
                if on_vector:
                    nc.vector.tensor_copy(out=dst, in_=src)
                else:
                    nc.scalar.copy(out=dst, in_=src)

            def new_result(hf, q):
                return carry.tile([P, C], F32, name="result", tag="slab%d" % ((hf * TOK_TILES + q) % 3))

            def pass_over(out_ps, hf, q, g, nh):
                tok, n_cols = slice(q * P, (q + 1) * P), slice(nh * 512, (nh + 1) * 512)
                nc.tensor.matmul_mx(
                    out=out_ps,
                    lhsT=h[(hf, g)][1][:, tok].bitcast(FP8X4),
                    lhsT_scale=h[(hf, g)][2][:, tok],
                    rhs=w_code[W_OUT][:, g, n_cols].bitcast(FP8X4),
                    rhs_scale=out_scale[:, g, n_cols],
                    start=(g == 0),
                    stop=(g == GROUPS - 1),
                )

            def store(hf, q, banks, vector_half):
                result = new_result(hf, q)
                first = hf * HALF + q * P
                for nh in range(C // 512):
                    n_cols = slice(nh * 512, (nh + 1) * 512)
                    copy_out(nh == vector_half, result[:, n_cols], banks[nh][:])
                    nc.sync.dma_start(out=out_rows[first : first + P, n_cols], in_=result[:, n_cols])

            def project(hf, q):
                banks = []
                for nh in range(C // 512):
                    out_ps = psum.tile([P, 512], F32, name="out_ps", tag="misc", bufs=3)
                    for g in range(GROUPS):
                        pass_over(out_ps[:], hf, q, g, nh)
                    banks.append(out_ps)
                store(hf, q, banks, None)

            last_grouped = [new_grouped(MIX_R), new_grouped(MIX_K), last_grouped_v]
            quarters = [slice(i * P, (i + 1) * P) for i in range(TOK_TILES)]
            gpsimd_gates = {5: (0, 0, 0), 7: (0, 0, 2), 9: (0, 1, 0), 11: (0, 1, 2)}
            vector_gates = {
                6: ((0, 0, 1),), 8: ((0, 0, 3),), 10: ((0, 1, 1),), 12: ((0, 1, 3),), 13: ((1, 0, 0),), 14: ((1, 0, 1),),
                15: ((1, 0, 2),), 16: ((1, 0, 3),),
            }
            late_gates = {16: ((1, 1, 0), (1, 1, 1))}
            quantise_turns = {
                10: ((0, 0, 0, 4),), 11: ((0, 1, 0, 1),), 12: ((0, 1, 1, 2),), 13: ((0, 1, 2, 3),),
                14: ((0, 1, 3, 4),), 16: ((1, 0, 0, 2),), 17: ((1, 1, 0, 2), (1, 0, 2, 4)),
            }
            project_turns = {11: ((0, 0),), 12: ((0, 1),), 13: ((0, 2),), 15: ((0, 3),), 17: ((1, 0), (1, 1))}
            start_k(0)
            start_v(0)
            for n in range(len(units)):
                if n + 1 < len(units):
                    start_rho(n + 1)
                weigh_unit(n)
                part_unit(n)
                if n == 2:
                    quantise_x(last_grouped[MIX_V], MIX_V, last_g, last_hf)
                if n == 4:
                    quantise_x(last_grouped[MIX_R], MIX_R, last_g, last_hf)
                    quantise_x(last_grouped[MIX_K], MIX_K, last_g, last_hf)
                for piece in vector_gates.get(n, ()):
                    gate_tokens(nc.vector, *piece)
                for piece in quantise_turns.get(n, ()):
                    quantise_h(*piece)
                if n + 1 < len(units):
                    start_k(n + 1)
                    start_v(n + 1)
                if n < len(tiles):
                    make_r(*tiles[n])
                for piece in project_turns.get(n, ()):
                    project(*piece)
                if n >= 1:
                    blend_unit(n - 1)
                if n in gpsimd_gates:
                    gate_tokens(nc.gpsimd, *gpsimd_gates[n])
                for piece in late_gates.get(n, ()):
                    gate_tokens(nc.vector, *piece)
                if n < 4:
                    regroup(MIX_R, last_grouped[MIX_R], last_mixed[MIX_R], quarters[n], n in (2, 3))
                    regroup(MIX_K, last_grouped[MIX_K], last_mixed[MIX_K], quarters[n], False)
            blend_unit(len(units) - 1)

        with tc.psum_pool(name="psum_end", bufs=4, reuse_waits="tile") as psum_end:
            hf = HALVES - 1
            banks = {}
            gate_tokens(nc.vector, hf, 1, 2)
            gate_tokens(nc.vector, hf, 1, 3)
            quantise_h(hf, 1, 2, 3)
            quantise_h(hf, 1, 3, 4)
            for g in range(GROUPS):
                for q in (2, 3):
                    for nh in range(C // 512):
                        if g == 0:
                            out_ps = psum_end.tile([P, 512], F32, name="out_ps", tag="misc")
                            banks[(q, nh)] = out_ps
                        pass_over(banks[(q, nh)][:], hf, q, g, nh)
                    if g == GROUPS - 1:
                        store(hf, q, (banks[(q, 0)], banks[(q, 1)]), 1)
